import numpy as np
import ml_dtypes


def mxq(x, axis, fmt="e4m3"):
    dtype, down = {"e4m3": (ml_dtypes.float8_e4m3fn, 7), "e5m2": (ml_dtypes.float8_e5m2, 14)}[fmt]
    v = np.moveaxis(np.asarray(x, np.float32).astype(ml_dtypes.bfloat16).astype(np.float64), axis, -1)
    blocks = v.reshape(v.shape[:-1] + (-1, 32))
    amax = np.abs(blocks).max(-1, keepdims=True)
    byte = np.maximum(np.where(amax > 0, np.frexp(amax)[1] - 1 + 127, 0) - down, 1)
    scale = np.exp2(byte - 127.0)
    codes = (blocks / scale).astype(np.float32).astype(dtype).astype(np.float64)
    return np.moveaxis((codes * scale).reshape(v.shape), -1, axis)


WIDE = False


def mx_kscale(k):
    if not WIDE:
        return np.ones(k)
    levels = np.array([10, -10, 5, -5, 0])
    a = np.random.permutation(np.resize(levels, k // 512 * 4)).reshape(k // 512, 4)
    idx = np.arange(k)
    return np.exp2(a[idx // 512, idx % 128 // 32])


BF16 = ml_dtypes.bfloat16


def bf(x):
    return np.asarray(x, np.float32).astype(BF16)


def f64(x):
    return np.asarray(x).astype(np.float64)


E2M1 = np.array([0.0, 0.5, 1.0, 1.5, 2.0, 3.0, 4.0, 6.0, -0.0, -0.5, -1.0, -1.5, -2.0, -3.0, -4.0, -6.0])


def pack_weight(w, fmt):
    k, n = w.shape
    w = f64(bf(w)).reshape(k // 32, 32, n)
    amax = np.abs(w).max(1)
    if fmt == "e4m3":
        byte = np.frexp(amax)[1] - 1 + 127 - 7
    else:
        mant, ex = np.frexp(amax / 6.0)
        byte = np.where(mant > 0.5, ex, ex - 1) + 127
    byte = np.clip(np.where(amax > 0, byte, 1), 1, 254)
    scaled = (w * np.exp2(127.0 - byte)[:, None, :]).reshape(k, n).astype(np.float32)
    by_word = np.ascontiguousarray(scaled.reshape(k // 512, 128, 4, n).transpose(0, 1, 3, 2))
    if fmt == "e4m3":
        words = by_word.astype(ml_dtypes.float8_e4m3fn).view(np.uint8)
    else:
        c = by_word.astype(ml_dtypes.float4_e2m1fn).view(np.uint8) & 0xF
        words = c[..., 0::2] | (c[..., 1::2] << 4)
    return np.ascontiguousarray(words), np.ascontiguousarray(byte.astype(np.uint8).reshape(k // 512, 16, n))


def unpack_weight(words, scales, fmt):
    g, p, n, _ = words.shape
    if fmt == "e4m3":
        vals = np.ascontiguousarray(words).view(ml_dtypes.float8_e4m3fn).astype(np.float64)
    else:
        nib = np.empty((g, p, n, 4), np.uint8)
        nib[..., 0::2] = words & 0xF
        nib[..., 1::2] = words >> 4
        vals = E2M1[nib]
    vals = vals * np.repeat(np.exp2(scales.astype(np.float64) - 127.0), 8, axis=1)[..., None]
    return vals.transpose(0, 1, 3, 2).reshape(g * 512, n)

def pack4(w):
    words, scales = pack_weight(w, "e2m1")
    return words.reshape(words.shape[0], 128, -1), scales


def unpack4(words, scales):
    return unpack_weight(words.reshape(words.shape[0], 128, -1, 2), scales, "e2m1")


B, SA, SB, D, H, DH = 1, 768, 256, 1024, 8, 128
S = SA + SB
EPS = 1e-6


def make_rope(s, dh):
    pos = np.arange(s, dtype=np.float64)
    inv_freq = 1.0 / (10000.0 ** (np.arange(0, dh, 2, dtype=np.float64) / dh))
    theta = pos[:, None] * inv_freq[None, :]
    cos, sin = np.cos(theta), np.sin(theta)
    row0 = np.stack([cos, -sin], axis=-1)
    row1 = np.stack([sin, cos], axis=-1)
    return np.stack([row0, row1], axis=-2)[None, None]


def rms_norm(x, w):
    return x * (1.0 / np.sqrt(np.mean(x * x, axis=-1, keepdims=True) + EPS)) * w


def apply_rope(x, freqs):
    x_ = x.reshape(*x.shape[:-1], -1, 1, 2)
    out = freqs[..., 0] * x_[..., 0] + freqs[..., 1] * x_[..., 1]
    return out.reshape(x.shape)


def qkv(x, w_kn, b):
    y = (mxq(x, 2, "e4m3") @ w_kn) + b
    y = y.reshape(x.shape[0], x.shape[1], 3 * H, DH).transpose(0, 2, 1, 3)
    return y[:, :H], y[:, H:2 * H], y[:, 2 * H:]


def setup_inputs():
    sa, sb = mx_kscale(D), mx_kscale(D)
    hidden_states_a = bf(np.random.standard_normal((B, SA, D)) * sa)
    hidden_states_b = bf(np.random.standard_normal((B, SB, D)) * sb)
    image_rotary_emb = bf(make_rope(S, DH))
    a_w = np.random.standard_normal((3 * D, D)) / np.sqrt(D) / sa
    a_qkv_b = bf(np.random.standard_normal(3 * D) * 0.2)
    b_w = np.random.standard_normal((3 * D, D)) / np.sqrt(D) / sb
    b_qkv_b = bf(np.random.standard_normal(3 * D) * 0.2)
    a_words, a_scales = pack4(np.ascontiguousarray(a_w.T))
    b_words, b_scales = pack4(np.ascontiguousarray(b_w.T))
    return {
        "hidden_states_a": hidden_states_a,
        "hidden_states_b": hidden_states_b,
        "image_rotary_emb": image_rotary_emb,
        "a_qkv_w_words": a_words,
        "a_qkv_w_scales": a_scales,
        "a_qkv_b": a_qkv_b,
        "b_qkv_w_words": b_words,
        "b_qkv_w_scales": b_scales,
        "b_qkv_b": b_qkv_b,
        "norm_q_a_w": bf(1.5 + 0.15 * np.random.standard_normal(DH)),
        "norm_k_a_w": bf(1.5 + 0.15 * np.random.standard_normal(DH)),
        "norm_q_b_w": bf(1.5 + 0.15 * np.random.standard_normal(DH)),
        "norm_k_b_w": bf(1.5 + 0.15 * np.random.standard_normal(DH)),
    }


def reference(hidden_states_a, hidden_states_b, image_rotary_emb, a_qkv_w_words, a_qkv_w_scales, a_qkv_b,
              b_qkv_w_words, b_qkv_w_scales, b_qkv_b, norm_q_a_w, norm_k_a_w, norm_q_b_w, norm_k_b_w):
    q_a, k_a, v_a = qkv(f64(hidden_states_a), unpack4(a_qkv_w_words, a_qkv_w_scales), f64(a_qkv_b))
    q_a = rms_norm(q_a, f64(norm_q_a_w))
    k_a = rms_norm(k_a, f64(norm_k_a_w))
    q_b, k_b, v_b = qkv(f64(hidden_states_b), unpack4(b_qkv_w_words, b_qkv_w_scales), f64(b_qkv_b))
    q_b = rms_norm(q_b, f64(norm_q_b_w))
    k_b = rms_norm(k_b, f64(norm_k_b_w))
    q = np.concatenate([q_b, q_a], axis=2)
    k = np.concatenate([k_b, k_a], axis=2)
    v = np.concatenate([v_b, v_a], axis=2)
    f = f64(image_rotary_emb)
    return apply_rope(q, f), apply_rope(k, f), v

@@ -1,0 +1,307 @@
+import concourse.mybir as mybir
+from concourse.masks import make_identity
+
+F32 = mybir.dt.float32
+BF16 = mybir.dt.bfloat16
+I32 = mybir.dt.int32
+U32 = mybir.dt.uint32
+U8 = mybir.dt.uint8
+FP8X4 = mybir.dt.float8_e4m3fn_x4
+FP4X4 = mybir.dt.float4_e2m1fn_x4
+ACT = mybir.ActivationFunctionType
+ALU = mybir.AluOpType
+
+P = 128
+D_MODEL = 1024
+K_PASS = 512
+PASSES = D_MODEL // K_PASS
+DH = 128
+PAIRS = DH // 2
+GROUP = 4
+BANK = GROUP * DH
+N_OUT = 3 * D_MODEL
+CHUNKS = N_OUT // BANK
+TILES = 2
+BLOCKS = 4
+EPS = 1e-6
+CHUNK_ORDER = (0, 2, 4, 1, 3, 5)
+
+FLOPS = 2 * BLOCKS * TILES * P * D_MODEL * N_OUT
+
+
+def tile_fluxjointattention_pa_kernel(
+    tc,
+    hidden_states_a,
+    hidden_states_b,
+    image_rotary_emb,
+    a_qkv_w_words,
+    a_qkv_w_scales,
+    a_qkv_b,
+    b_qkv_w_words,
+    b_qkv_w_scales,
+    b_qkv_b,
+    norm_q_a_w,
+    norm_k_a_w,
+    norm_q_b_w,
+    norm_k_b_w,
+    out_0,
+    out_1,
+    out_2,
+):
+    nc = tc.nc
+    words_in = (b_qkv_w_words, a_qkv_w_words)
+    scales_in = (b_qkv_w_scales, a_qkv_w_scales)
+    bias_in = (b_qkv_b, a_qkv_b)
+    gain_in = (norm_q_b_w, norm_k_b_w, norm_q_a_w, norm_k_a_w)
+    outs = (out_0, out_1, out_2)
+
+    with (
+        tc.tile_pool(name="keep", bufs=1) as keep,
+        tc.tile_pool(name="stage", bufs=2) as stage,
+        tc.tile_pool(name="work", bufs=4) as work,
+        tc.tile_pool(name="result", bufs=6) as result,
+        tc.psum_pool(name="prep", bufs=2) as prep,
+        tc.psum_pool(name="sums", bufs=6) as sums,
+    ):
+        x_sb = keep.tile([P, BLOCKS, TILES, D_MODEL], BF16)
+        x_codes = keep.tile([P, BLOCKS, TILES * PASSES * P], U32, align_bytes=64)
+        x_planes = keep.tile([P, BLOCKS, TILES * PASSES * P], U8, align_bytes=64)
+        w_words = keep.tile([P, 2, PASSES, 2 * N_OUT], U8, align_bytes=64)
+        w_planes = keep.tile([P, 2, PASSES, N_OUT], U8, align_bytes=64)
+        bias_rows = keep.tile([P, 2, N_OUT], BF16)
+        gain_rows = keep.tile([P, 4 * DH], BF16)
+        bias_sb = keep.tile([P, 2, CHUNKS, BANK], F32)
+        gains = keep.tile([P, 4, 2, PAIRS], F32)
+        gains_swapped = keep.tile([P, 4, 2, PAIRS], F32)
+        rope_sb = keep.tile([P, BLOCKS * TILES, 4 * PAIRS], BF16)
+        table = keep.tile([P, BLOCKS * TILES, 4, 2, PAIRS], F32)
+        ident = keep.tile([P, P], F32)
+        ones = keep.tile([P, P], BF16)
+        eps = keep.tile([P, 1], F32)
+
+        nc.vector.memset(w_planes[:, 0].rearrange("p g n -> p (g n)").bitcast(I32), 0)
+        nc.vector.memset(gain_rows[:].bitcast(I32), 0)
+        nc.vector.memset(bias_rows[:, 0].bitcast(I32), 0)
+        nc.vector.memset(ones[:], 1.0)
+        nc.vector.memset(eps[:], EPS)
+        nc.gpsimd.memset(w_planes[:, 1].rearrange("p g n -> p (g n)").bitcast(F32), 0.0)
+        nc.gpsimd.memset(bias_rows[:, 1].bitcast(F32), 0.0)
+        make_identity(nc, ident[:])
+
+        def load_x(blk):
+            if blk == 0:
+                rows = hidden_states_b[0]
+            else:
+                rows = hidden_states_a[0, (blk - 1) * TILES * P : blk * TILES * P, :]
+            nc.sync.dma_start(out=x_sb[:, blk], in_=rows.rearrange("(p t) k -> p t k", t=TILES))
+
+        def load_weights(s):
+            planes = w_planes[:, s].bitcast(I32)
+            rows = scales_in[s].bitcast(I32)
+            for r in range(4):
+                nc.sync.dma_start(out=planes[r:P:32], in_=rows[:, r:16:4, :].rearrange("g q n -> q g n"))
+            words = w_words[:].bitcast(I32)
+            width = 2 * BANK // 4
+            for c in CHUNK_ORDER:
+                nc.sync.dma_start(
+                    out=words[:, s, :, c * width : (c + 1) * width],
+                    in_=words_in[s].bitcast(I32)[:, :, c * width : (c + 1) * width].rearrange("g p n -> p g n"),
+                )
+
+        for v in range(4):
+            nc.scalar.dma_start(
+                out=gain_rows[0:1, v * DH : (v + 1) * DH], in_=gain_in[v].rearrange("(o n) -> o n", o=1)
+            )
+        nc.scalar.dma_start(
+            out=rope_sb[:].rearrange("p (k t) f -> p k (t f)", t=TILES),
+            in_=image_rotary_emb.rearrange("a b (k p t) j r c -> p (a b k) (t j r c)", p=P, t=TILES),
+        )
+        for s in range(2):
+            nc.scalar.dma_start(out=bias_rows[0:1, s, :], in_=bias_in[s].rearrange("(o n) -> o n", o=1))
+        load_x(0)
+        load_weights(0)
+        for blk in range(1, BLOCKS):
+            load_x(blk)
+        load_weights(1)
+
+        def quantise_block(blk):
+            x_pairs = x_sb[:].bitcast(F32)
+            grouped = stage.tile([P, TILES, PASSES, P, 2], F32, align_bytes=64)
+            for t in range(TILES):
+                x_t = prep.tile([P, PASSES * 2, P], F32, tag="prep")
+                for g in range(PASSES):
+                    for u in range(2):
+                        nc.tensor.transpose(
+                            x_t[:, 2 * g + u, :],
+                            x_pairs[:, blk, t, 256 * g + u : 256 * (g + 1) : 2],
+                            ident[:],
+                        )
+                nc.scalar.copy(out=grouped[:, t], in_=x_t[:].rearrange("p (g u) r -> p g r u", u=2))
+            nc.vector.quantize_mx(
+                out=x_codes[:, blk, :].bitcast(FP8X4),
+                scales=x_planes[:, blk, :],
+                in_=grouped[:].rearrange("p t g r u -> p (t g r u)").bitcast(BF16),
+            )
+
+        def spread_gains():
+            spread = prep.tile([P, BANK], F32, tag="prep")
+            nc.tensor.matmul(spread[:], lhsT=ones[:], rhs=gain_rows[:], start=True, stop=True)
+            planes = spread[:].rearrange("p (v j i) -> p v i j", v=4, i=2)
+            nc.scalar.copy(out=gains[:], in_=planes)
+            nc.scalar.copy(out=gains_swapped[:, :, 0, :], in_=planes[:, :, 1, :])
+            nc.scalar.copy(out=gains_swapped[:, :, 1, :], in_=planes[:, :, 0, :])
+
+        def spread_bias(s):
+            for c in CHUNK_ORDER:
+                spread = prep.tile([P, BANK], F32, tag="prep")
+                nc.tensor.matmul(
+                    spread[:], lhsT=ones[:], rhs=bias_rows[:, s, c * BANK : (c + 1) * BANK], start=True, stop=True
+                )
+                if c < 4:
+                    nc.scalar.copy(
+                        out=bias_sb[:, s, c].rearrange("p (h i j) -> p h i j", h=GROUP, i=2),
+                        in_=spread[:].rearrange("p (h j i) -> p h i j", h=GROUP, i=2),
+                    )
+                else:
+                    nc.scalar.copy(out=bias_sb[:, s, c], in_=spread[:])
+
+        def build_tables(s):
+            first = 0 if s == 0 else TILES
+            last = TILES if s == 0 else BLOCKS * TILES
+            n = last - first
+            coef = rope_sb[:, first:last, :].rearrange("p n (j c) -> p n c j", c=4)
+            for qk in range(2):
+                nc.gpsimd.tensor_tensor(
+                    out=table[:, first:last, 2 * qk],
+                    in0=coef[:, :, 0:4:3, :],
+                    in1=gains[:, 2 * s + qk].unsqueeze(1).to_broadcast([P, n, 2, PAIRS]),
+                    op=ALU.mult,
+                )
+                nc.gpsimd.tensor_tensor(
+                    out=table[:, first:last, 2 * qk + 1],
+                    in0=coef[:, :, 1:3, :],
+                    in1=gains_swapped[:, 2 * s + qk].unsqueeze(1).to_broadcast([P, n, 2, PAIRS]),
+                    op=ALU.mult,
+                )
+
+        def project(blk, s, t, c):
+            acc = sums.tile([P, BANK], F32)
+            for g in range(PASSES):
+                cols = slice((t * PASSES + g) * P, (t * PASSES + g + 1) * P)
+                nc.tensor.matmul_mx(
+                    out=acc[:],
+                    lhsT=x_codes[:, blk, cols].bitcast(FP8X4),
+                    lhsT_scale=x_planes[:, blk, cols],
+                    rhs=w_words[:, s, g, 2 * c * BANK : 2 * (c + 1) * BANK].bitcast(FP4X4),
+                    rhs_scale=w_planes[:, s, g, c * BANK : (c + 1) * BANK],
+                    start=(g == 0),
+                    stop=(g == PASSES - 1),
+                )
+            return acc
+
+        def store(blk, part, m, out_sb):
+            rows = outs[part][0, m * GROUP : (m + 1) * GROUP, blk * TILES * P : (blk + 1) * TILES * P, :]
+            nc.sync.dma_start(
+                out=rows.rearrange("h (p t) d -> p h (t d)", t=TILES),
+                in_=out_sb[:].rearrange("p h t d -> p h (t d)"),
+            )
+
+        def values_step(blk, s, m):
+            c = 4 + m
+            out_sb = result.tile([P, GROUP, TILES, DH], F32)
+            for t in range(TILES):
+                acc = project(blk, s, t, c)
+                nc.vector.tensor_tensor(
+                    out=out_sb[:, :, t, :],
+                    in0=acc[:].rearrange("p (h d) -> p h d", h=GROUP),
+                    in1=bias_sb[:, s, c].rearrange("p (h d) -> p h d", h=GROUP),
+                    op=ALU.add,
+                )
+            store(blk, 2, m, out_sb)
+
+        def rotated_step(blk, s, qk, m):
+            c = 2 * qk + m
+            tiles = slice(blk * TILES, (blk + 1) * TILES)
+            u = work.tile([P, TILES, GROUP, 2, PAIRS], F32)
+            squares = work.tile([P, TILES, GROUP, DH], BF16)
+            straight = work.tile([P, TILES, GROUP, 2, PAIRS], F32)
+            crossed = work.tile([P, TILES, GROUP, 2, PAIRS], F32)
+            sum_sq = work.tile([P, TILES * GROUP], F32)
+            rms = work.tile([P, TILES * GROUP], F32)
+            inv_rms = work.tile([P, TILES * GROUP], F32)
+            out_sb = result.tile([P, GROUP, TILES, DH], F32)
+
+            for t in range(TILES):
+                acc = project(blk, s, t, c)
+                nc.vector.tensor_tensor(
+                    out=u[:, t],
+                    in0=acc[:].rearrange("p (h j i) -> p h i j", h=GROUP, i=2),
+                    in1=bias_sb[:, s, c].rearrange("p (h i j) -> p h i j", h=GROUP, i=2),
+                    op=ALU.add,
+                )
+            for t in range(TILES):
+                for h in range(GROUP):
+                    nc.scalar.activation(
+                        out=squares[:, t, h, :],
+                        in_=u[:, t, h].rearrange("p i j -> p (i j)"),
+                        func=ACT.Square,
+                        accum_out=sum_sq[:, t * GROUP + h : t * GROUP + h + 1],
+                    )
+            nc.scalar.activation(out=rms[:], in_=sum_sq[:], func=ACT.Sqrt, bias=eps[:], scale=1.0 / DH)
+            nc.vector.reciprocal(out=inv_rms[:], in_=rms[:])
+            nc.vector.tensor_tensor(
+                out=straight[:].rearrange("p t h i j -> p t h (i j)"),
+                in0=u[:].rearrange("p t h i j -> p t h (i j)"),
+                in1=table[:, tiles, 2 * qk]
+                .rearrange("p t i j -> p t (i j)")
+                .unsqueeze(2)
+                .to_broadcast([P, TILES, GROUP, DH]),
+                op=ALU.mult,
+            )
+            nc.vector.tensor_tensor(
+                out=crossed[:, :, :, 0, :],
+                in0=u[:, :, :, 1, :],
+                in1=table[:, tiles, 2 * qk + 1, 0, :].unsqueeze(2).to_broadcast([P, TILES, GROUP, PAIRS]),
+                op=ALU.mult,
+            )
+            nc.gpsimd.tensor_tensor(
+                out=crossed[:, :, :, 1, :],
+                in0=u[:, :, :, 0, :],
+                in1=table[:, tiles, 2 * qk + 1, 1, :].unsqueeze(2).to_broadcast([P, TILES, GROUP, PAIRS]),
+                op=ALU.mult,
+            )
+            nc.gpsimd.tensor_tensor(
+                out=straight[:].rearrange("p t h i j -> p (t h i j)"),
+                in0=straight[:].rearrange("p t h i j -> p (t h i j)"),
+                in1=crossed[:].rearrange("p t h i j -> p (t h i j)"),
+                op=ALU.add,
+            )
+            for t in range(TILES):
+                for h in range(GROUP):
+                    nc.scalar.activation(
+                        out=out_sb[:, h, t, :].rearrange("p (j i) -> p j i", i=2),
+                        in_=straight[:, t, h].rearrange("p i j -> p j i"),
+                        func=ACT.Copy,
+                        scale=inv_rms[:, t * GROUP + h : t * GROUP + h + 1],
+                    )
+            store(blk, qk, m, out_sb)
+
+        def block_half(blk, m):
+            s = 0 if blk == 0 else 1
+            rotated_step(blk, s, 0, m)
+            rotated_step(blk, s, 1, m)
+            values_step(blk, s, m)
+
+        quantise_block(0)
+        spread_gains()
+        spread_bias(0)
+        build_tables(0)
+        block_half(0, 0)
+        for blk in range(1, BLOCKS):
+            quantise_block(blk)
+        spread_bias(1)
+        build_tables(1)
+        block_half(0, 1)
+        for blk in range(1, BLOCKS):
+            for m in range(2):
+                block_half(blk, m)

@@ -61,7 +61,8 @@ def tile_fluxjointattention_pa_kernel(
         tc.tile_pool(name="work", bufs=4) as work,
         tc.tile_pool(name="result", bufs=6) as result,
         tc.psum_pool(name="prep", bufs=2) as prep,
-        tc.psum_pool(name="sums", bufs=6) as sums,
+        tc.psum_pool(name="coefs", bufs=2) as coefs,
+        tc.psum_pool(name="sums", bufs=4) as sums,
     ):
         x_sb = keep.tile([P, BLOCKS, TILES, D_MODEL], BF16)
         x_codes = keep.tile([P, BLOCKS, TILES * PASSES * P], U32, align_bytes=64)
@@ -72,9 +73,9 @@ def tile_fluxjointattention_pa_kernel(
         gain_rows = keep.tile([P, 4 * DH], BF16)
         bias_sb = keep.tile([P, 2, CHUNKS, BANK], F32)
         gains = keep.tile([P, 4, 2, PAIRS], F32)
-        gains_swapped = keep.tile([P, 4, 2, PAIRS], F32)
         rope_sb = keep.tile([P, BLOCKS * TILES, 4 * PAIRS], BF16)
-        table = keep.tile([P, BLOCKS * TILES, 4, 2, PAIRS], F32)
+        table_v = keep.tile([P, 2, BLOCKS * TILES, DH + PAIRS], F32)
+        table_g = keep.tile([P, 2, BLOCKS * TILES, PAIRS], F32)
         ident = keep.tile([P, P], F32)
         ones = keep.tile([P, P], BF16)
         eps = keep.tile([P, 1], F32)
@@ -148,8 +149,6 @@ def tile_fluxjointattention_pa_kernel(
             nc.tensor.matmul(spread[:], lhsT=ones[:], rhs=gain_rows[:], start=True, stop=True)
             planes = spread[:].rearrange("p (v j i) -> p v i j", v=4, i=2)
             nc.scalar.copy(out=gains[:], in_=planes)
-            nc.scalar.copy(out=gains_swapped[:, :, 0, :], in_=planes[:, :, 1, :])
-            nc.scalar.copy(out=gains_swapped[:, :, 1, :], in_=planes[:, :, 0, :])
 
         def spread_bias(s):
             for c in CHUNK_ORDER:
@@ -171,18 +170,36 @@ def tile_fluxjointattention_pa_kernel(
             n = last - first
             coef = rope_sb[:, first:last, :].rearrange("p n (j c) -> p n c j", c=4)
             for qk in range(2):
+                gain = gains[:, 2 * s + qk]
                 nc.gpsimd.tensor_tensor(
-                    out=table[:, first:last, 2 * qk],
+                    out=table_v[:, qk, first:last, 0:DH].rearrange("p n (i j) -> p n i j", i=2),
                     in0=coef[:, :, 0:4:3, :],
-                    in1=gains[:, 2 * s + qk].unsqueeze(1).to_broadcast([P, n, 2, PAIRS]),
+                    in1=gain.unsqueeze(1).to_broadcast([P, n, 2, PAIRS]),
                     op=ALU.mult,
                 )
                 nc.gpsimd.tensor_tensor(
-                    out=table[:, first:last, 2 * qk + 1],
-                    in0=coef[:, :, 1:3, :],
-                    in1=gains_swapped[:, 2 * s + qk].unsqueeze(1).to_broadcast([P, n, 2, PAIRS]),
+                    out=table_v[:, qk, first:last, DH : DH + PAIRS],
+                    in0=coef[:, :, 1, :],
+                    in1=gain[:, 1, :].unsqueeze(1).to_broadcast([P, n, PAIRS]),
                     op=ALU.mult,
                 )
+                nc.gpsimd.tensor_tensor(
+                    out=table_g[:, qk, first:last, :],
+                    in0=coef[:, :, 2, :],
+                    in1=gain[:, 0, :].unsqueeze(1).to_broadcast([P, n, PAIRS]),
+                    op=ALU.mult,
+                )
+
+        def table_to_psum(blk, qk):
+            coef_ps = coefs.tile([P, TILES, DH + PAIRS], F32)
+            nc.tensor.matmul(
+                coef_ps[:].rearrange("p t f -> p (t f)"),
+                lhsT=ident[:],
+                rhs=table_v[:, qk, blk * TILES : (blk + 1) * TILES, :].rearrange("p t f -> p (t f)"),
+                start=True,
+                stop=True,
+            )
+            return coef_ps
 
         def project(blk, s, t, c):
             acc = sums.tile([P, BANK], F32)
@@ -219,7 +236,7 @@ def tile_fluxjointattention_pa_kernel(
                 )
             store(blk, 2, m, out_sb)
 
-        def rotated_step(blk, s, qk, m):
+        def rotated_step(blk, s, qk, m, coef_ps):
             c = 2 * qk + m
             tiles = slice(blk * TILES, (blk + 1) * TILES)
             u = work.tile([P, TILES, GROUP, 2, PAIRS], F32)
@@ -252,22 +269,19 @@ def tile_fluxjointattention_pa_kernel(
             nc.vector.tensor_tensor(
                 out=straight[:].rearrange("p t h i j -> p t h (i j)"),
                 in0=u[:].rearrange("p t h i j -> p t h (i j)"),
-                in1=table[:, tiles, 2 * qk]
-                .rearrange("p t i j -> p t (i j)")
-                .unsqueeze(2)
-                .to_broadcast([P, TILES, GROUP, DH]),
+                in1=coef_ps[:, :, 0:DH].unsqueeze(2).to_broadcast([P, TILES, GROUP, DH]),
                 op=ALU.mult,
             )
             nc.vector.tensor_tensor(
                 out=crossed[:, :, :, 0, :],
                 in0=u[:, :, :, 1, :],
-                in1=table[:, tiles, 2 * qk + 1, 0, :].unsqueeze(2).to_broadcast([P, TILES, GROUP, PAIRS]),
+                in1=coef_ps[:, :, DH : DH + PAIRS].unsqueeze(2).to_broadcast([P, TILES, GROUP, PAIRS]),
                 op=ALU.mult,
             )
             nc.gpsimd.tensor_tensor(
                 out=crossed[:, :, :, 1, :],
                 in0=u[:, :, :, 0, :],
-                in1=table[:, tiles, 2 * qk + 1, 1, :].unsqueeze(2).to_broadcast([P, TILES, GROUP, PAIRS]),
+                in1=table_g[:, qk, tiles, :].unsqueeze(2).to_broadcast([P, TILES, GROUP, PAIRS]),
                 op=ALU.mult,
             )
             nc.gpsimd.tensor_tensor(
@@ -286,22 +300,26 @@ def tile_fluxjointattention_pa_kernel(
                     )
             store(blk, qk, m, out_sb)
 
-        def block_half(blk, m):
+        def block_half(blk, m, coef_q, coef_k):
             s = 0 if blk == 0 else 1
-            rotated_step(blk, s, 0, m)
-            rotated_step(blk, s, 1, m)
+            rotated_step(blk, s, 0, m, coef_q)
+            rotated_step(blk, s, 1, m, coef_k)
             values_step(blk, s, m)
 
         quantise_block(0)
         spread_gains()
         spread_bias(0)
         build_tables(0)
-        block_half(0, 0)
+        coef_q = table_to_psum(0, 0)
+        coef_k = table_to_psum(0, 1)
+        block_half(0, 0, coef_q, coef_k)
         for blk in range(1, BLOCKS):
             quantise_block(blk)
         spread_bias(1)
         build_tables(1)
-        block_half(0, 1)
+        block_half(0, 1, coef_q, coef_k)
         for blk in range(1, BLOCKS):
+            coef_q = table_to_psum(blk, 0)
+            coef_k = table_to_psum(blk, 1)
             for m in range(2):
-                block_half(blk, m)
+                block_half(blk, m, coef_q, coef_k)

@@ -57,17 +57,18 @@ def tile_fluxjointattention_pa_kernel(
 
     with (
         tc.tile_pool(name="keep", bufs=1) as keep,
-        tc.tile_pool(name="stage", bufs=2) as stage,
+        tc.tile_pool(name="stage", bufs=3) as stage,
         tc.tile_pool(name="work", bufs=4) as work,
         tc.tile_pool(name="result", bufs=6) as result,
         tc.psum_pool(name="prep", bufs=2) as prep,
         tc.psum_pool(name="coefs", bufs=2) as coefs,
         tc.psum_pool(name="sums", bufs=4) as sums,
+        tc.manual_schedule(),
     ):
         x_sb = keep.tile([P, BLOCKS, TILES, D_MODEL], BF16)
-        x_codes = keep.tile([P, BLOCKS, TILES * PASSES * P], U32, align_bytes=64)
-        x_planes = keep.tile([P, BLOCKS, TILES * PASSES * P], U8, align_bytes=64)
-        w_words = keep.tile([P, 2, PASSES, 2 * N_OUT], U8, align_bytes=64)
+        x_codes = keep.tile([P, BLOCKS, TILES, PASSES * P], U32, align_bytes=64)
+        x_planes = keep.tile([P, BLOCKS, TILES, PASSES * P], U8, align_bytes=64)
+        w_words = keep.tile([P, 2, CHUNKS, PASSES, 2 * BANK], U8, align_bytes=64)
         w_planes = keep.tile([P, 2, PASSES, N_OUT], U8, align_bytes=64)
         bias_rows = keep.tile([P, 2, N_OUT], BF16)
         gain_rows = keep.tile([P, 4 * DH], BF16)
@@ -81,13 +82,13 @@ def tile_fluxjointattention_pa_kernel(
         eps = keep.tile([P, 1], F32)
 
         nc.vector.memset(w_planes[:, 0].rearrange("p g n -> p (g n)").bitcast(I32), 0)
-        nc.vector.memset(gain_rows[:].bitcast(I32), 0)
         nc.vector.memset(bias_rows[:, 0].bitcast(I32), 0)
+        nc.vector.memset(gain_rows[:].bitcast(I32), 0)
         nc.vector.memset(ones[:], 1.0)
         nc.vector.memset(eps[:], EPS)
+        make_identity(nc, ident[:])
         nc.gpsimd.memset(w_planes[:, 1].rearrange("p g n -> p (g n)").bitcast(F32), 0.0)
         nc.gpsimd.memset(bias_rows[:, 1].bitcast(F32), 0.0)
-        make_identity(nc, ident[:])
 
         def load_x(blk):
             if blk == 0:
@@ -96,73 +97,94 @@ def tile_fluxjointattention_pa_kernel(
                 rows = hidden_states_a[0, (blk - 1) * TILES * P : blk * TILES * P, :]
             nc.sync.dma_start(out=x_sb[:, blk], in_=rows.rearrange("(p t) k -> p t k", t=TILES))
 
-        def load_weights(s):
+        def load_scales(s):
             planes = w_planes[:, s].bitcast(I32)
             rows = scales_in[s].bitcast(I32)
             for r in range(4):
                 nc.sync.dma_start(out=planes[r:P:32], in_=rows[:, r:16:4, :].rearrange("g q n -> q g n"))
-            words = w_words[:].bitcast(I32)
-            width = 2 * BANK // 4
-            for c in CHUNK_ORDER:
-                nc.sync.dma_start(
-                    out=words[:, s, :, c * width : (c + 1) * width],
-                    in_=words_in[s].bitcast(I32)[:, :, c * width : (c + 1) * width].rearrange("g p n -> p g n"),
-                )
 
-        for v in range(4):
-            nc.scalar.dma_start(
-                out=gain_rows[0:1, v * DH : (v + 1) * DH], in_=gain_in[v].rearrange("(o n) -> o n", o=1)
+        def load_words(s, c):
+            width = 2 * BANK // 4
+            nc.sync.dma_start(
+                out=w_words[:, s, c].bitcast(I32),
+                in_=words_in[s].bitcast(I32)[:, :, c * width : (c + 1) * width].rearrange("g p n -> p g n"),
             )
-        nc.scalar.dma_start(
-            out=rope_sb[:].rearrange("p (k t) f -> p k (t f)", t=TILES),
-            in_=image_rotary_emb.rearrange("a b (k p t) j r c -> p (a b k) (t j r c)", p=P, t=TILES),
-        )
-        for s in range(2):
-            nc.scalar.dma_start(out=bias_rows[0:1, s, :], in_=bias_in[s].rearrange("(o n) -> o n", o=1))
+
+        def load_vectors(s, queue):
+            first = 0 if s == 0 else 1
+            last = 1 if s == 0 else BLOCKS
+            queue.dma_start(out=bias_rows[0:1, s, :], in_=bias_in[s].rearrange("(o n) -> o n", o=1))
+            for v in (2 * s, 2 * s + 1):
+                queue.dma_start(
+                    out=gain_rows[0:1, v * DH : (v + 1) * DH], in_=gain_in[v].rearrange("(o n) -> o n", o=1)
+                )
+            queue.dma_start(
+                out=rope_sb[:, first * TILES : last * TILES, :].rearrange("p (k t) f -> p k (t f)", t=TILES),
+                in_=image_rotary_emb.rearrange("a b (k p t) j r c -> p (a b k) (t j r c)", p=P, t=TILES)[
+                    :, first:last, :
+                ],
+            )
+
         load_x(0)
-        load_weights(0)
+        load_scales(0)
+        load_words(0, CHUNK_ORDER[0])
+        load_vectors(0, nc.scalar)
+        for c in CHUNK_ORDER[1:]:
+            load_words(0, c)
         for blk in range(1, BLOCKS):
             load_x(blk)
-        load_weights(1)
+        load_vectors(1, nc.sync)
+        load_scales(1)
+        for c in CHUNK_ORDER:
+            load_words(1, c)
 
-        def quantise_block(blk):
+        grouped_x = {}
+
+        def transpose_tile(blk, t):
             x_pairs = x_sb[:].bitcast(F32)
-            grouped = stage.tile([P, TILES, PASSES, P, 2], F32, align_bytes=64)
-            for t in range(TILES):
-                x_t = prep.tile([P, PASSES * 2, P], F32, tag="prep")
-                for g in range(PASSES):
-                    for u in range(2):
-                        nc.tensor.transpose(
-                            x_t[:, 2 * g + u, :],
-                            x_pairs[:, blk, t, 256 * g + u : 256 * (g + 1) : 2],
-                            ident[:],
-                        )
-                nc.scalar.copy(out=grouped[:, t], in_=x_t[:].rearrange("p (g u) r -> p g r u", u=2))
+            x_t = prep.tile([P, PASSES * 2, P], F32, tag="prep")
+            for g in range(PASSES):
+                for u in range(2):
+                    nc.tensor.transpose(
+                        x_t[:, 2 * g + u, :], x_pairs[:, blk, t, 256 * g + u : 256 * (g + 1) : 2], ident[:]
+                    )
+            grouped = stage.tile([P, PASSES, P, 2], F32, align_bytes=64)
+            nc.scalar.copy(out=grouped[:], in_=x_t[:].rearrange("p (g u) r -> p g r u", u=2))
+            grouped_x[(blk, t)] = grouped
+
+        def quantise_tile(blk, t):
             nc.vector.quantize_mx(
-                out=x_codes[:, blk, :].bitcast(FP8X4),
-                scales=x_planes[:, blk, :],
-                in_=grouped[:].rearrange("p t g r u -> p (t g r u)").bitcast(BF16),
+                out=x_codes[:, blk, t, :].bitcast(FP8X4),
+                scales=x_planes[:, blk, t, :],
+                in_=grouped_x[(blk, t)][:].rearrange("p g r u -> p (g r u)").bitcast(BF16),
             )
 
-        def spread_gains():
+        def spread_gains(s):
             spread = prep.tile([P, BANK], F32, tag="prep")
-            nc.tensor.matmul(spread[:], lhsT=ones[:], rhs=gain_rows[:], start=True, stop=True)
-            planes = spread[:].rearrange("p (v j i) -> p v i j", v=4, i=2)
-            nc.scalar.copy(out=gains[:], in_=planes)
+            nc.tensor.matmul(
+                spread[:, 0 : 2 * DH],
+                lhsT=ones[:],
+                rhs=gain_rows[:, 2 * s * DH : 2 * (s + 1) * DH],
+                start=True,
+                stop=True,
+            )
+            nc.scalar.copy(
+                out=gains[:, 2 * s : 2 * (s + 1)],
+                in_=spread[:, 0 : 2 * DH].rearrange("p (v j i) -> p v i j", v=2, i=2),
+            )
 
-        def spread_bias(s):
-            for c in CHUNK_ORDER:
-                spread = prep.tile([P, BANK], F32, tag="prep")
-                nc.tensor.matmul(
-                    spread[:], lhsT=ones[:], rhs=bias_rows[:, s, c * BANK : (c + 1) * BANK], start=True, stop=True
+        def spread_bias(s, c):
+            spread = prep.tile([P, BANK], F32, tag="prep")
+            nc.tensor.matmul(
+                spread[:], lhsT=ones[:], rhs=bias_rows[:, s, c * BANK : (c + 1) * BANK], start=True, stop=True
+            )
+            if c < 4:
+                nc.scalar.copy(
+                    out=bias_sb[:, s, c].rearrange("p (h i j) -> p h i j", h=GROUP, i=2),
+                    in_=spread[:].rearrange("p (h j i) -> p h i j", h=GROUP, i=2),
                 )
-                if c < 4:
-                    nc.scalar.copy(
-                        out=bias_sb[:, s, c].rearrange("p (h i j) -> p h i j", h=GROUP, i=2),
-                        in_=spread[:].rearrange("p (h j i) -> p h i j", h=GROUP, i=2),
-                    )
-                else:
-                    nc.scalar.copy(out=bias_sb[:, s, c], in_=spread[:])
+            else:
+                nc.scalar.copy(out=bias_sb[:, s, c], in_=spread[:])
 
         def build_tables(s):
             first = 0 if s == 0 else TILES
@@ -171,13 +193,13 @@ def tile_fluxjointattention_pa_kernel(
             coef = rope_sb[:, first:last, :].rearrange("p n (j c) -> p n c j", c=4)
             for qk in range(2):
                 gain = gains[:, 2 * s + qk]
-                nc.gpsimd.tensor_tensor(
+                nc.vector.tensor_tensor(
                     out=table_v[:, qk, first:last, 0:DH].rearrange("p n (i j) -> p n i j", i=2),
                     in0=coef[:, :, 0:4:3, :],
                     in1=gain.unsqueeze(1).to_broadcast([P, n, 2, PAIRS]),
                     op=ALU.mult,
                 )
-                nc.gpsimd.tensor_tensor(
+                nc.vector.tensor_tensor(
                     out=table_v[:, qk, first:last, DH : DH + PAIRS],
                     in0=coef[:, :, 1, :],
                     in1=gain[:, 1, :].unsqueeze(1).to_broadcast([P, n, PAIRS]),
@@ -190,72 +212,82 @@ def tile_fluxjointattention_pa_kernel(
                     op=ALU.mult,
                 )
 
-        def table_to_psum(blk, qk):
-            coef_ps = coefs.tile([P, TILES, DH + PAIRS], F32)
-            nc.tensor.matmul(
-                coef_ps[:].rearrange("p t f -> p (t f)"),
-                lhsT=ident[:],
-                rhs=table_v[:, qk, blk * TILES : (blk + 1) * TILES, :].rearrange("p t f -> p (t f)"),
-                start=True,
-                stop=True,
-            )
-            return coef_ps
+        steps = [(blk, m, part) for blk in range(BLOCKS) for m in range(2) for part in range(3)]
+        live = {}
+        coef_ps = {}
+        sums_ps = {}
 
-        def project(blk, s, t, c):
-            acc = sums.tile([P, BANK], F32)
-            for g in range(PASSES):
-                cols = slice((t * PASSES + g) * P, (t * PASSES + g + 1) * P)
-                nc.tensor.matmul_mx(
-                    out=acc[:],
-                    lhsT=x_codes[:, blk, cols].bitcast(FP8X4),
-                    lhsT_scale=x_planes[:, blk, cols],
-                    rhs=w_words[:, s, g, 2 * c * BANK : 2 * (c + 1) * BANK].bitcast(FP4X4),
-                    rhs_scale=w_planes[:, s, g, c * BANK : (c + 1) * BANK],
-                    start=(g == 0),
-                    stop=(g == PASSES - 1),
-                )
-            return acc
+        def stage_project(n):
+            blk, m, part = steps[n]
+            s = 0 if blk == 0 else 1
+            c = 2 * part + m
+            for t in range(TILES):
+                acc = sums.tile([P, BANK], F32)
+                for g in range(PASSES):
+                    nc.tensor.matmul_mx(
+                        out=acc[:],
+                        lhsT=x_codes[:, blk, t, g * P : (g + 1) * P].bitcast(FP8X4),
+                        lhsT_scale=x_planes[:, blk, t, g * P : (g + 1) * P],
+                        rhs=w_words[:, s, c, g, :].bitcast(FP4X4),
+                        rhs_scale=w_planes[:, s, g, c * BANK : (c + 1) * BANK],
+                        start=(g == 0),
+                        stop=(g == PASSES - 1),
+                    )
+                sums_ps[(n, t)] = acc
 
-        def store(blk, part, m, out_sb):
+        def store(n, out_sb):
+            blk, m, part = steps[n]
             rows = outs[part][0, m * GROUP : (m + 1) * GROUP, blk * TILES * P : (blk + 1) * TILES * P, :]
             nc.sync.dma_start(
                 out=rows.rearrange("h (p t) d -> p h (t d)", t=TILES),
                 in_=out_sb[:].rearrange("p h t d -> p h (t d)"),
             )
 
-        def values_step(blk, s, m):
-            c = 4 + m
-            out_sb = result.tile([P, GROUP, TILES, DH], F32)
-            for t in range(TILES):
-                acc = project(blk, s, t, c)
-                nc.vector.tensor_tensor(
-                    out=out_sb[:, :, t, :],
-                    in0=acc[:].rearrange("p (h d) -> p h d", h=GROUP),
-                    in1=bias_sb[:, s, c].rearrange("p (h d) -> p h d", h=GROUP),
-                    op=ALU.add,
-                )
-            store(blk, 2, m, out_sb)
+        def stage_bias(n):
+            blk, m, part = steps[n]
+            s = 0 if blk == 0 else 1
+            c = 2 * part + m
+            if part == 2:
+                out_sb = result.tile([P, GROUP, TILES, DH], F32)
+                for t in range(TILES):
+                    nc.vector.tensor_tensor(
+                        out=out_sb[:, :, t, :],
+                        in0=sums_ps[(n, t)][:].rearrange("p (h d) -> p h d", h=GROUP),
+                        in1=bias_sb[:, s, c].rearrange("p (h d) -> p h d", h=GROUP),
+                        op=ALU.add,
+                    )
+                store(n, out_sb)
+            else:
+                u = work.tile([P, TILES, GROUP, 2, PAIRS], F32)
+                for t in range(TILES):
+                    nc.vector.tensor_tensor(
+                        out=u[:, t],
+                        in0=sums_ps[(n, t)][:].rearrange("p (h j i) -> p h i j", h=GROUP, i=2),
+                        in1=bias_sb[:, s, c].rearrange("p (h i j) -> p h i j", h=GROUP, i=2),
+                        op=ALU.add,
+                    )
+                live[n] = {"u": u}
 
-        def rotated_step(blk, s, qk, m, coef_ps):
-            c = 2 * qk + m
-            tiles = slice(blk * TILES, (blk + 1) * TILES)
-            u = work.tile([P, TILES, GROUP, 2, PAIRS], F32)
+        def stage_coefficients(n):
+            blk, m, part = steps[n]
+            coef = coefs.tile([P, TILES, DH + PAIRS], F32)
+            nc.tensor.matmul(
+                coef[:].rearrange("p t f -> p (t f)"),
+                lhsT=ident[:],
+                rhs=table_v[:, part, blk * TILES : (blk + 1) * TILES, :].rearrange("p t f -> p (t f)"),
+                start=True,
+                stop=True,
+            )
+            coef_ps[(blk, part)] = coef
+
+        def stage_products(n):
+            blk, m, part = steps[n]
+            u = live[n]["u"]
+            coef = coef_ps[(blk, part)]
             squares = work.tile([P, TILES, GROUP, DH], BF16)
+            sum_sq = work.tile([P, TILES * GROUP], F32)
             straight = work.tile([P, TILES, GROUP, 2, PAIRS], F32)
             crossed = work.tile([P, TILES, GROUP, 2, PAIRS], F32)
-            sum_sq = work.tile([P, TILES * GROUP], F32)
-            rms = work.tile([P, TILES * GROUP], F32)
-            inv_rms = work.tile([P, TILES * GROUP], F32)
-            out_sb = result.tile([P, GROUP, TILES, DH], F32)
-
-            for t in range(TILES):
-                acc = project(blk, s, t, c)
-                nc.vector.tensor_tensor(
-                    out=u[:, t],
-                    in0=acc[:].rearrange("p (h j i) -> p h i j", h=GROUP, i=2),
-                    in1=bias_sb[:, s, c].rearrange("p (h i j) -> p h i j", h=GROUP, i=2),
-                    op=ALU.add,
-                )
             for t in range(TILES):
                 for h in range(GROUP):
                     nc.scalar.activation(
@@ -264,62 +296,105 @@ def tile_fluxjointattention_pa_kernel(
                         func=ACT.Square,
                         accum_out=sum_sq[:, t * GROUP + h : t * GROUP + h + 1],
                     )
-            nc.scalar.activation(out=rms[:], in_=sum_sq[:], func=ACT.Sqrt, bias=eps[:], scale=1.0 / DH)
-            nc.vector.reciprocal(out=inv_rms[:], in_=rms[:])
             nc.vector.tensor_tensor(
                 out=straight[:].rearrange("p t h i j -> p t h (i j)"),
                 in0=u[:].rearrange("p t h i j -> p t h (i j)"),
-                in1=coef_ps[:, :, 0:DH].unsqueeze(2).to_broadcast([P, TILES, GROUP, DH]),
+                in1=coef[:, :, 0:DH].unsqueeze(2).to_broadcast([P, TILES, GROUP, DH]),
                 op=ALU.mult,
             )
             nc.vector.tensor_tensor(
                 out=crossed[:, :, :, 0, :],
                 in0=u[:, :, :, 1, :],
-                in1=coef_ps[:, :, DH : DH + PAIRS].unsqueeze(2).to_broadcast([P, TILES, GROUP, PAIRS]),
+                in1=coef[:, :, DH : DH + PAIRS].unsqueeze(2).to_broadcast([P, TILES, GROUP, PAIRS]),
                 op=ALU.mult,
             )
             nc.gpsimd.tensor_tensor(
                 out=crossed[:, :, :, 1, :],
                 in0=u[:, :, :, 0, :],
-                in1=table_g[:, qk, tiles, :].unsqueeze(2).to_broadcast([P, TILES, GROUP, PAIRS]),
+                in1=table_g[:, part, blk * TILES : (blk + 1) * TILES, :]
+                .unsqueeze(2)
+                .to_broadcast([P, TILES, GROUP, PAIRS]),
                 op=ALU.mult,
             )
+            live[n]["sum_sq"] = sum_sq
+            live[n]["straight"] = straight
+            live[n]["crossed"] = crossed
+
+        def stage_root(n):
+            rms = work.tile([P, TILES * GROUP], F32)
+            nc.scalar.activation(out=rms[:], in_=live[n]["sum_sq"][:], func=ACT.Sqrt, bias=eps[:], scale=1.0 / DH)
+            live[n]["rms"] = rms
+
+        def stage_add(n):
+            inv_rms = work.tile([P, TILES * GROUP], F32)
+            nc.vector.reciprocal(out=inv_rms[:], in_=live[n]["rms"][:])
+            straight = live[n]["straight"]
             nc.gpsimd.tensor_tensor(
                 out=straight[:].rearrange("p t h i j -> p (t h i j)"),
                 in0=straight[:].rearrange("p t h i j -> p (t h i j)"),
-                in1=crossed[:].rearrange("p t h i j -> p (t h i j)"),
+                in1=live[n]["crossed"][:].rearrange("p t h i j -> p (t h i j)"),
                 op=ALU.add,
             )
+            live[n]["inv_rms"] = inv_rms
+
+        def stage_scale(n):
+            rotated = live[n]["straight"]
+            inv_rms = live[n]["inv_rms"]
+            out_sb = result.tile([P, GROUP, TILES, DH], F32)
             for t in range(TILES):
                 for h in range(GROUP):
                     nc.scalar.activation(
                         out=out_sb[:, h, t, :].rearrange("p (j i) -> p j i", i=2),
-                        in_=straight[:, t, h].rearrange("p i j -> p j i"),
+                        in_=rotated[:, t, h].rearrange("p i j -> p j i"),
                         func=ACT.Copy,
                         scale=inv_rms[:, t * GROUP + h : t * GROUP + h + 1],
                     )
-            store(blk, qk, m, out_sb)
+            store(n, out_sb)
 
-        def block_half(blk, m, coef_q, coef_k):
-            s = 0 if blk == 0 else 1
-            rotated_step(blk, s, 0, m, coef_q)
-            rotated_step(blk, s, 1, m, coef_k)
-            values_step(blk, s, m)
+        def is_rotated(n):
+            return 0 <= n < len(steps) and steps[n][2] < 2
 
-        quantise_block(0)
-        spread_gains()
-        spread_bias(0)
-        build_tables(0)
-        coef_q = table_to_psum(0, 0)
-        coef_k = table_to_psum(0, 1)
-        block_half(0, 0, coef_q, coef_k)
-        for blk in range(1, BLOCKS):
-            quantise_block(blk)
-        spread_bias(1)
-        build_tables(1)
-        block_half(0, 1, coef_q, coef_k)
-        for blk in range(1, BLOCKS):
-            coef_q = table_to_psum(blk, 0)
-            coef_k = table_to_psum(blk, 1)
-            for m in range(2):
-                block_half(blk, m, coef_q, coef_k)
+        def spread_bias_of(n):
+            if n < 2 * CHUNKS:
+                blk, m, part = steps[n]
+                spread_bias(blk, 2 * part + m)
+
+        def prepare(i):
+            spread_bias_of(i + 2)
+            blk, t = divmod(i + 5, 2 * 3)
+            if 1 <= blk < BLOCKS and t < TILES:
+                transpose_tile(blk, t)
+            blk, t = divmod(i + 4, 2 * 3)
+            if 1 <= blk < BLOCKS and t < TILES:
+                quantise_tile(blk, t)
+            if i == 0:
+                build_tables(0)
+            if i == 2:
+                spread_gains(1)
+            if i == 3:
+                build_tables(1)
+
+        for t in range(TILES):
+            transpose_tile(0, t)
+        for t in range(TILES):
+            quantise_tile(0, t)
+        spread_bias_of(0)
+        spread_bias_of(1)
+        stage_project(0)
+        spread_gains(0)
+        for i in range(len(steps) + 3):
+            if i + 1 < len(steps):
+                stage_project(i + 1)
+            if is_rotated(i - 1) and steps[i - 1][1] == 0:
+                stage_coefficients(i - 1)
+            if i < len(steps):
+                stage_bias(i)
+            if is_rotated(i - 1):
+                stage_products(i - 1)
+            if is_rotated(i - 3):
+                stage_scale(i - 3)
+            if is_rotated(i - 1):
+                stage_root(i - 1)
+            if is_rotated(i - 2):
+                stage_add(i - 2)
+            prepare(i)

@@ -75,8 +75,7 @@ def tile_fluxjointattention_pa_kernel(
         bias_sb = keep.tile([P, 2, CHUNKS, BANK], F32)
         gains = keep.tile([P, 4, 2, PAIRS], F32)
         rope_sb = keep.tile([P, BLOCKS * TILES, 4 * PAIRS], BF16)
-        table_v = keep.tile([P, 2, BLOCKS * TILES, DH + PAIRS], F32)
-        table_g = keep.tile([P, 2, BLOCKS * TILES, PAIRS], F32)
+        table = keep.tile([P, 2, BLOCKS * TILES, 2 * DH], F32)
         ident = keep.tile([P, P], F32)
         ones = keep.tile([P, P], BF16)
         eps = keep.tile([P, 1], F32)
@@ -194,23 +193,18 @@ def tile_fluxjointattention_pa_kernel(
             for qk in range(2):
                 gain = gains[:, 2 * s + qk]
                 nc.vector.tensor_tensor(
-                    out=table_v[:, qk, first:last, 0:DH].rearrange("p n (i j) -> p n i j", i=2),
+                    out=table[:, qk, first:last, 0:DH].rearrange("p n (i j) -> p n i j", i=2),
                     in0=coef[:, :, 0:4:3, :],
                     in1=gain.unsqueeze(1).to_broadcast([P, n, 2, PAIRS]),
                     op=ALU.mult,
                 )
-                nc.vector.tensor_tensor(
-                    out=table_v[:, qk, first:last, DH : DH + PAIRS],
-                    in0=coef[:, :, 1, :],
-                    in1=gain[:, 1, :].unsqueeze(1).to_broadcast([P, n, PAIRS]),
-                    op=ALU.mult,
-                )
-                nc.gpsimd.tensor_tensor(
-                    out=table_g[:, qk, first:last, :],
-                    in0=coef[:, :, 2, :],
-                    in1=gain[:, 0, :].unsqueeze(1).to_broadcast([P, n, PAIRS]),
-                    op=ALU.mult,
-                )
+                for i in range(2):
+                    nc.vector.tensor_tensor(
+                        out=table[:, qk, first:last, DH + i * PAIRS : DH + (i + 1) * PAIRS],
+                        in0=coef[:, :, 1 + i, :],
+                        in1=gain[:, 1 - i, :].unsqueeze(1).to_broadcast([P, n, PAIRS]),
+                        op=ALU.mult,
+                    )
 
         steps = [(blk, m, part) for blk in range(BLOCKS) for m in range(2) for part in range(3)]
         live = {}
@@ -270,11 +264,11 @@ def tile_fluxjointattention_pa_kernel(
 
         def stage_coefficients(n):
             blk, m, part = steps[n]
-            coef = coefs.tile([P, TILES, DH + PAIRS], F32)
+            coef = coefs.tile([P, TILES, 2 * DH], F32)
             nc.tensor.matmul(
                 coef[:].rearrange("p t f -> p (t f)"),
                 lhsT=ident[:],
-                rhs=table_v[:, part, blk * TILES : (blk + 1) * TILES, :].rearrange("p t f -> p (t f)"),
+                rhs=table[:, part, blk * TILES : (blk + 1) * TILES, :].rearrange("p t f -> p (t f)"),
                 start=True,
                 stop=True,
             )
@@ -302,20 +296,15 @@ def tile_fluxjointattention_pa_kernel(
                 in1=coef[:, :, 0:DH].unsqueeze(2).to_broadcast([P, TILES, GROUP, DH]),
                 op=ALU.mult,
             )
-            nc.vector.tensor_tensor(
-                out=crossed[:, :, :, 0, :],
-                in0=u[:, :, :, 1, :],
-                in1=coef[:, :, DH : DH + PAIRS].unsqueeze(2).to_broadcast([P, TILES, GROUP, PAIRS]),
-                op=ALU.mult,
-            )
-            nc.gpsimd.tensor_tensor(
-                out=crossed[:, :, :, 1, :],
-                in0=u[:, :, :, 0, :],
-                in1=table_g[:, part, blk * TILES : (blk + 1) * TILES, :]
-                .unsqueeze(2)
-                .to_broadcast([P, TILES, GROUP, PAIRS]),
-                op=ALU.mult,
-            )
+            for i in range(2):
+                nc.vector.tensor_tensor(
+                    out=crossed[:, :, :, i, :],
+                    in0=u[:, :, :, 1 - i, :],
+                    in1=coef[:, :, DH + i * PAIRS : DH + (i + 1) * PAIRS]
+                    .unsqueeze(2)
+                    .to_broadcast([P, TILES, GROUP, PAIRS]),
+                    op=ALU.mult,
+                )
             live[n]["sum_sq"] = sum_sq
             live[n]["straight"] = straight
             live[n]["crossed"] = crossed

@@ -24,7 +24,7 @@ CHUNKS = N_OUT // BANK
 TILES = 2
 BLOCKS = 4
 EPS = 1e-6
-CHUNK_ORDER = (0, 2, 4, 1, 3, 5)
+CHUNK_ORDER = (0, 4, 2, 1, 5, 3)
 
 FLOPS = 2 * BLOCKS * TILES * P * D_MODEL * N_OUT
 
@@ -58,7 +58,7 @@ def tile_fluxjointattention_pa_kernel(
     with (
         tc.tile_pool(name="keep", bufs=1) as keep,
         tc.tile_pool(name="stage", bufs=3) as stage,
-        tc.tile_pool(name="work", bufs=4) as work,
+        tc.tile_pool(name="work", bufs=5) as work,
         tc.tile_pool(name="result", bufs=6) as result,
         tc.psum_pool(name="prep", bufs=2) as prep,
         tc.psum_pool(name="coefs", bufs=2) as coefs,
@@ -69,25 +69,27 @@ def tile_fluxjointattention_pa_kernel(
         x_codes = keep.tile([P, BLOCKS, TILES, PASSES * P], U32, align_bytes=64)
         x_planes = keep.tile([P, BLOCKS, TILES, PASSES * P], U8, align_bytes=64)
         w_words = keep.tile([P, 2, CHUNKS, PASSES, 2 * BANK], U8, align_bytes=64)
-        w_planes = keep.tile([P, 2, PASSES, N_OUT], U8, align_bytes=64)
-        bias_rows = keep.tile([P, 2, N_OUT], BF16)
-        gain_rows = keep.tile([P, 4 * DH], BF16)
+        w_planes = [keep.tile([P, PASSES, N_OUT], U8, align_bytes=64, name="w_planes_%d" % s) for s in range(2)]
+        bias_vec = [keep.tile([P, BANK], BF16, name="bias_vec_%d" % s) for s in range(2)]
+        gain_vec = [keep.tile([P, 2 * DH], BF16, name="gain_vec_%d" % s) for s in range(2)]
         bias_sb = keep.tile([P, 2, CHUNKS, BANK], F32)
         gains = keep.tile([P, 4, 2, PAIRS], F32)
         rope_sb = keep.tile([P, BLOCKS * TILES, 4 * PAIRS], BF16)
-        table = keep.tile([P, 2, BLOCKS * TILES, 2 * DH], F32)
+        table_v = keep.tile([P, 2, BLOCKS * TILES, DH + PAIRS], F32)
+        table_g = keep.tile([P, 2, BLOCKS * TILES, PAIRS], F32)
         ident = keep.tile([P, P], F32)
-        ones = keep.tile([P, P], BF16)
+        ident_bf = keep.tile([P, P], BF16)
         eps = keep.tile([P, 1], F32)
 
-        nc.vector.memset(w_planes[:, 0].rearrange("p g n -> p (g n)").bitcast(I32), 0)
-        nc.vector.memset(bias_rows[:, 0].bitcast(I32), 0)
-        nc.vector.memset(gain_rows[:].bitcast(I32), 0)
-        nc.vector.memset(ones[:], 1.0)
+        nc.vector.memset(bias_vec[0][:].bitcast(I32), 0)
+        nc.vector.memset(w_planes[0][:].rearrange("p g n -> p (g n)").bitcast(I32), 0)
+        nc.vector.memset(gain_vec[0][:].bitcast(I32), 0)
+        nc.vector.memset(bias_vec[1][:].bitcast(I32), 0)
+        nc.vector.memset(gain_vec[1][:].bitcast(I32), 0)
         nc.vector.memset(eps[:], EPS)
+        nc.vector.memset(w_planes[1][:].rearrange("p g n -> p (g n)").bitcast(I32), 0)
         make_identity(nc, ident[:])
-        nc.gpsimd.memset(w_planes[:, 1].rearrange("p g n -> p (g n)").bitcast(F32), 0.0)
-        nc.gpsimd.memset(bias_rows[:, 1].bitcast(F32), 0.0)
+        nc.vector.tensor_copy(out=ident_bf[:], in_=ident[:])
 
         def load_x(blk):
             if blk == 0:
@@ -97,7 +99,7 @@ def tile_fluxjointattention_pa_kernel(
             nc.sync.dma_start(out=x_sb[:, blk], in_=rows.rearrange("(p t) k -> p t k", t=TILES))
 
         def load_scales(s):
-            planes = w_planes[:, s].bitcast(I32)
+            planes = w_planes[s][:].bitcast(I32)
             rows = scales_in[s].bitcast(I32)
             for r in range(4):
                 nc.sync.dma_start(out=planes[r:P:32], in_=rows[:, r:16:4, :].rearrange("g q n -> q g n"))
@@ -109,13 +111,16 @@ def tile_fluxjointattention_pa_kernel(
                 in_=words_in[s].bitcast(I32)[:, :, c * width : (c + 1) * width].rearrange("g p n -> p g n"),
             )
 
-        def load_vectors(s, queue):
+        def load_bias(s, queue):
+            queue.dma_start(out=bias_vec[s][0:CHUNKS, :], in_=bias_in[s].rearrange("(c n) -> c n", c=CHUNKS))
+
+        def load_rotation(s, queue):
             first = 0 if s == 0 else 1
             last = 1 if s == 0 else BLOCKS
-            queue.dma_start(out=bias_rows[0:1, s, :], in_=bias_in[s].rearrange("(o n) -> o n", o=1))
-            for v in (2 * s, 2 * s + 1):
+            for qk in range(2):
                 queue.dma_start(
-                    out=gain_rows[0:1, v * DH : (v + 1) * DH], in_=gain_in[v].rearrange("(o n) -> o n", o=1)
+                    out=gain_vec[s][0:1, qk * DH : (qk + 1) * DH],
+                    in_=gain_in[2 * s + qk].rearrange("(o n) -> o n", o=1),
                 )
             queue.dma_start(
                 out=rope_sb[:, first * TILES : last * TILES, :].rearrange("p (k t) f -> p k (t f)", t=TILES),
@@ -125,14 +130,19 @@ def tile_fluxjointattention_pa_kernel(
             )
 
         load_x(0)
+        load_bias(0, nc.sync)
         load_scales(0)
         load_words(0, CHUNK_ORDER[0])
-        load_vectors(0, nc.scalar)
-        for c in CHUNK_ORDER[1:]:
+        load_words(0, CHUNK_ORDER[1])
+        load_rotation(0, nc.sync)
+        load_words(0, CHUNK_ORDER[2])
+        load_x(1)
+        for c in CHUNK_ORDER[3:]:
             load_words(0, c)
-        for blk in range(1, BLOCKS):
+        for blk in range(2, BLOCKS):
             load_x(blk)
-        load_vectors(1, nc.sync)
+        load_bias(1, nc.sync)
+        load_rotation(1, nc.sync)
         load_scales(1)
         for c in CHUNK_ORDER:
             load_words(1, c)
@@ -158,12 +168,15 @@ def tile_fluxjointattention_pa_kernel(
                 in_=grouped_x[(blk, t)][:].rearrange("p g r u -> p (g r u)").bitcast(BF16),
             )
 
+        def row_selector(row):
+            return ident_bf[:, row : row + 1].to_broadcast([P, P])
+
         def spread_gains(s):
             spread = prep.tile([P, BANK], F32, tag="prep")
             nc.tensor.matmul(
                 spread[:, 0 : 2 * DH],
-                lhsT=ones[:],
-                rhs=gain_rows[:, 2 * s * DH : 2 * (s + 1) * DH],
+                lhsT=row_selector(0),
+                rhs=gain_vec[s][:],
                 start=True,
                 stop=True,
             )
@@ -174,9 +187,7 @@ def tile_fluxjointattention_pa_kernel(
 
         def spread_bias(s, c):
             spread = prep.tile([P, BANK], F32, tag="prep")
-            nc.tensor.matmul(
-                spread[:], lhsT=ones[:], rhs=bias_rows[:, s, c * BANK : (c + 1) * BANK], start=True, stop=True
-            )
+            nc.tensor.matmul(spread[:], lhsT=row_selector(c), rhs=bias_vec[s][:], start=True, stop=True)
             if c < 4:
                 nc.scalar.copy(
                     out=bias_sb[:, s, c].rearrange("p (h i j) -> p h i j", h=GROUP, i=2),
@@ -193,20 +204,25 @@ def tile_fluxjointattention_pa_kernel(
             for qk in range(2):
                 gain = gains[:, 2 * s + qk]
                 nc.vector.tensor_tensor(
-                    out=table[:, qk, first:last, 0:DH].rearrange("p n (i j) -> p n i j", i=2),
+                    out=table_v[:, qk, first:last, 0:DH].rearrange("p n (i j) -> p n i j", i=2),
                     in0=coef[:, :, 0:4:3, :],
                     in1=gain.unsqueeze(1).to_broadcast([P, n, 2, PAIRS]),
                     op=ALU.mult,
                 )
-                for i in range(2):
-                    nc.vector.tensor_tensor(
-                        out=table[:, qk, first:last, DH + i * PAIRS : DH + (i + 1) * PAIRS],
-                        in0=coef[:, :, 1 + i, :],
-                        in1=gain[:, 1 - i, :].unsqueeze(1).to_broadcast([P, n, PAIRS]),
-                        op=ALU.mult,
-                    )
+                nc.vector.tensor_tensor(
+                    out=table_v[:, qk, first:last, DH : DH + PAIRS],
+                    in0=coef[:, :, 1, :],
+                    in1=gain[:, 1, :].unsqueeze(1).to_broadcast([P, n, PAIRS]),
+                    op=ALU.mult,
+                )
+                nc.gpsimd.tensor_tensor(
+                    out=table_g[:, qk, first:last, :],
+                    in0=coef[:, :, 2, :],
+                    in1=gain[:, 0, :].unsqueeze(1).to_broadcast([P, n, PAIRS]),
+                    op=ALU.mult,
+                )
 
-        steps = [(blk, m, part) for blk in range(BLOCKS) for m in range(2) for part in range(3)]
+        steps = [(blk, m, part) for blk in range(BLOCKS) for m in range(2) for part in (0, 2, 1)]
         live = {}
         coef_ps = {}
         sums_ps = {}
@@ -223,7 +239,7 @@ def tile_fluxjointattention_pa_kernel(
                         lhsT=x_codes[:, blk, t, g * P : (g + 1) * P].bitcast(FP8X4),
                         lhsT_scale=x_planes[:, blk, t, g * P : (g + 1) * P],
                         rhs=w_words[:, s, c, g, :].bitcast(FP4X4),
-                        rhs_scale=w_planes[:, s, g, c * BANK : (c + 1) * BANK],
+                        rhs_scale=w_planes[s][:, g, c * BANK : (c + 1) * BANK],
                         start=(g == 0),
                         stop=(g == PASSES - 1),
                     )
@@ -264,11 +280,11 @@ def tile_fluxjointattention_pa_kernel(
 
         def stage_coefficients(n):
             blk, m, part = steps[n]
-            coef = coefs.tile([P, TILES, 2 * DH], F32)
+            coef = coefs.tile([P, TILES, DH + PAIRS], F32)
             nc.tensor.matmul(
                 coef[:].rearrange("p t f -> p (t f)"),
                 lhsT=ident[:],
-                rhs=table[:, part, blk * TILES : (blk + 1) * TILES, :].rearrange("p t f -> p (t f)"),
+                rhs=table_v[:, part, blk * TILES : (blk + 1) * TILES, :].rearrange("p t f -> p (t f)"),
                 start=True,
                 stop=True,
             )
@@ -296,15 +312,20 @@ def tile_fluxjointattention_pa_kernel(
                 in1=coef[:, :, 0:DH].unsqueeze(2).to_broadcast([P, TILES, GROUP, DH]),
                 op=ALU.mult,
             )
-            for i in range(2):
-                nc.vector.tensor_tensor(
-                    out=crossed[:, :, :, i, :],
-                    in0=u[:, :, :, 1 - i, :],
-                    in1=coef[:, :, DH + i * PAIRS : DH + (i + 1) * PAIRS]
-                    .unsqueeze(2)
-                    .to_broadcast([P, TILES, GROUP, PAIRS]),
-                    op=ALU.mult,
-                )
+            nc.vector.tensor_tensor(
+                out=crossed[:, :, :, 0, :],
+                in0=u[:, :, :, 1, :],
+                in1=coef[:, :, DH : DH + PAIRS].unsqueeze(2).to_broadcast([P, TILES, GROUP, PAIRS]),
+                op=ALU.mult,
+            )
+            nc.gpsimd.tensor_tensor(
+                out=crossed[:, :, :, 1, :],
+                in0=u[:, :, :, 0, :],
+                in1=table_g[:, part, blk * TILES : (blk + 1) * TILES, :]
+                .unsqueeze(2)
+                .to_broadcast([P, TILES, GROUP, PAIRS]),
+                op=ALU.mult,
+            )
             live[n]["sum_sq"] = sum_sq
             live[n]["straight"] = straight
             live[n]["crossed"] = crossed
@@ -378,12 +399,12 @@ def tile_fluxjointattention_pa_kernel(
                 stage_coefficients(i - 1)
             if i < len(steps):
                 stage_bias(i)
+            if is_rotated(i - 2):
+                stage_add(i - 2)
             if is_rotated(i - 1):
                 stage_products(i - 1)
             if is_rotated(i - 3):
                 stage_scale(i - 3)
             if is_rotated(i - 1):
                 stage_root(i - 1)
-            if is_rotated(i - 2):
-                stage_add(i - 2)
             prepare(i)

@@ -136,13 +136,13 @@ def tile_fluxjointattention_pa_kernel(
         load_words(0, CHUNK_ORDER[1])
         load_rotation(0, nc.sync)
         load_words(0, CHUNK_ORDER[2])
+        load_rotation(1, nc.sync)
         load_x(1)
         for c in CHUNK_ORDER[3:]:
             load_words(0, c)
         for blk in range(2, BLOCKS):
             load_x(blk)
         load_bias(1, nc.sync)
-        load_rotation(1, nc.sync)
         load_scales(1)
         for c in CHUNK_ORDER:
             load_words(1, c)
@@ -379,9 +379,8 @@ def tile_fluxjointattention_pa_kernel(
                 quantise_tile(blk, t)
             if i == 0:
                 build_tables(0)
-            if i == 2:
                 spread_gains(1)
-            if i == 3:
+            if i == 1:
                 build_tables(1)
 
         for t in range(TILES):

@@ -16,6 +16,7 @@ D_MODEL = 1024
 K_PASS = 512
 PASSES = D_MODEL // K_PASS
 DH = 128
+HEADS = 8
 PAIRS = DH // 2
 GROUP = 4
 BANK = GROUP * DH
@@ -23,8 +24,11 @@ N_OUT = 3 * D_MODEL
 CHUNKS = N_OUT // BANK
 TILES = 2
 BLOCKS = 4
+NT = BLOCKS * TILES
 EPS = 1e-6
-CHUNK_ORDER = (0, 4, 2, 1, 5, 3)
+ROW_BLOCKS = (0, 3)
+COL_FIRST = 1
+COL_TILES = 2 * TILES
 
 FLOPS = 2 * BLOCKS * TILES * P * D_MODEL * N_OUT
 
@@ -58,38 +62,49 @@ def tile_fluxjointattention_pa_kernel(
     with (
         tc.tile_pool(name="keep", bufs=1) as keep,
         tc.tile_pool(name="stage", bufs=3) as stage,
-        tc.tile_pool(name="work", bufs=5) as work,
-        tc.tile_pool(name="result", bufs=6) as result,
-        tc.psum_pool(name="prep", bufs=2) as prep,
-        tc.psum_pool(name="coefs", bufs=2) as coefs,
+        tc.tile_pool(name="rowwork", bufs=4) as rowwork,
+        tc.tile_pool(name="colwork", bufs=3) as colwork,
+        tc.tile_pool(name="small", bufs=6) as small,
+        tc.tile_pool(name="result", bufs=4) as result,
         tc.psum_pool(name="sums", bufs=4) as sums,
+        tc.psum_pool(name="turn", bufs=2) as turn,
+        tc.psum_pool(name="stats", bufs=1) as stats,
+        tc.psum_pool(name="coefs", bufs=1) as coefs,
         tc.manual_schedule(),
     ):
         x_sb = keep.tile([P, BLOCKS, TILES, D_MODEL], BF16)
-        x_codes = keep.tile([P, BLOCKS, TILES, PASSES * P], U32, align_bytes=64)
-        x_planes = keep.tile([P, BLOCKS, TILES, PASSES * P], U8, align_bytes=64)
+        x_codes = keep.tile([P, PASSES, NT * P], U32, align_bytes=64)
+        x_planes = keep.tile([P, PASSES, NT * P], U8, align_bytes=64)
         w_words = keep.tile([P, 2, CHUNKS, PASSES, 2 * BANK], U8, align_bytes=64)
         w_planes = [keep.tile([P, PASSES, N_OUT], U8, align_bytes=64, name="w_planes_%d" % s) for s in range(2)]
-        bias_vec = [keep.tile([P, BANK], BF16, name="bias_vec_%d" % s) for s in range(2)]
-        gain_vec = [keep.tile([P, 2 * DH], BF16, name="gain_vec_%d" % s) for s in range(2)]
-        bias_sb = keep.tile([P, 2, CHUNKS, BANK], F32)
-        gains = keep.tile([P, 4, 2, PAIRS], F32)
-        rope_sb = keep.tile([P, BLOCKS * TILES, 4 * PAIRS], BF16)
-        table_v = keep.tile([P, 2, BLOCKS * TILES, DH + PAIRS], F32)
-        table_g = keep.tile([P, 2, BLOCKS * TILES, PAIRS], F32)
+        bias_bc = [keep.tile([P, N_OUT], BF16, name="bias_bc_%d" % s) for s in range(2)]
+        gain_bc = keep.tile([P, 4, DH], BF16)
+        rope_sb = keep.tile([P, NT, 4 * PAIRS], BF16)
+        table_v = keep.tile([P, 2, 2, TILES, DH], F32)
+        table_g = keep.tile([P, 2, 2, TILES, 2, PAIRS], F32)
+        rows_bf = keep.tile([P, P], BF16)
+        cols = keep.tile([P, 32], F32)
+        picked = keep.tile([P, 2, COL_TILES, DH], BF16)
+        tabs = keep.tile([P, 2, 2, COL_TILES * P], F32)
         ident = keep.tile([P, P], F32)
+        swap = keep.tile([P, P], F32)
         ident_bf = keep.tile([P, P], BF16)
         eps = keep.tile([P, 1], F32)
+        ones = keep.tile([P, 2], F32)
+        sum_ps = stats.tile([P, 2 * HEADS * COL_TILES], F32)
 
-        nc.vector.memset(bias_vec[0][:].bitcast(I32), 0)
         nc.vector.memset(w_planes[0][:].rearrange("p g n -> p (g n)").bitcast(I32), 0)
-        nc.vector.memset(gain_vec[0][:].bitcast(I32), 0)
-        nc.vector.memset(bias_vec[1][:].bitcast(I32), 0)
-        nc.vector.memset(gain_vec[1][:].bitcast(I32), 0)
         nc.vector.memset(eps[:], EPS)
+        nc.vector.memset(ones[:], 1.0)
+        nc.vector.memset(rows_bf[:].bitcast(I32), 0)
         nc.vector.memset(w_planes[1][:].rearrange("p g n -> p (g n)").bitcast(I32), 0)
         make_identity(nc, ident[:])
         nc.vector.tensor_copy(out=ident_bf[:], in_=ident[:])
+        pairs_of = "p (j i) -> p j i"
+        for i in range(2):
+            nc.vector.tensor_copy(
+                out=swap[:].rearrange(pairs_of, i=2)[:, :, i], in_=ident[:].rearrange(pairs_of, i=2)[:, :, 1 - i]
+            )
 
         def load_x(blk):
             if blk == 0:
@@ -111,193 +126,245 @@ def tile_fluxjointattention_pa_kernel(
                 in_=words_in[s].bitcast(I32)[:, :, c * width : (c + 1) * width].rearrange("g p n -> p g n"),
             )
 
-        def load_bias(s, queue):
-            queue.dma_start(out=bias_vec[s][0:CHUNKS, :], in_=bias_in[s].rearrange("(c n) -> c n", c=CHUNKS))
+        def load_bias(s, first, last):
+            nc.sync.dma_start(
+                out=bias_bc[s][:, first * BANK : last * BANK],
+                in_=bias_in[s][first * BANK : last * BANK].partition_broadcast(P),
+            )
 
-        def load_rotation(s, queue):
-            first = 0 if s == 0 else 1
-            last = 1 if s == 0 else BLOCKS
+        def load_gains(s):
             for qk in range(2):
-                queue.dma_start(
-                    out=gain_vec[s][0:1, qk * DH : (qk + 1) * DH],
-                    in_=gain_in[2 * s + qk].rearrange("(o n) -> o n", o=1),
-                )
-            queue.dma_start(
+                nc.sync.dma_start(out=gain_bc[:, 2 * s + qk, :], in_=gain_in[2 * s + qk].partition_broadcast(P))
+
+        def load_rope(first, last):
+            nc.sync.dma_start(
                 out=rope_sb[:, first * TILES : last * TILES, :].rearrange("p (k t) f -> p k (t f)", t=TILES),
                 in_=image_rotary_emb.rearrange("a b (k p t) j r c -> p (a b k) (t j r c)", p=P, t=TILES)[
                     :, first:last, :
                 ],
             )
 
+        def load_rows():
+            nc.sync.dma_start(
+                out=rows_bf[0 : 2 * HEADS, :], in_=a_qkv_b[0 : 2 * HEADS * DH].rearrange("(h f) -> h f", f=DH)
+            )
+            for qk in range(2):
+                nc.sync.dma_start(
+                    out=rows_bf[2 * HEADS + qk : 2 * HEADS + qk + 1, :],
+                    in_=gain_in[2 + qk].rearrange("(o n) -> o n", o=1),
+                )
+
         load_x(0)
-        load_bias(0, nc.sync)
-        load_scales(0)
-        load_words(0, CHUNK_ORDER[0])
-        load_words(0, CHUNK_ORDER[1])
-        load_rotation(0, nc.sync)
-        load_words(0, CHUNK_ORDER[2])
-        load_rotation(1, nc.sync)
         load_x(1)
-        for c in CHUNK_ORDER[3:]:
-            load_words(0, c)
-        for blk in range(2, BLOCKS):
-            load_x(blk)
-        load_bias(1, nc.sync)
+        load_x(2)
+        load_scales(0)
+        load_words(0, 0)
+        load_rope(0, BLOCKS)
+        load_words(0, 4)
+        load_bias(0, 0, 1)
+        load_gains(0)
+        load_bias(0, 4, CHUNKS)
+        load_rows()
         load_scales(1)
-        for c in CHUNK_ORDER:
-            load_words(1, c)
+        load_words(1, 0)
+        load_words(0, 2)
+        load_bias(0, 1, 4)
+        load_words(1, 2)
+        load_words(0, 5)
+        load_words(0, 1)
+        load_x(3)
+        load_words(0, 3)
+        load_words(1, 1)
+        load_words(1, 3)
+        load_gains(1)
+        load_bias(1, 0, CHUNKS)
+        load_words(1, 4)
+        load_words(1, 5)
 
         grouped_x = {}
 
         def transpose_tile(blk, t):
             x_pairs = x_sb[:].bitcast(F32)
-            x_t = prep.tile([P, PASSES * 2, P], F32, tag="prep")
+            if blk < BLOCKS - 1:
+                x_t = sums.tile([P, PASSES * 2, P], F32, tag="acc")
+            else:
+                x_t = turn.tile([P, PASSES * 2, P], F32, tag="turn")
             for g in range(PASSES):
                 for u in range(2):
                     nc.tensor.transpose(
                         x_t[:, 2 * g + u, :], x_pairs[:, blk, t, 256 * g + u : 256 * (g + 1) : 2], ident[:]
                     )
             grouped = stage.tile([P, PASSES, P, 2], F32, align_bytes=64)
-            nc.scalar.copy(out=grouped[:], in_=x_t[:].rearrange("p (g u) r -> p g r u", u=2))
+            if t == 0:
+                nc.scalar.copy(out=grouped[:], in_=x_t[:].rearrange("p (g u) r -> p g r u", u=2))
+            else:
+                nc.vector.tensor_copy(out=grouped[:], in_=x_t[:].rearrange("p (g u) r -> p g r u", u=2))
             grouped_x[(blk, t)] = grouped
 
         def quantise_tile(blk, t):
-            nc.vector.quantize_mx(
-                out=x_codes[:, blk, t, :].bitcast(FP8X4),
-                scales=x_planes[:, blk, t, :],
-                in_=grouped_x[(blk, t)][:].rearrange("p g r u -> p (g r u)").bitcast(BF16),
-            )
+            n = blk * TILES + t
+            for g in range(PASSES):
+                nc.vector.quantize_mx(
+                    out=x_codes[:, g, n * P : (n + 1) * P].bitcast(FP8X4),
+                    scales=x_planes[:, g, n * P : (n + 1) * P],
+                    in_=grouped_x[(blk, t)][:, g].rearrange("p r u -> p (r u)").bitcast(BF16),
+                )
 
-        def row_selector(row):
-            return ident_bf[:, row : row + 1].to_broadcast([P, P])
+        def build_row_tables(kb):
+            blk = ROW_BLOCKS[kb]
+            s = 0 if blk == 0 else 1
+            coef = rope_sb[:, blk * TILES : (blk + 1) * TILES, :].rearrange("p n (j c) -> p n c j", c=4)
+            for qk in range(2):
+                gain = gain_bc[:, 2 * s + qk, :].rearrange("p (j i) -> p i j", i=2)
+                nc.vector.tensor_tensor(
+                    out=table_v[:, kb, qk].rearrange("p n (i j) -> p n i j", i=2),
+                    in0=coef[:, :, 0:4:3, :],
+                    in1=gain.unsqueeze(1).to_broadcast([P, TILES, 2, PAIRS]),
+                    op=ALU.mult,
+                )
+                for i in range(2):
+                    nc.gpsimd.tensor_tensor(
+                        out=table_g[:, kb, qk, :, i, :],
+                        in0=coef[:, :, 1 + i, :],
+                        in1=gain[:, 1 - i, :].unsqueeze(1).to_broadcast([P, TILES, PAIRS]),
+                        op=ALU.mult,
+                    )
 
-        def spread_gains(s):
-            spread = prep.tile([P, BANK], F32, tag="prep")
+        coef_ps = {}
+
+        def stage_coefficients(kb):
+            coef = coefs.tile([P, 2, TILES, DH], F32)
             nc.tensor.matmul(
-                spread[:, 0 : 2 * DH],
-                lhsT=row_selector(0),
-                rhs=gain_vec[s][:],
+                coef[:].rearrange("p q t f -> p (q t f)"),
+                lhsT=ident[:],
+                rhs=table_v[:, kb].rearrange("p q t f -> p (q t f)"),
                 start=True,
                 stop=True,
             )
-            nc.scalar.copy(
-                out=gains[:, 2 * s : 2 * (s + 1)],
-                in_=spread[:, 0 : 2 * DH].rearrange("p (v j i) -> p v i j", v=2, i=2),
+            coef_ps[kb] = coef
+
+        def pick_coefficients():
+            first = COL_FIRST * TILES
+            coef = rope_sb[:, first : first + COL_TILES, :].rearrange("p n (j c) -> p n j c", c=4)
+            nc.vector.tensor_copy(
+                out=picked[:, 0].rearrange("p n (j e) -> p n j e", e=2), in_=coef[:, :, :, 0:4:3]
+            )
+            for e in range(2):
+                nc.vector.tensor_copy(
+                    out=picked[:, 1].rearrange("p n (j e) -> p n j e", e=2)[:, :, :, e], in_=coef[:, :, :, 2 - e]
+                )
+
+        def turn_columns():
+            col_ps = turn.tile([P, P], BF16, tag="turn")
+            nc.tensor.transpose(col_ps[:], rows_bf[:], ident_bf[:])
+            nc.vector.tensor_copy(out=cols[:, 0 : 2 * HEADS + 2], in_=col_ps[:, 0 : 2 * HEADS + 2])
+
+        tab_tiles = []
+
+        def turn_tables():
+            tab_ps = turn.tile([P, 2, COL_TILES * P], BF16, tag="turn")
+            for k in range(2):
+                for n in range(COL_TILES):
+                    nc.tensor.transpose(tab_ps[:, k, n * P : (n + 1) * P], picked[:, k, n, :], ident_bf[:])
+            tab_tiles.append(tab_ps)
+            nc.scalar.activation(
+                out=tabs[:, 0].rearrange("p k n -> p (k n)"),
+                in_=tab_ps[:].rearrange("p k n -> p (k n)"),
+                func=ACT.Copy,
+                scale=cols[:, 2 * HEADS : 2 * HEADS + 1],
             )
 
-        def spread_bias(s, c):
-            spread = prep.tile([P, BANK], F32, tag="prep")
-            nc.tensor.matmul(spread[:], lhsT=row_selector(c), rhs=bias_vec[s][:], start=True, stop=True)
-            if c < 4:
-                nc.scalar.copy(
-                    out=bias_sb[:, s, c].rearrange("p (h i j) -> p h i j", h=GROUP, i=2),
-                    in_=spread[:].rearrange("p (h j i) -> p h i j", h=GROUP, i=2),
-                )
-            else:
-                nc.scalar.copy(out=bias_sb[:, s, c], in_=spread[:])
+        def key_tables():
+            tab_ps = tab_tiles[0]
+            nc.vector.tensor_scalar(
+                out=tabs[:, 1].rearrange("p k n -> p (k n)"),
+                in0=tab_ps[:].rearrange("p k n -> p (k n)"),
+                scalar1=cols[:, 2 * HEADS + 1 : 2 * HEADS + 2],
+                scalar2=None,
+                op0=ALU.mult,
+            )
 
-        def build_tables(s):
-            first = 0 if s == 0 else TILES
-            last = TILES if s == 0 else BLOCKS * TILES
-            n = last - first
-            coef = rope_sb[:, first:last, :].rearrange("p n (j c) -> p n c j", c=4)
-            for qk in range(2):
-                gain = gains[:, 2 * s + qk]
-                nc.vector.tensor_tensor(
-                    out=table_v[:, qk, first:last, 0:DH].rearrange("p n (i j) -> p n i j", i=2),
-                    in0=coef[:, :, 0:4:3, :],
-                    in1=gain.unsqueeze(1).to_broadcast([P, n, 2, PAIRS]),
-                    op=ALU.mult,
-                )
-                nc.vector.tensor_tensor(
-                    out=table_v[:, qk, first:last, DH : DH + PAIRS],
-                    in0=coef[:, :, 1, :],
-                    in1=gain[:, 1, :].unsqueeze(1).to_broadcast([P, n, PAIRS]),
-                    op=ALU.mult,
-                )
-                nc.gpsimd.tensor_tensor(
-                    out=table_g[:, qk, first:last, :],
-                    in0=coef[:, :, 2, :],
-                    in1=gain[:, 0, :].unsqueeze(1).to_broadcast([P, n, PAIRS]),
-                    op=ALU.mult,
-                )
-
-        steps = [(blk, m, part) for blk in range(BLOCKS) for m in range(2) for part in (0, 2, 1)]
         live = {}
-        coef_ps = {}
-        sums_ps = {}
 
-        def stage_project(n):
-            blk, m, part = steps[n]
-            s = 0 if blk == 0 else 1
-            c = 2 * part + m
-            for t in range(TILES):
-                acc = sums.tile([P, BANK], F32)
+        def project(n):
+            kind = steps[n][0]
+            st = live.setdefault(n, {})
+            if kind == "col":
+                part, h = steps[n][1:]
+                c = 2 * part + h // GROUP
+                hl = h % GROUP
+                first = COL_FIRST * TILES * P
+                acc = sums.tile([P, BANK], F32, tag="acc")
                 for g in range(PASSES):
                     nc.tensor.matmul_mx(
                         out=acc[:],
-                        lhsT=x_codes[:, blk, t, g * P : (g + 1) * P].bitcast(FP8X4),
-                        lhsT_scale=x_planes[:, blk, t, g * P : (g + 1) * P],
+                        lhsT=w_words[:, 1, c, g, hl * 2 * DH : (hl + 1) * 2 * DH].bitcast(FP4X4),
+                        lhsT_scale=w_planes[1][:, g, c * BANK + hl * DH : c * BANK + (hl + 1) * DH],
+                        rhs=x_codes[:, g, first : first + BANK].bitcast(FP8X4),
+                        rhs_scale=x_planes[:, g, first : first + BANK],
+                        start=(g == 0),
+                        stop=(g == PASSES - 1),
+                    )
+                st["acc"] = acc
+                return
+            blk, part, m = steps[n][1:]
+            s = 0 if blk == 0 else 1
+            c = 2 * part + m
+            for t in range(TILES):
+                k = blk * TILES + t
+                acc = sums.tile([P, BANK], F32, tag="acc")
+                for g in range(PASSES):
+                    nc.tensor.matmul_mx(
+                        out=acc[:],
+                        lhsT=x_codes[:, g, k * P : (k + 1) * P].bitcast(FP8X4),
+                        lhsT_scale=x_planes[:, g, k * P : (k + 1) * P],
                         rhs=w_words[:, s, c, g, :].bitcast(FP4X4),
                         rhs_scale=w_planes[s][:, g, c * BANK : (c + 1) * BANK],
                         start=(g == 0),
                         stop=(g == PASSES - 1),
                     )
-                sums_ps[(n, t)] = acc
+                st[("acc", t)] = acc
 
-        def store(n, out_sb):
-            blk, m, part = steps[n]
+        def store_rows(n, out_sb):
+            blk, part, m = steps[n][1:]
             rows = outs[part][0, m * GROUP : (m + 1) * GROUP, blk * TILES * P : (blk + 1) * TILES * P, :]
             nc.sync.dma_start(
                 out=rows.rearrange("h (p t) d -> p h (t d)", t=TILES),
                 in_=out_sb[:].rearrange("p h t d -> p h (t d)"),
             )
 
-        def stage_bias(n):
-            blk, m, part = steps[n]
+        def row_bias(n):
+            blk, part, m = steps[n][1:]
             s = 0 if blk == 0 else 1
             c = 2 * part + m
+            st = live[n]
+            bias = bias_bc[s][:, c * BANK : (c + 1) * BANK]
             if part == 2:
-                out_sb = result.tile([P, GROUP, TILES, DH], F32)
+                out_sb = result.tile([P, GROUP, TILES, DH], F32, tag="out_sb")
                 for t in range(TILES):
                     nc.vector.tensor_tensor(
                         out=out_sb[:, :, t, :],
-                        in0=sums_ps[(n, t)][:].rearrange("p (h d) -> p h d", h=GROUP),
-                        in1=bias_sb[:, s, c].rearrange("p (h d) -> p h d", h=GROUP),
+                        in0=st[("acc", t)][:].rearrange("p (h d) -> p h d", h=GROUP),
+                        in1=bias.rearrange("p (h d) -> p h d", h=GROUP),
                         op=ALU.add,
                     )
-                store(n, out_sb)
+                store_rows(n, out_sb)
             else:
-                u = work.tile([P, TILES, GROUP, 2, PAIRS], F32)
+                u = rowwork.tile([P, TILES, GROUP, 2, PAIRS], F32)
                 for t in range(TILES):
                     nc.vector.tensor_tensor(
                         out=u[:, t],
-                        in0=sums_ps[(n, t)][:].rearrange("p (h j i) -> p h i j", h=GROUP, i=2),
-                        in1=bias_sb[:, s, c].rearrange("p (h i j) -> p h i j", h=GROUP, i=2),
+                        in0=st[("acc", t)][:].rearrange("p (h j i) -> p h i j", h=GROUP, i=2),
+                        in1=bias.rearrange("p (h j i) -> p h i j", h=GROUP, i=2),
                         op=ALU.add,
                     )
-                live[n] = {"u": u}
+                st["u"] = u
 
-        def stage_coefficients(n):
-            blk, m, part = steps[n]
-            coef = coefs.tile([P, TILES, DH + PAIRS], F32)
-            nc.tensor.matmul(
-                coef[:].rearrange("p t f -> p (t f)"),
-                lhsT=ident[:],
-                rhs=table_v[:, part, blk * TILES : (blk + 1) * TILES, :].rearrange("p t f -> p (t f)"),
-                start=True,
-                stop=True,
-            )
-            coef_ps[(blk, part)] = coef
-
-        def stage_products(n):
-            blk, m, part = steps[n]
-            u = live[n]["u"]
-            coef = coef_ps[(blk, part)]
-            squares = work.tile([P, TILES, GROUP, DH], BF16)
-            sum_sq = work.tile([P, TILES * GROUP], F32)
-            straight = work.tile([P, TILES, GROUP, 2, PAIRS], F32)
-            crossed = work.tile([P, TILES, GROUP, 2, PAIRS], F32)
+        def row_squares(n):
+            st = live[n]
+            u = st["u"]
+            squares = rowwork.tile([P, TILES, GROUP, DH], BF16)
+            sum_sq = small.tile([P, TILES * GROUP], F32)
             for t in range(TILES):
                 for h in range(GROUP):
                     nc.scalar.activation(
@@ -306,51 +373,61 @@ def tile_fluxjointattention_pa_kernel(
                         func=ACT.Square,
                         accum_out=sum_sq[:, t * GROUP + h : t * GROUP + h + 1],
                     )
+            rms = small.tile([P, TILES * GROUP], F32)
+            nc.scalar.activation(out=rms[:], in_=sum_sq[:], func=ACT.Sqrt, bias=eps[:], scale=1.0 / DH)
+            st["rms"] = rms
+
+        def row_straight(n):
+            blk, part, m = steps[n][1:]
+            kb = ROW_BLOCKS.index(blk)
+            st = live[n]
+            u = st["u"]
+            straight = rowwork.tile([P, TILES, GROUP, 2, PAIRS], F32)
             nc.vector.tensor_tensor(
                 out=straight[:].rearrange("p t h i j -> p t h (i j)"),
                 in0=u[:].rearrange("p t h i j -> p t h (i j)"),
-                in1=coef[:, :, 0:DH].unsqueeze(2).to_broadcast([P, TILES, GROUP, DH]),
+                in1=coef_ps[kb][:, part].unsqueeze(2).to_broadcast([P, TILES, GROUP, DH]),
                 op=ALU.mult,
             )
-            nc.vector.tensor_tensor(
-                out=crossed[:, :, :, 0, :],
-                in0=u[:, :, :, 1, :],
-                in1=coef[:, :, DH : DH + PAIRS].unsqueeze(2).to_broadcast([P, TILES, GROUP, PAIRS]),
-                op=ALU.mult,
-            )
-            nc.gpsimd.tensor_tensor(
-                out=crossed[:, :, :, 1, :],
-                in0=u[:, :, :, 0, :],
-                in1=table_g[:, part, blk * TILES : (blk + 1) * TILES, :]
-                .unsqueeze(2)
-                .to_broadcast([P, TILES, GROUP, PAIRS]),
-                op=ALU.mult,
-            )
-            live[n]["sum_sq"] = sum_sq
-            live[n]["straight"] = straight
-            live[n]["crossed"] = crossed
+            st["straight"] = straight
 
-        def stage_root(n):
-            rms = work.tile([P, TILES * GROUP], F32)
-            nc.scalar.activation(out=rms[:], in_=live[n]["sum_sq"][:], func=ACT.Sqrt, bias=eps[:], scale=1.0 / DH)
-            live[n]["rms"] = rms
+        def row_crossed(n):
+            blk, part, m = steps[n][1:]
+            kb = ROW_BLOCKS.index(blk)
+            st = live[n]
+            u = st["u"]
+            crossed = rowwork.tile([P, TILES, GROUP, 2, PAIRS], F32)
+            for i in range(2):
+                nc.gpsimd.tensor_tensor(
+                    out=crossed[:, :, :, i, :],
+                    in0=u[:, :, :, 1 - i, :],
+                    in1=table_g[:, kb, part, :, i, :].unsqueeze(2).to_broadcast([P, TILES, GROUP, PAIRS]),
+                    op=ALU.mult,
+                )
+            st["crossed"] = crossed
 
-        def stage_add(n):
-            inv_rms = work.tile([P, TILES * GROUP], F32)
-            nc.vector.reciprocal(out=inv_rms[:], in_=live[n]["rms"][:])
-            straight = live[n]["straight"]
+        def row_add(n):
+            st = live[n]
+            straight = st["straight"]
             nc.gpsimd.tensor_tensor(
                 out=straight[:].rearrange("p t h i j -> p (t h i j)"),
                 in0=straight[:].rearrange("p t h i j -> p (t h i j)"),
-                in1=live[n]["crossed"][:].rearrange("p t h i j -> p (t h i j)"),
+                in1=st["crossed"][:].rearrange("p t h i j -> p (t h i j)"),
                 op=ALU.add,
             )
-            live[n]["inv_rms"] = inv_rms
 
-        def stage_scale(n):
-            rotated = live[n]["straight"]
-            inv_rms = live[n]["inv_rms"]
-            out_sb = result.tile([P, GROUP, TILES, DH], F32)
+        def reciprocal(n):
+            st = live[n]
+            inv_rms = small.tile([P, TILES * GROUP], F32)
+            width = COL_TILES if steps[n][0] == "col" else TILES * GROUP
+            nc.vector.reciprocal(out=inv_rms[:, 0:width], in_=st["rms"][:])
+            st["inv_rms"] = inv_rms
+
+        def row_scale(n):
+            st = live[n]
+            rotated = st["straight"]
+            inv_rms = st["inv_rms"]
+            out_sb = result.tile([P, GROUP, TILES, DH], F32, tag="out_sb")
             for t in range(TILES):
                 for h in range(GROUP):
                     nc.scalar.activation(
@@ -359,51 +436,156 @@ def tile_fluxjointattention_pa_kernel(
                         func=ACT.Copy,
                         scale=inv_rms[:, t * GROUP + h : t * GROUP + h + 1],
                     )
-            store(n, out_sb)
+            store_rows(n, out_sb)
 
-        def is_rotated(n):
-            return 0 <= n < len(steps) and steps[n][2] < 2
+        def col_square(n):
+            part, h = steps[n][1:]
+            st = live[n]
+            bias = cols[:, part * HEADS + h : part * HEADS + h + 1]
+            sq = colwork.tile([P, BANK], F32)
+            nc.scalar.activation(out=sq[:], in_=st["acc"][:], func=ACT.Square, bias=bias, scale=1.0)
+            st["sq"] = sq
 
-        def spread_bias_of(n):
-            if n < 2 * CHUNKS:
-                blk, m, part = steps[n]
-                spread_bias(blk, 2 * part + m)
+        def col_products(n):
+            part, h = steps[n][1:]
+            st = live[n]
+            bias = cols[:, part * HEADS + h : part * HEADS + h + 1]
+            for k, name in enumerate(("straight", "crossed")):
+                prod = colwork.tile([P, BANK], F32, tag=name)
+                nc.vector.scalar_tensor_tensor(
+                    out=prod[:], in0=st["acc"][:], scalar=bias, in1=tabs[:, part, k, :], op0=ALU.add, op1=ALU.mult
+                )
+                st[name] = prod
 
-        def prepare(i):
-            spread_bias_of(i + 2)
-            blk, t = divmod(i + 5, 2 * 3)
-            if 1 <= blk < BLOCKS and t < TILES:
+        def col_sums(n):
+            st = live[n]
+            first = (n - n_row - n_val) * COL_TILES
+            for k in range(COL_TILES):
+                nc.tensor.matmul(
+                    sum_ps[:, first + k : first + k + 1],
+                    lhsT=st["sq"][:, k * P : (k + 1) * P],
+                    rhs=ones[:, 0:1],
+                    start=True,
+                    stop=True,
+                )
+
+        def col_turn(n):
+            st = live[n]
+            rot = turn.tile([P, COL_TILES, DH], F32, tag="turn")
+            for k in range(COL_TILES):
+                nc.tensor.matmul(
+                    rot[:, k, :], lhsT=st["straight"][:, k * P : (k + 1) * P], rhs=ident[:],
+                    is_transpose=True, start=True, stop=False,
+                )
+                nc.tensor.matmul(
+                    rot[:, k, :], lhsT=st["crossed"][:, k * P : (k + 1) * P], rhs=swap[:],
+                    is_transpose=True, start=False, stop=True,
+                )
+            st["rot"] = rot
+
+        def col_root(n):
+            st = live[n]
+            rms = small.tile([P, COL_TILES], F32, tag="col_rms")
+            first = (n - n_row - n_val) * COL_TILES
+            nc.scalar.activation(
+                out=rms[:], in_=sum_ps[:, first : first + COL_TILES], func=ACT.Sqrt, bias=eps[:], scale=1.0 / DH
+            )
+            st["rms"] = rms
+
+        def col_scale(n):
+            part, h = steps[n][1:]
+            st = live[n]
+            out_sb = result.tile([P, COL_TILES, DH], F32, tag="col_out")
+            for k in range(COL_TILES):
+                nc.scalar.activation(
+                    out=out_sb[:, k, :], in_=st["rot"][:, k, :], func=ACT.Copy, scale=st["inv_rms"][:, k : k + 1]
+                )
+            first = COL_FIRST * TILES * P
+            rows = outs[part][0, h, first : first + COL_TILES * P, :]
+            nc.sync.dma_start(
+                out=rows.rearrange("(b p t) d -> p b (t d)", p=P, t=TILES),
+                in_=out_sb[:].rearrange("p (b t) d -> p b (t d)", t=TILES),
+            )
+
+        row_steps = [("row", blk, part, m) for blk in ROW_BLOCKS for m in range(2) for part in range(2)]
+        val_steps = [("row", blk, 2, m) for blk in range(BLOCKS) for m in range(2)]
+        col_steps = [("col", part, GROUP * m + h) for m in range(2) for part in range(2) for h in range(GROUP)]
+        steps = row_steps + val_steps + col_steps
+        n_row, n_val = len(row_steps), len(val_steps)
+
+        def rows_of(r):
+            return r if 0 <= r < n_row else None
+
+        def vals_of(r):
+            return n_row + r if 0 <= r < n_val else None
+
+        def cols_of(r, k):
+            return n_row + n_val + 2 * (r - 1) + k if 1 <= r <= len(col_steps) // 2 else None
+
+        def do(fn, n):
+            if n is not None:
+                fn(n)
+
+        def row_gpsimd(n):
+            row_crossed(n)
+            row_add(n)
+
+        def x_tile(blk, t):
+            transpose_tile(blk, t)
+
+        for blk in range(BLOCKS - 1):
+            for t in range(TILES):
                 transpose_tile(blk, t)
-            blk, t = divmod(i + 4, 2 * 3)
-            if 1 <= blk < BLOCKS and t < TILES:
+            for t in range(TILES):
                 quantise_tile(blk, t)
-            if i == 0:
-                build_tables(0)
-                spread_gains(1)
-            if i == 1:
-                build_tables(1)
 
-        for t in range(TILES):
-            transpose_tile(0, t)
-        for t in range(TILES):
-            quantise_tile(0, t)
-        spread_bias_of(0)
-        spread_bias_of(1)
-        stage_project(0)
-        spread_gains(0)
-        for i in range(len(steps) + 3):
-            if i + 1 < len(steps):
-                stage_project(i + 1)
-            if is_rotated(i - 1) and steps[i - 1][1] == 0:
-                stage_coefficients(i - 1)
-            if i < len(steps):
-                stage_bias(i)
-            if is_rotated(i - 2):
-                stage_add(i - 2)
-            if is_rotated(i - 1):
-                stage_products(i - 1)
-            if is_rotated(i - 3):
-                stage_scale(i - 3)
-            if is_rotated(i - 1):
-                stage_root(i - 1)
-            prepare(i)
+        prep = {
+            (0, 1): lambda: (build_row_tables(0), stage_coefficients(0)),
+            (0, 2): lambda: pick_coefficients(),
+            (0, 3): lambda: (turn_columns(), turn_tables()),
+            (1, 1): lambda: key_tables(),
+            (1, 2): lambda: transpose_tile(3, 0),
+            (2, 0): lambda: quantise_tile(3, 0),
+            (2, 2): lambda: transpose_tile(3, 1),
+            (3, 0): lambda: (quantise_tile(3, 1), build_row_tables(1)),
+            (4, 0): lambda: stage_coefficients(1),
+        }
+
+        def hook(r, k):
+            if (r, k) in prep:
+                prep[(r, k)]()
+
+        for r in range(len(col_steps) // 2 + 3):
+            t1, t2, t2_old = cols_of(r, 0), cols_of(r, 1), cols_of(r - 1, 1)
+            do(project, t1)
+            do(row_bias, vals_of(r - 1))
+            do(col_root, t2_old)
+            do(col_turn, t2_old)
+            do(col_square, t1)
+            do(reciprocal, t2_old)
+            do(reciprocal, rows_of(r - 1))
+            hook(r, 0)
+            do(project, rows_of(r))
+            if r == 0:
+                do(project, vals_of(r))
+            do(col_products, t1)
+            do(col_scale, t2_old)
+            do(row_scale, rows_of(r - 1))
+            do(col_sums, t1)
+            do(project, t2)
+            hook(r, 1)
+            do(row_bias, rows_of(r))
+            do(col_root, t1)
+            do(col_turn, t1)
+            do(col_square, t2)
+            do(reciprocal, t1)
+            hook(r, 2)
+            do(row_straight, rows_of(r))
+            do(row_gpsimd, rows_of(r))
+            if r > 0:
+                do(project, vals_of(r))
+            do(row_squares, rows_of(r))
+            do(col_products, t2)
+            do(col_sums, t2)
+            do(col_scale, t1)
+            hook(r, 3)

@@ -29,6 +29,7 @@ EPS = 1e-6
 ROW_BLOCKS = (0, 3)
 COL_FIRST = 1
 COL_TILES = 2 * TILES
+VECTOR_SCALES = 0
 
 FLOPS = 2 * BLOCKS * TILES * P * D_MODEL * N_OUT
 
@@ -67,8 +68,7 @@ def tile_fluxjointattention_pa_kernel(
         tc.tile_pool(name="small", bufs=6) as small,
         tc.tile_pool(name="result", bufs=4) as result,
         tc.psum_pool(name="sums", bufs=4) as sums,
-        tc.psum_pool(name="turn", bufs=2) as turn,
-        tc.psum_pool(name="stats", bufs=1) as stats,
+        tc.psum_pool(name="turn", bufs=3) as turn,
         tc.psum_pool(name="coefs", bufs=1) as coefs,
         tc.manual_schedule(),
     ):
@@ -91,7 +91,6 @@ def tile_fluxjointattention_pa_kernel(
         ident_bf = keep.tile([P, P], BF16)
         eps = keep.tile([P, 1], F32)
         ones = keep.tile([P, 2], F32)
-        sum_ps = stats.tile([P, 2 * HEADS * COL_TILES], F32)
 
         nc.vector.memset(w_planes[0][:].rearrange("p g n -> p (g n)").bitcast(I32), 0)
         nc.vector.memset(eps[:], EPS)
@@ -160,11 +159,11 @@ def tile_fluxjointattention_pa_kernel(
         load_scales(0)
         load_words(0, 0)
         load_rope(0, BLOCKS)
-        load_words(0, 4)
+        load_rows()
         load_bias(0, 0, 1)
         load_gains(0)
+        load_words(0, 4)
         load_bias(0, 4, CHUNKS)
-        load_rows()
         load_scales(1)
         load_words(1, 0)
         load_words(0, 2)
@@ -194,20 +193,22 @@ def tile_fluxjointattention_pa_kernel(
                     nc.tensor.transpose(
                         x_t[:, 2 * g + u, :], x_pairs[:, blk, t, 256 * g + u : 256 * (g + 1) : 2], ident[:]
                     )
-            grouped = stage.tile([P, PASSES, P, 2], F32, align_bytes=64)
             if t == 0:
-                nc.scalar.copy(out=grouped[:], in_=x_t[:].rearrange("p (g u) r -> p g r u", u=2))
+                grouped = stage.tile([P, PASSES, TILES, P, 2], F32, align_bytes=64)
+                grouped_x[blk] = grouped
+                nc.scalar.copy(out=grouped_x[blk][:, :, t], in_=x_t[:].rearrange("p (g u) r -> p g r u", u=2))
             else:
-                nc.vector.tensor_copy(out=grouped[:], in_=x_t[:].rearrange("p (g u) r -> p g r u", u=2))
-            grouped_x[(blk, t)] = grouped
+                nc.scalar.copy(out=grouped_x[blk][:, :, t], in_=x_t[:].rearrange("p (g u) r -> p g r u", u=2))
 
         def quantise_tile(blk, t):
-            n = blk * TILES + t
+            if t == 0:
+                return
+            n = blk * TILES
             for g in range(PASSES):
                 nc.vector.quantize_mx(
-                    out=x_codes[:, g, n * P : (n + 1) * P].bitcast(FP8X4),
-                    scales=x_planes[:, g, n * P : (n + 1) * P],
-                    in_=grouped_x[(blk, t)][:, g].rearrange("p r u -> p (r u)").bitcast(BF16),
+                    out=x_codes[:, g, n * P : (n + TILES) * P].bitcast(FP8X4),
+                    scales=x_planes[:, g, n * P : (n + TILES) * P],
+                    in_=grouped_x[blk][:, g].rearrange("p t r u -> p (t r u)").bitcast(BF16),
                 )
 
         def build_row_tables(kb):
@@ -246,18 +247,18 @@ def tile_fluxjointattention_pa_kernel(
         def pick_coefficients():
             first = COL_FIRST * TILES
             coef = rope_sb[:, first : first + COL_TILES, :].rearrange("p n (j c) -> p n j c", c=4)
-            nc.vector.tensor_copy(
+            nc.gpsimd.tensor_copy(
                 out=picked[:, 0].rearrange("p n (j e) -> p n j e", e=2), in_=coef[:, :, :, 0:4:3]
             )
             for e in range(2):
-                nc.vector.tensor_copy(
+                nc.gpsimd.tensor_copy(
                     out=picked[:, 1].rearrange("p n (j e) -> p n j e", e=2)[:, :, :, e], in_=coef[:, :, :, 2 - e]
                 )
 
         def turn_columns():
             col_ps = turn.tile([P, P], BF16, tag="turn")
             nc.tensor.transpose(col_ps[:], rows_bf[:], ident_bf[:])
-            nc.vector.tensor_copy(out=cols[:, 0 : 2 * HEADS + 2], in_=col_ps[:, 0 : 2 * HEADS + 2])
+            nc.scalar.copy(out=cols[:, 0 : 2 * HEADS + 2], in_=col_ps[:, 0 : 2 * HEADS + 2])
 
         tab_tiles = []
 
@@ -276,12 +277,11 @@ def tile_fluxjointattention_pa_kernel(
 
         def key_tables():
             tab_ps = tab_tiles[0]
-            nc.vector.tensor_scalar(
+            nc.scalar.activation(
                 out=tabs[:, 1].rearrange("p k n -> p (k n)"),
-                in0=tab_ps[:].rearrange("p k n -> p (k n)"),
-                scalar1=cols[:, 2 * HEADS + 1 : 2 * HEADS + 2],
-                scalar2=None,
-                op0=ALU.mult,
+                in_=tab_ps[:].rearrange("p k n -> p (k n)"),
+                func=ACT.Copy,
+                scale=cols[:, 2 * HEADS + 1 : 2 * HEADS + 2],
             )
 
         live = {}
@@ -373,9 +373,11 @@ def tile_fluxjointattention_pa_kernel(
                         func=ACT.Square,
                         accum_out=sum_sq[:, t * GROUP + h : t * GROUP + h + 1],
                     )
-            rms = small.tile([P, TILES * GROUP], F32)
-            nc.scalar.activation(out=rms[:], in_=sum_sq[:], func=ACT.Sqrt, bias=eps[:], scale=1.0 / DH)
-            st["rms"] = rms
+            inv_rms = small.tile([P, TILES * GROUP], F32)
+            nc.scalar.activation(
+                out=inv_rms[:], in_=sum_sq[:], func=ACT.Abs_reciprocal_sqrt, bias=eps[:], scale=1.0 / DH
+            )
+            st["inv_rms"] = inv_rms
 
         def row_straight(n):
             blk, part, m = steps[n][1:]
@@ -443,7 +445,7 @@ def tile_fluxjointattention_pa_kernel(
             st = live[n]
             bias = cols[:, part * HEADS + h : part * HEADS + h + 1]
             sq = colwork.tile([P, BANK], F32)
-            nc.scalar.activation(out=sq[:], in_=st["acc"][:], func=ACT.Square, bias=bias, scale=1.0)
+            nc.scalar.activation(out=sq[:], in_=st["acc"][:], func=ACT.Identity, bias=bias, scale=1.0)
             st["sq"] = sq
 
         def col_products(n):
@@ -459,15 +461,10 @@ def tile_fluxjointattention_pa_kernel(
 
         def col_sums(n):
             st = live[n]
-            first = (n - n_row - n_val) * COL_TILES
+            plain = turn.tile([P, COL_TILES, DH], F32, tag="turn")
             for k in range(COL_TILES):
-                nc.tensor.matmul(
-                    sum_ps[:, first + k : first + k + 1],
-                    lhsT=st["sq"][:, k * P : (k + 1) * P],
-                    rhs=ones[:, 0:1],
-                    start=True,
-                    stop=True,
-                )
+                nc.tensor.transpose(plain[:, k, :], st["sq"][:, k * P : (k + 1) * P], ident[:])
+            st["plain"] = plain
 
         def col_turn(n):
             st = live[n]
@@ -485,21 +482,34 @@ def tile_fluxjointattention_pa_kernel(
 
         def col_root(n):
             st = live[n]
-            rms = small.tile([P, COL_TILES], F32, tag="col_rms")
-            first = (n - n_row - n_val) * COL_TILES
+            junk = colwork.tile([P, COL_TILES, DH], BF16)
+            sum_sq = small.tile([P, COL_TILES], F32, tag="col_sum")
+            for k in range(COL_TILES):
+                nc.scalar.activation(
+                    out=junk[:, k, :], in_=st["plain"][:, k, :], func=ACT.Square, accum_out=sum_sq[:, k : k + 1]
+                )
+            inv_rms = small.tile([P, COL_TILES], F32, tag="col_inv")
             nc.scalar.activation(
-                out=rms[:], in_=sum_ps[:, first : first + COL_TILES], func=ACT.Sqrt, bias=eps[:], scale=1.0 / DH
+                out=inv_rms[:], in_=sum_sq[:], func=ACT.Abs_reciprocal_sqrt, bias=eps[:], scale=1.0 / DH
             )
-            st["rms"] = rms
+            st["inv_rms"] = inv_rms
 
         def col_scale(n):
             part, h = steps[n][1:]
             st = live[n]
             out_sb = result.tile([P, COL_TILES, DH], F32, tag="col_out")
-            for k in range(COL_TILES):
-                nc.scalar.activation(
-                    out=out_sb[:, k, :], in_=st["rot"][:, k, :], func=ACT.Copy, scale=st["inv_rms"][:, k : k + 1]
+            if n % 2 == VECTOR_SCALES:
+                nc.vector.tensor_tensor(
+                    out=out_sb[:],
+                    in0=st["rot"][:],
+                    in1=st["inv_rms"][:].unsqueeze(2).to_broadcast([P, COL_TILES, DH]),
+                    op=ALU.mult,
                 )
+            else:
+                for k in range(COL_TILES):
+                    nc.scalar.activation(
+                        out=out_sb[:, k, :], in_=st["rot"][:, k, :], func=ACT.Copy, scale=st["inv_rms"][:, k : k + 1]
+                    )
             first = COL_FIRST * TILES * P
             rows = outs[part][0, h, first : first + COL_TILES * P, :]
             nc.sync.dma_start(
@@ -513,15 +523,6 @@ def tile_fluxjointattention_pa_kernel(
         steps = row_steps + val_steps + col_steps
         n_row, n_val = len(row_steps), len(val_steps)
 
-        def rows_of(r):
-            return r if 0 <= r < n_row else None
-
-        def vals_of(r):
-            return n_row + r if 0 <= r < n_val else None
-
-        def cols_of(r, k):
-            return n_row + n_val + 2 * (r - 1) + k if 1 <= r <= len(col_steps) // 2 else None
-
         def do(fn, n):
             if n is not None:
                 fn(n)
@@ -530,8 +531,21 @@ def tile_fluxjointattention_pa_kernel(
             row_crossed(n)
             row_add(n)
 
-        def x_tile(blk, t):
-            transpose_tile(blk, t)
+        fillers = []
+        for k in range(n_row):
+            fillers += [k, n_row + k]
+        LEAD = 2
+        SCALE_LAG = 3
+        n_slots = len(col_steps) + LEAD + 3
+
+        def filler(k):
+            return fillers[k] if 0 <= k < len(fillers) else None
+
+        def col(k):
+            return n_row + n_val + k - LEAD if 0 <= k - LEAD < len(col_steps) else None
+
+        def is_row(n):
+            return n is not None and n < n_row
 
         for blk in range(BLOCKS - 1):
             for t in range(TILES):
@@ -540,52 +554,37 @@ def tile_fluxjointattention_pa_kernel(
                 quantise_tile(blk, t)
 
         prep = {
+            (0, 0): lambda: (pick_coefficients(), turn_columns()),
             (0, 1): lambda: (build_row_tables(0), stage_coefficients(0)),
-            (0, 2): lambda: pick_coefficients(),
-            (0, 3): lambda: (turn_columns(), turn_tables()),
-            (1, 1): lambda: key_tables(),
-            (1, 2): lambda: transpose_tile(3, 0),
-            (2, 0): lambda: quantise_tile(3, 0),
-            (2, 2): lambda: transpose_tile(3, 1),
-            (3, 0): lambda: (quantise_tile(3, 1), build_row_tables(1)),
-            (4, 0): lambda: stage_coefficients(1),
+            (0, 2): lambda: turn_tables(),
+            (3, 1): lambda: key_tables(),
+            (3, 2): lambda: transpose_tile(3, 0),
+            (4, 2): lambda: transpose_tile(3, 1),
+            (5, 0): lambda: (quantise_tile(3, 1), build_row_tables(1)),
+            (7, 1): lambda: stage_coefficients(1),
         }
 
         def hook(r, k):
             if (r, k) in prep:
                 prep[(r, k)]()
 
-        for r in range(len(col_steps) // 2 + 3):
-            t1, t2, t2_old = cols_of(r, 0), cols_of(r, 1), cols_of(r - 1, 1)
-            do(project, t1)
-            do(row_bias, vals_of(r - 1))
-            do(col_root, t2_old)
-            do(col_turn, t2_old)
-            do(col_square, t1)
-            do(reciprocal, t2_old)
-            do(reciprocal, rows_of(r - 1))
-            hook(r, 0)
-            do(project, rows_of(r))
-            if r == 0:
-                do(project, vals_of(r))
-            do(col_products, t1)
-            do(col_scale, t2_old)
-            do(row_scale, rows_of(r - 1))
-            do(col_sums, t1)
-            do(project, t2)
-            hook(r, 1)
-            do(row_bias, rows_of(r))
-            do(col_root, t1)
-            do(col_turn, t1)
-            do(col_square, t2)
-            do(reciprocal, t1)
-            hook(r, 2)
-            do(row_straight, rows_of(r))
-            do(row_gpsimd, rows_of(r))
-            if r > 0:
-                do(project, vals_of(r))
-            do(row_squares, rows_of(r))
-            do(col_products, t2)
-            do(col_sums, t2)
-            do(col_scale, t1)
-            hook(r, 3)
+        project(fillers[0])
+        for k in range(n_slots):
+            do(project, col(k))
+            do(row_bias, filler(k))
+            hook(k, 0)
+            do(col_sums, col(k - 1))
+            do(col_square, col(k))
+            do(col_turn, col(k - 2))
+            do(col_root, col(k - 1))
+            do(col_products, col(k))
+            do(project, filler(k + 1))
+            hook(k, 1)
+            do(col_scale, col(k - 2))
+            if is_row(filler(k)):
+                row_straight(filler(k))
+                row_gpsimd(filler(k))
+                row_squares(filler(k))
+            if is_row(filler(k - SCALE_LAG)):
+                row_scale(filler(k - SCALE_LAG))
+            hook(k, 2)

@@ -29,7 +29,8 @@ EPS = 1e-6
 ROW_BLOCKS = (0, 3)
 COL_FIRST = 1
 COL_TILES = 2 * TILES
-VECTOR_SCALES = 0
+VECTOR_SCALES = (0, 1, 2, 3)
+GPSIMD_CROSSES = (1, 3)
 
 FLOPS = 2 * BLOCKS * TILES * P * D_MODEL * N_OUT
 
@@ -454,9 +455,12 @@ def tile_fluxjointattention_pa_kernel(
             bias = cols[:, part * HEADS + h : part * HEADS + h + 1]
             for k, name in enumerate(("straight", "crossed")):
                 prod = colwork.tile([P, BANK], F32, tag=name)
-                nc.vector.scalar_tensor_tensor(
-                    out=prod[:], in0=st["acc"][:], scalar=bias, in1=tabs[:, part, k, :], op0=ALU.add, op1=ALU.mult
-                )
+                if k == 1 and n % 4 in GPSIMD_CROSSES:
+                    nc.gpsimd.tensor_tensor(out=prod[:], in0=st["sq"][:], in1=tabs[:, part, k, :], op=ALU.mult)
+                else:
+                    nc.vector.scalar_tensor_tensor(
+                        out=prod[:], in0=st["acc"][:], scalar=bias, in1=tabs[:, part, k, :], op0=ALU.add, op1=ALU.mult
+                    )
                 st[name] = prod
 
         def col_sums(n):
@@ -498,7 +502,7 @@ def tile_fluxjointattention_pa_kernel(
             part, h = steps[n][1:]
             st = live[n]
             out_sb = result.tile([P, COL_TILES, DH], F32, tag="col_out")
-            if n % 2 == VECTOR_SCALES:
+            if n % 4 in VECTOR_SCALES:
                 nc.vector.tensor_tensor(
                     out=out_sb[:],
                     in0=st["rot"][:],

@@ -24,13 +24,12 @@ N_OUT = 3 * D_MODEL
 CHUNKS = N_OUT // BANK
 TILES = 2
 BLOCKS = 4
-NT = BLOCKS * TILES
+ALL_TILES = BLOCKS * TILES
 EPS = 1e-6
 ROW_BLOCKS = (0, 3)
 COL_FIRST = 1
 COL_TILES = 2 * TILES
-VECTOR_SCALES = (0, 1, 2, 3)
-GPSIMD_CROSSES = (1, 3)
+COL_TOKEN = COL_FIRST * TILES * P
 
 FLOPS = 2 * BLOCKS * TILES * P * D_MODEL * N_OUT
 
@@ -74,29 +73,27 @@ def tile_fluxjointattention_pa_kernel(
         tc.manual_schedule(),
     ):
         x_sb = keep.tile([P, BLOCKS, TILES, D_MODEL], BF16)
-        x_codes = keep.tile([P, PASSES, NT * P], U32, align_bytes=64)
-        x_planes = keep.tile([P, PASSES, NT * P], U8, align_bytes=64)
+        x_codes = keep.tile([P, PASSES, ALL_TILES * P], U32, align_bytes=64)
+        x_planes = keep.tile([P, PASSES, ALL_TILES * P], U8, align_bytes=64)
         w_words = keep.tile([P, 2, CHUNKS, PASSES, 2 * BANK], U8, align_bytes=64)
         w_planes = [keep.tile([P, PASSES, N_OUT], U8, align_bytes=64, name="w_planes_%d" % s) for s in range(2)]
-        bias_bc = [keep.tile([P, N_OUT], BF16, name="bias_bc_%d" % s) for s in range(2)]
-        gain_bc = keep.tile([P, 4, DH], BF16)
-        rope_sb = keep.tile([P, NT, 4 * PAIRS], BF16)
-        table_v = keep.tile([P, 2, 2, TILES, DH], F32)
-        table_g = keep.tile([P, 2, 2, TILES, 2, PAIRS], F32)
-        rows_bf = keep.tile([P, P], BF16)
-        cols = keep.tile([P, 32], F32)
+        bias_all = [keep.tile([P, N_OUT], BF16, name="bias_all_%d" % s) for s in range(2)]
+        gain_all = keep.tile([P, 4, DH], BF16)
+        rope_sb = keep.tile([P, ALL_TILES, 4 * PAIRS], BF16)
+        row_straight_tab = keep.tile([P, 2, 2, TILES, DH], F32)
+        row_crossed_tab = keep.tile([P, 2, 2, TILES, 2, PAIRS], F32)
+        vec_rows = keep.tile([P, P], BF16)
+        vec_cols = keep.tile([P, 2 * HEADS + 2], F32)
         picked = keep.tile([P, 2, COL_TILES, DH], BF16)
-        tabs = keep.tile([P, 2, 2, COL_TILES * P], F32)
+        col_tab = keep.tile([P, 2, 2, COL_TILES * P], F32)
         ident = keep.tile([P, P], F32)
         swap = keep.tile([P, P], F32)
         ident_bf = keep.tile([P, P], BF16)
         eps = keep.tile([P, 1], F32)
-        ones = keep.tile([P, 2], F32)
 
         nc.vector.memset(w_planes[0][:].rearrange("p g n -> p (g n)").bitcast(I32), 0)
         nc.vector.memset(eps[:], EPS)
-        nc.vector.memset(ones[:], 1.0)
-        nc.vector.memset(rows_bf[:].bitcast(I32), 0)
+        nc.vector.memset(vec_rows[:].bitcast(I32), 0)
         nc.vector.memset(w_planes[1][:].rearrange("p g n -> p (g n)").bitcast(I32), 0)
         make_identity(nc, ident[:])
         nc.vector.tensor_copy(out=ident_bf[:], in_=ident[:])
@@ -128,29 +125,27 @@ def tile_fluxjointattention_pa_kernel(
 
         def load_bias(s, first, last):
             nc.sync.dma_start(
-                out=bias_bc[s][:, first * BANK : last * BANK],
+                out=bias_all[s][:, first * BANK : last * BANK],
                 in_=bias_in[s][first * BANK : last * BANK].partition_broadcast(P),
             )
 
         def load_gains(s):
             for qk in range(2):
-                nc.sync.dma_start(out=gain_bc[:, 2 * s + qk, :], in_=gain_in[2 * s + qk].partition_broadcast(P))
+                nc.sync.dma_start(out=gain_all[:, 2 * s + qk, :], in_=gain_in[2 * s + qk].partition_broadcast(P))
 
-        def load_rope(first, last):
+        def load_rope():
             nc.sync.dma_start(
-                out=rope_sb[:, first * TILES : last * TILES, :].rearrange("p (k t) f -> p k (t f)", t=TILES),
-                in_=image_rotary_emb.rearrange("a b (k p t) j r c -> p (a b k) (t j r c)", p=P, t=TILES)[
-                    :, first:last, :
-                ],
+                out=rope_sb[:].rearrange("p (k t) f -> p k (t f)", t=TILES),
+                in_=image_rotary_emb.rearrange("a b (k p t) j r c -> p (a b k) (t j r c)", p=P, t=TILES),
             )
 
-        def load_rows():
+        def load_vec_rows():
             nc.sync.dma_start(
-                out=rows_bf[0 : 2 * HEADS, :], in_=a_qkv_b[0 : 2 * HEADS * DH].rearrange("(h f) -> h f", f=DH)
+                out=vec_rows[0 : 2 * HEADS, :], in_=a_qkv_b[0 : 2 * HEADS * DH].rearrange("(h f) -> h f", f=DH)
             )
             for qk in range(2):
                 nc.sync.dma_start(
-                    out=rows_bf[2 * HEADS + qk : 2 * HEADS + qk + 1, :],
+                    out=vec_rows[2 * HEADS + qk : 2 * HEADS + qk + 1, :],
                     in_=gain_in[2 + qk].rearrange("(o n) -> o n", o=1),
                 )
 
@@ -159,8 +154,8 @@ def tile_fluxjointattention_pa_kernel(
         load_x(2)
         load_scales(0)
         load_words(0, 0)
-        load_rope(0, BLOCKS)
-        load_rows()
+        load_rope()
+        load_vec_rows()
         load_bias(0, 0, 1)
         load_gains(0)
         load_words(0, 4)
@@ -176,10 +171,11 @@ def tile_fluxjointattention_pa_kernel(
         load_words(0, 3)
         load_words(1, 1)
         load_words(1, 3)
-        load_gains(1)
-        load_bias(1, 0, CHUNKS)
         load_words(1, 4)
         load_words(1, 5)
+        load_bias(1, 4, CHUNKS)
+        load_gains(1)
+        load_bias(1, 0, 4)
 
         grouped_x = {}
 
@@ -197,18 +193,14 @@ def tile_fluxjointattention_pa_kernel(
             if t == 0:
                 grouped = stage.tile([P, PASSES, TILES, P, 2], F32, align_bytes=64)
                 grouped_x[blk] = grouped
-                nc.scalar.copy(out=grouped_x[blk][:, :, t], in_=x_t[:].rearrange("p (g u) r -> p g r u", u=2))
-            else:
-                nc.scalar.copy(out=grouped_x[blk][:, :, t], in_=x_t[:].rearrange("p (g u) r -> p g r u", u=2))
+            nc.scalar.copy(out=grouped_x[blk][:, :, t], in_=x_t[:].rearrange("p (g u) r -> p g r u", u=2))
 
-        def quantise_tile(blk, t):
-            if t == 0:
-                return
-            n = blk * TILES
+        def quantise_block(blk):
+            first = blk * TILES * P
             for g in range(PASSES):
                 nc.vector.quantize_mx(
-                    out=x_codes[:, g, n * P : (n + TILES) * P].bitcast(FP8X4),
-                    scales=x_planes[:, g, n * P : (n + TILES) * P],
+                    out=x_codes[:, g, first : first + TILES * P].bitcast(FP8X4),
+                    scales=x_planes[:, g, first : first + TILES * P],
                     in_=grouped_x[blk][:, g].rearrange("p t r u -> p (t r u)").bitcast(BF16),
                 )
 
@@ -217,16 +209,16 @@ def tile_fluxjointattention_pa_kernel(
             s = 0 if blk == 0 else 1
             coef = rope_sb[:, blk * TILES : (blk + 1) * TILES, :].rearrange("p n (j c) -> p n c j", c=4)
             for qk in range(2):
-                gain = gain_bc[:, 2 * s + qk, :].rearrange("p (j i) -> p i j", i=2)
+                gain = gain_all[:, 2 * s + qk, :].rearrange("p (j i) -> p i j", i=2)
                 nc.vector.tensor_tensor(
-                    out=table_v[:, kb, qk].rearrange("p n (i j) -> p n i j", i=2),
+                    out=row_straight_tab[:, kb, qk].rearrange("p n (i j) -> p n i j", i=2),
                     in0=coef[:, :, 0:4:3, :],
                     in1=gain.unsqueeze(1).to_broadcast([P, TILES, 2, PAIRS]),
                     op=ALU.mult,
                 )
                 for i in range(2):
                     nc.gpsimd.tensor_tensor(
-                        out=table_g[:, kb, qk, :, i, :],
+                        out=row_crossed_tab[:, kb, qk, :, i, :],
                         in0=coef[:, :, 1 + i, :],
                         in1=gain[:, 1 - i, :].unsqueeze(1).to_broadcast([P, TILES, PAIRS]),
                         op=ALU.mult,
@@ -239,7 +231,7 @@ def tile_fluxjointattention_pa_kernel(
             nc.tensor.matmul(
                 coef[:].rearrange("p q t f -> p (q t f)"),
                 lhsT=ident[:],
-                rhs=table_v[:, kb].rearrange("p q t f -> p (q t f)"),
+                rhs=row_straight_tab[:, kb].rearrange("p q t f -> p (q t f)"),
                 start=True,
                 stop=True,
             )
@@ -256,53 +248,50 @@ def tile_fluxjointattention_pa_kernel(
                     out=picked[:, 1].rearrange("p n (j e) -> p n j e", e=2)[:, :, :, e], in_=coef[:, :, :, 2 - e]
                 )
 
-        def turn_columns():
+        def turn_vectors():
             col_ps = turn.tile([P, P], BF16, tag="turn")
-            nc.tensor.transpose(col_ps[:], rows_bf[:], ident_bf[:])
-            nc.scalar.copy(out=cols[:, 0 : 2 * HEADS + 2], in_=col_ps[:, 0 : 2 * HEADS + 2])
+            nc.tensor.transpose(col_ps[:], vec_rows[:], ident_bf[:])
+            nc.scalar.copy(out=vec_cols[:], in_=col_ps[:, 0 : 2 * HEADS + 2])
 
-        tab_tiles = []
+        picked_ps = []
+
+        def scale_tables(qk):
+            nc.scalar.activation(
+                out=col_tab[:, qk].rearrange("p k n -> p (k n)"),
+                in_=picked_ps[0][:].rearrange("p k n -> p (k n)"),
+                func=ACT.Copy,
+                scale=vec_cols[:, 2 * HEADS + qk : 2 * HEADS + qk + 1],
+            )
 
         def turn_tables():
             tab_ps = turn.tile([P, 2, COL_TILES * P], BF16, tag="turn")
             for k in range(2):
                 for n in range(COL_TILES):
                     nc.tensor.transpose(tab_ps[:, k, n * P : (n + 1) * P], picked[:, k, n, :], ident_bf[:])
-            tab_tiles.append(tab_ps)
-            nc.scalar.activation(
-                out=tabs[:, 0].rearrange("p k n -> p (k n)"),
-                in_=tab_ps[:].rearrange("p k n -> p (k n)"),
-                func=ACT.Copy,
-                scale=cols[:, 2 * HEADS : 2 * HEADS + 1],
-            )
+            picked_ps.append(tab_ps)
+            scale_tables(0)
 
-        def key_tables():
-            tab_ps = tab_tiles[0]
-            nc.scalar.activation(
-                out=tabs[:, 1].rearrange("p k n -> p (k n)"),
-                in_=tab_ps[:].rearrange("p k n -> p (k n)"),
-                func=ACT.Copy,
-                scale=cols[:, 2 * HEADS + 1 : 2 * HEADS + 2],
-            )
-
+        row_steps = [("row", blk, part, m) for blk in ROW_BLOCKS for m in range(2) for part in range(2)]
+        val_steps = [("row", blk, 2, m) for blk in range(BLOCKS) for m in range(2)]
+        col_steps = [("col", part, GROUP * m + h) for m in range(2) for part in range(2) for h in range(GROUP)]
+        steps = row_steps + val_steps + col_steps
+        n_row, n_val = len(row_steps), len(val_steps)
         live = {}
 
         def project(n):
-            kind = steps[n][0]
             st = live.setdefault(n, {})
-            if kind == "col":
+            if steps[n][0] == "col":
                 part, h = steps[n][1:]
                 c = 2 * part + h // GROUP
                 hl = h % GROUP
-                first = COL_FIRST * TILES * P
                 acc = sums.tile([P, BANK], F32, tag="acc")
                 for g in range(PASSES):
                     nc.tensor.matmul_mx(
                         out=acc[:],
                         lhsT=w_words[:, 1, c, g, hl * 2 * DH : (hl + 1) * 2 * DH].bitcast(FP4X4),
                         lhsT_scale=w_planes[1][:, g, c * BANK + hl * DH : c * BANK + (hl + 1) * DH],
-                        rhs=x_codes[:, g, first : first + BANK].bitcast(FP8X4),
-                        rhs_scale=x_planes[:, g, first : first + BANK],
+                        rhs=x_codes[:, g, COL_TOKEN : COL_TOKEN + BANK].bitcast(FP8X4),
+                        rhs_scale=x_planes[:, g, COL_TOKEN : COL_TOKEN + BANK],
                         start=(g == 0),
                         stop=(g == PASSES - 1),
                     )
@@ -339,7 +328,7 @@ def tile_fluxjointattention_pa_kernel(
             s = 0 if blk == 0 else 1
             c = 2 * part + m
             st = live[n]
-            bias = bias_bc[s][:, c * BANK : (c + 1) * BANK]
+            bias = bias_all[s][:, c * BANK : (c + 1) * BANK]
             if part == 2:
                 out_sb = result.tile([P, GROUP, TILES, DH], F32, tag="out_sb")
                 for t in range(TILES):
@@ -361,6 +350,13 @@ def tile_fluxjointattention_pa_kernel(
                     )
                 st["u"] = u
 
+        def inverse_rms(sum_sq, width, tag):
+            inv_rms = small.tile([P, width], F32, tag=tag)
+            nc.scalar.activation(
+                out=inv_rms[:], in_=sum_sq[:], func=ACT.Abs_reciprocal_sqrt, bias=eps[:], scale=1.0 / DH
+            )
+            return inv_rms
+
         def row_squares(n):
             st = live[n]
             u = st["u"]
@@ -374,13 +370,9 @@ def tile_fluxjointattention_pa_kernel(
                         func=ACT.Square,
                         accum_out=sum_sq[:, t * GROUP + h : t * GROUP + h + 1],
                     )
-            inv_rms = small.tile([P, TILES * GROUP], F32)
-            nc.scalar.activation(
-                out=inv_rms[:], in_=sum_sq[:], func=ACT.Abs_reciprocal_sqrt, bias=eps[:], scale=1.0 / DH
-            )
-            st["inv_rms"] = inv_rms
+            st["inv_rms"] = inverse_rms(sum_sq, TILES * GROUP, "inv_rms")
 
-        def row_straight(n):
+        def row_products(n):
             blk, part, m = steps[n][1:]
             kb = ROW_BLOCKS.index(blk)
             st = live[n]
@@ -392,43 +384,25 @@ def tile_fluxjointattention_pa_kernel(
                 in1=coef_ps[kb][:, part].unsqueeze(2).to_broadcast([P, TILES, GROUP, DH]),
                 op=ALU.mult,
             )
-            st["straight"] = straight
-
-        def row_crossed(n):
-            blk, part, m = steps[n][1:]
-            kb = ROW_BLOCKS.index(blk)
-            st = live[n]
-            u = st["u"]
             crossed = rowwork.tile([P, TILES, GROUP, 2, PAIRS], F32)
             for i in range(2):
                 nc.gpsimd.tensor_tensor(
                     out=crossed[:, :, :, i, :],
                     in0=u[:, :, :, 1 - i, :],
-                    in1=table_g[:, kb, part, :, i, :].unsqueeze(2).to_broadcast([P, TILES, GROUP, PAIRS]),
+                    in1=row_crossed_tab[:, kb, part, :, i, :].unsqueeze(2).to_broadcast([P, TILES, GROUP, PAIRS]),
                     op=ALU.mult,
                 )
-            st["crossed"] = crossed
-
-        def row_add(n):
-            st = live[n]
-            straight = st["straight"]
             nc.gpsimd.tensor_tensor(
                 out=straight[:].rearrange("p t h i j -> p (t h i j)"),
                 in0=straight[:].rearrange("p t h i j -> p (t h i j)"),
-                in1=st["crossed"][:].rearrange("p t h i j -> p (t h i j)"),
+                in1=crossed[:].rearrange("p t h i j -> p (t h i j)"),
                 op=ALU.add,
             )
-
-        def reciprocal(n):
-            st = live[n]
-            inv_rms = small.tile([P, TILES * GROUP], F32)
-            width = COL_TILES if steps[n][0] == "col" else TILES * GROUP
-            nc.vector.reciprocal(out=inv_rms[:, 0:width], in_=st["rms"][:])
-            st["inv_rms"] = inv_rms
+            st["rotated"] = straight
 
         def row_scale(n):
             st = live[n]
-            rotated = st["straight"]
+            rotated = st["rotated"]
             inv_rms = st["inv_rms"]
             out_sb = result.tile([P, GROUP, TILES, DH], F32, tag="out_sb")
             for t in range(TILES):
@@ -441,106 +415,96 @@ def tile_fluxjointattention_pa_kernel(
                     )
             store_rows(n, out_sb)
 
-        def col_square(n):
+        def col_bias_of(n):
             part, h = steps[n][1:]
+            return vec_cols[:, part * HEADS + h : part * HEADS + h + 1]
+
+        def col_plain(n):
             st = live[n]
-            bias = cols[:, part * HEADS + h : part * HEADS + h + 1]
-            sq = colwork.tile([P, BANK], F32)
-            nc.scalar.activation(out=sq[:], in_=st["acc"][:], func=ACT.Identity, bias=bias, scale=1.0)
-            st["sq"] = sq
+            plain = colwork.tile([P, BANK], F32)
+            nc.scalar.activation(out=plain[:], in_=st["acc"][:], func=ACT.Identity, bias=col_bias_of(n), scale=1.0)
+            st["plain"] = plain
 
         def col_products(n):
-            part, h = steps[n][1:]
+            part = steps[n][1]
             st = live[n]
-            bias = cols[:, part * HEADS + h : part * HEADS + h + 1]
             for k, name in enumerate(("straight", "crossed")):
                 prod = colwork.tile([P, BANK], F32, tag=name)
-                if k == 1 and n % 4 in GPSIMD_CROSSES:
-                    nc.gpsimd.tensor_tensor(out=prod[:], in0=st["sq"][:], in1=tabs[:, part, k, :], op=ALU.mult)
+                if k == 1 and n % 2 == 1:
+                    nc.gpsimd.tensor_tensor(out=prod[:], in0=st["plain"][:], in1=col_tab[:, part, k, :], op=ALU.mult)
                 else:
                     nc.vector.scalar_tensor_tensor(
-                        out=prod[:], in0=st["acc"][:], scalar=bias, in1=tabs[:, part, k, :], op0=ALU.add, op1=ALU.mult
+                        out=prod[:],
+                        in0=st["acc"][:],
+                        scalar=col_bias_of(n),
+                        in1=col_tab[:, part, k, :],
+                        op0=ALU.add,
+                        op1=ALU.mult,
                     )
                 st[name] = prod
 
-        def col_sums(n):
+        def col_turn_plain(n):
             st = live[n]
-            plain = turn.tile([P, COL_TILES, DH], F32, tag="turn")
+            plain_ps = turn.tile([P, COL_TILES, DH], F32, tag="turn")
             for k in range(COL_TILES):
-                nc.tensor.transpose(plain[:, k, :], st["sq"][:, k * P : (k + 1) * P], ident[:])
-            st["plain"] = plain
+                nc.tensor.transpose(plain_ps[:, k, :], st["plain"][:, k * P : (k + 1) * P], ident[:])
+            st["plain_ps"] = plain_ps
 
-        def col_turn(n):
+        def col_turn_products(n):
             st = live[n]
-            rot = turn.tile([P, COL_TILES, DH], F32, tag="turn")
+            rotated_ps = turn.tile([P, COL_TILES, DH], F32, tag="turn")
             for k in range(COL_TILES):
                 nc.tensor.matmul(
-                    rot[:, k, :], lhsT=st["straight"][:, k * P : (k + 1) * P], rhs=ident[:],
-                    is_transpose=True, start=True, stop=False,
+                    rotated_ps[:, k, :],
+                    lhsT=st["straight"][:, k * P : (k + 1) * P],
+                    rhs=ident[:],
+                    is_transpose=True,
+                    start=True,
+                    stop=False,
                 )
                 nc.tensor.matmul(
-                    rot[:, k, :], lhsT=st["crossed"][:, k * P : (k + 1) * P], rhs=swap[:],
-                    is_transpose=True, start=False, stop=True,
+                    rotated_ps[:, k, :],
+                    lhsT=st["crossed"][:, k * P : (k + 1) * P],
+                    rhs=swap[:],
+                    is_transpose=True,
+                    start=False,
+                    stop=True,
                 )
-            st["rot"] = rot
+            st["rotated_ps"] = rotated_ps
 
-        def col_root(n):
+        def col_squares(n):
             st = live[n]
-            junk = colwork.tile([P, COL_TILES, DH], BF16)
+            squares = colwork.tile([P, COL_TILES, DH], BF16, tag="col_squares")
             sum_sq = small.tile([P, COL_TILES], F32, tag="col_sum")
             for k in range(COL_TILES):
                 nc.scalar.activation(
-                    out=junk[:, k, :], in_=st["plain"][:, k, :], func=ACT.Square, accum_out=sum_sq[:, k : k + 1]
+                    out=squares[:, k, :], in_=st["plain_ps"][:, k, :], func=ACT.Square, accum_out=sum_sq[:, k : k + 1]
                 )
-            inv_rms = small.tile([P, COL_TILES], F32, tag="col_inv")
-            nc.scalar.activation(
-                out=inv_rms[:], in_=sum_sq[:], func=ACT.Abs_reciprocal_sqrt, bias=eps[:], scale=1.0 / DH
-            )
-            st["inv_rms"] = inv_rms
+            st["inv_rms"] = inverse_rms(sum_sq, COL_TILES, "col_inv")
 
         def col_scale(n):
             part, h = steps[n][1:]
             st = live[n]
             out_sb = result.tile([P, COL_TILES, DH], F32, tag="col_out")
-            if n % 4 in VECTOR_SCALES:
-                nc.vector.tensor_tensor(
-                    out=out_sb[:],
-                    in0=st["rot"][:],
-                    in1=st["inv_rms"][:].unsqueeze(2).to_broadcast([P, COL_TILES, DH]),
-                    op=ALU.mult,
-                )
-            else:
-                for k in range(COL_TILES):
-                    nc.scalar.activation(
-                        out=out_sb[:, k, :], in_=st["rot"][:, k, :], func=ACT.Copy, scale=st["inv_rms"][:, k : k + 1]
-                    )
-            first = COL_FIRST * TILES * P
-            rows = outs[part][0, h, first : first + COL_TILES * P, :]
+            nc.vector.tensor_tensor(
+                out=out_sb[:],
+                in0=st["rotated_ps"][:],
+                in1=st["inv_rms"][:].unsqueeze(2).to_broadcast([P, COL_TILES, DH]),
+                op=ALU.mult,
+            )
+            rows = outs[part][0, h, COL_TOKEN : COL_TOKEN + COL_TILES * P, :]
             nc.sync.dma_start(
                 out=rows.rearrange("(b p t) d -> p b (t d)", p=P, t=TILES),
                 in_=out_sb[:].rearrange("p (b t) d -> p b (t d)", t=TILES),
             )
-
-        row_steps = [("row", blk, part, m) for blk in ROW_BLOCKS for m in range(2) for part in range(2)]
-        val_steps = [("row", blk, 2, m) for blk in range(BLOCKS) for m in range(2)]
-        col_steps = [("col", part, GROUP * m + h) for m in range(2) for part in range(2) for h in range(GROUP)]
-        steps = row_steps + val_steps + col_steps
-        n_row, n_val = len(row_steps), len(val_steps)
-
-        def do(fn, n):
-            if n is not None:
-                fn(n)
-
-        def row_gpsimd(n):
-            row_crossed(n)
-            row_add(n)
 
         fillers = []
         for k in range(n_row):
             fillers += [k, n_row + k]
         LEAD = 2
         SCALE_LAG = 3
-        n_slots = len(col_steps) + LEAD + 3
+        DRAIN = 2
+        n_slots = len(col_steps) + LEAD + DRAIN
 
         def filler(k):
             return fillers[k] if 0 <= k < len(fillers) else None
@@ -551,44 +515,45 @@ def tile_fluxjointattention_pa_kernel(
         def is_row(n):
             return n is not None and n < n_row
 
-        for blk in range(BLOCKS - 1):
-            for t in range(TILES):
-                transpose_tile(blk, t)
-            for t in range(TILES):
-                quantise_tile(blk, t)
+        def do(stage_of, n):
+            if n is not None:
+                stage_of(n)
 
-        prep = {
-            (0, 0): lambda: (pick_coefficients(), turn_columns()),
+        extras = {
+            (0, 0): lambda: (pick_coefficients(), turn_vectors()),
             (0, 1): lambda: (build_row_tables(0), stage_coefficients(0)),
             (0, 2): lambda: turn_tables(),
-            (3, 1): lambda: key_tables(),
+            (3, 1): lambda: scale_tables(1),
             (3, 2): lambda: transpose_tile(3, 0),
             (4, 2): lambda: transpose_tile(3, 1),
-            (5, 0): lambda: (quantise_tile(3, 1), build_row_tables(1)),
+            (5, 0): lambda: (quantise_block(3), build_row_tables(1)),
             (7, 1): lambda: stage_coefficients(1),
         }
 
-        def hook(r, k):
-            if (r, k) in prep:
-                prep[(r, k)]()
+        def extra(k, place):
+            if (k, place) in extras:
+                extras[(k, place)]()
 
+        for blk in range(BLOCKS - 1):
+            for t in range(TILES):
+                transpose_tile(blk, t)
+            quantise_block(blk)
         project(fillers[0])
         for k in range(n_slots):
             do(project, col(k))
             do(row_bias, filler(k))
-            hook(k, 0)
-            do(col_sums, col(k - 1))
-            do(col_square, col(k))
-            do(col_turn, col(k - 2))
-            do(col_root, col(k - 1))
+            extra(k, 0)
+            do(col_turn_plain, col(k - 1))
+            do(col_plain, col(k))
+            do(col_turn_products, col(k - 2))
+            do(col_squares, col(k - 1))
             do(col_products, col(k))
             do(project, filler(k + 1))
-            hook(k, 1)
+            extra(k, 1)
             do(col_scale, col(k - 2))
             if is_row(filler(k)):
-                row_straight(filler(k))
-                row_gpsimd(filler(k))
+                row_products(filler(k))
                 row_squares(filler(k))
             if is_row(filler(k - SCALE_LAG)):
                 row_scale(filler(k - SCALE_LAG))
-            hook(k, 2)
+            extra(k, 2)

@@ -428,20 +428,20 @@ def tile_fluxjointattention_pa_kernel(
         def col_products(n):
             part = steps[n][1]
             st = live[n]
-            for k, name in enumerate(("straight", "crossed")):
-                prod = colwork.tile([P, BANK], F32, tag=name)
-                if k == 1 and n % 2 == 1:
-                    nc.gpsimd.tensor_tensor(out=prod[:], in0=st["plain"][:], in1=col_tab[:, part, k, :], op=ALU.mult)
-                else:
-                    nc.vector.scalar_tensor_tensor(
-                        out=prod[:],
-                        in0=st["acc"][:],
-                        scalar=col_bias_of(n),
-                        in1=col_tab[:, part, k, :],
-                        op0=ALU.add,
-                        op1=ALU.mult,
-                    )
-                st[name] = prod
+            products = colwork.tile([P, 2, BANK], F32, tag="products")
+            on_gpsimd = n % 4 == 1
+            kinds = 1 if on_gpsimd else 2
+            nc.vector.scalar_tensor_tensor(
+                out=products[:, 0:kinds, :],
+                in0=st["acc"][:].unsqueeze(1).to_broadcast([P, kinds, BANK]),
+                scalar=col_bias_of(n),
+                in1=col_tab[:, part, 0:kinds, :],
+                op0=ALU.add,
+                op1=ALU.mult,
+            )
+            if on_gpsimd:
+                nc.gpsimd.tensor_tensor(out=products[:, 1, :], in0=st["plain"][:], in1=col_tab[:, part, 1, :], op=ALU.mult)
+            st["products"] = products
 
         def col_turn_plain(n):
             st = live[n]
@@ -456,7 +456,7 @@ def tile_fluxjointattention_pa_kernel(
             for k in range(COL_TILES):
                 nc.tensor.matmul(
                     rotated_ps[:, k, :],
-                    lhsT=st["straight"][:, k * P : (k + 1) * P],
+                    lhsT=st["products"][:, 0, k * P : (k + 1) * P],
                     rhs=ident[:],
                     is_transpose=True,
                     start=True,
@@ -464,7 +464,7 @@ def tile_fluxjointattention_pa_kernel(
                 )
                 nc.tensor.matmul(
                     rotated_ps[:, k, :],
-                    lhsT=st["crossed"][:, k * P : (k + 1) * P],
+                    lhsT=st["products"][:, 1, k * P : (k + 1) * P],
                     rhs=swap[:],
                     is_transpose=True,
                     start=False,

@@ -350,27 +350,46 @@ def tile_fluxjointattention_pa_kernel(
                     )
                 st["u"] = u
 
-        def inverse_rms(sum_sq, width, tag):
-            inv_rms = small.tile([P, width], F32, tag=tag)
-            nc.scalar.activation(
-                out=inv_rms[:], in_=sum_sq[:], func=ACT.Abs_reciprocal_sqrt, bias=eps[:], scale=1.0 / DH
-            )
-            return inv_rms
+        sums_of = {}
 
-        def row_squares(n):
+        def slot_sums(k, n):
+            if k not in sums_of:
+                sum_sq = small.tile([P, COL_TILES + TILES * GROUP], F32, tag="sum_sq")
+                sums_of[k] = (sum_sq, [])
+            sums_of[k][1].append(n)
+            return sums_of[k][0]
+
+        def inverse_rms(k):
+            if k not in sums_of:
+                return
+            sum_sq, writers = sums_of[k]
+            first = 0 if any(steps[n][0] == "col" for n in writers) else COL_TILES
+            last = COL_TILES + TILES * GROUP if any(steps[n][0] == "row" for n in writers) else COL_TILES
+            inv_rms = small.tile([P, COL_TILES + TILES * GROUP], F32, tag="inv_rms")
+            nc.scalar.activation(
+                out=inv_rms[:, first:last],
+                in_=sum_sq[:, first:last],
+                func=ACT.Abs_reciprocal_sqrt,
+                bias=eps[:],
+                scale=1.0 / DH,
+            )
+            for n in writers:
+                live[n]["inv_rms"] = inv_rms[:, 0:COL_TILES] if steps[n][0] == "col" else inv_rms[:, COL_TILES:]
+
+        def row_squares(k, n):
             st = live[n]
             u = st["u"]
             squares = rowwork.tile([P, TILES, GROUP, DH], BF16)
-            sum_sq = small.tile([P, TILES * GROUP], F32)
+            sum_sq = slot_sums(k, n)
             for t in range(TILES):
                 for h in range(GROUP):
+                    column = COL_TILES + t * GROUP + h
                     nc.scalar.activation(
                         out=squares[:, t, h, :],
                         in_=u[:, t, h].rearrange("p i j -> p (i j)"),
                         func=ACT.Square,
-                        accum_out=sum_sq[:, t * GROUP + h : t * GROUP + h + 1],
+                        accum_out=sum_sq[:, column : column + 1],
                     )
-            st["inv_rms"] = inverse_rms(sum_sq, TILES * GROUP, "inv_rms")
 
         def row_products(n):
             blk, part, m = steps[n][1:]
@@ -472,15 +491,14 @@ def tile_fluxjointattention_pa_kernel(
                 )
             st["rotated_ps"] = rotated_ps
 
-        def col_squares(n):
+        def col_squares(slot, n):
             st = live[n]
             squares = colwork.tile([P, COL_TILES, DH], BF16, tag="col_squares")
-            sum_sq = small.tile([P, COL_TILES], F32, tag="col_sum")
+            sum_sq = slot_sums(slot, n)
             for k in range(COL_TILES):
                 nc.scalar.activation(
                     out=squares[:, k, :], in_=st["plain_ps"][:, k, :], func=ACT.Square, accum_out=sum_sq[:, k : k + 1]
                 )
-            st["inv_rms"] = inverse_rms(sum_sq, COL_TILES, "col_inv")
 
         def col_scale(n):
             part, h = steps[n][1:]
@@ -489,7 +507,7 @@ def tile_fluxjointattention_pa_kernel(
             nc.vector.tensor_tensor(
                 out=out_sb[:],
                 in0=st["rotated_ps"][:],
-                in1=st["inv_rms"][:].unsqueeze(2).to_broadcast([P, COL_TILES, DH]),
+                in1=st["inv_rms"].unsqueeze(2).to_broadcast([P, COL_TILES, DH]),
                 op=ALU.mult,
             )
             rows = outs[part][0, h, COL_TOKEN : COL_TOKEN + COL_TILES * P, :]
@@ -545,15 +563,17 @@ def tile_fluxjointattention_pa_kernel(
             extra(k, 0)
             do(col_turn_plain, col(k - 1))
             do(col_plain, col(k))
+            inverse_rms(k - 1)
             do(col_turn_products, col(k - 2))
-            do(col_squares, col(k - 1))
+            if col(k - 1) is not None:
+                col_squares(k, col(k - 1))
             do(col_products, col(k))
             do(project, filler(k + 1))
             extra(k, 1)
             do(col_scale, col(k - 2))
             if is_row(filler(k)):
                 row_products(filler(k))
-                row_squares(filler(k))
+                row_squares(k, filler(k))
             if is_row(filler(k - SCALE_LAG)):
                 row_scale(filler(k - SCALE_LAG))
             extra(k, 2)

@@ -90,11 +90,13 @@ def tile_fluxjointattention_pa_kernel(
         swap = keep.tile([P, P], F32)
         ident_bf = keep.tile([P, P], BF16)
         eps = keep.tile([P, 1], F32)
+        idle_sb = keep.tile([P, BANK], BF16)
 
+        nc.gpsimd.memset(idle_sb[:].bitcast(F32), 0.0)
         nc.vector.memset(w_planes[0][:].rearrange("p g n -> p (g n)").bitcast(I32), 0)
         nc.vector.memset(eps[:], EPS)
         nc.vector.memset(vec_rows[:].bitcast(I32), 0)
-        nc.vector.memset(w_planes[1][:].rearrange("p g n -> p (g n)").bitcast(I32), 0)
+        nc.gpsimd.memset(w_planes[1][:].rearrange("p g n -> p (g n)").bitcast(F32), 0.0)
         make_identity(nc, ident[:])
         nc.vector.tensor_copy(out=ident_bf[:], in_=ident[:])
         pairs_of = "p (j i) -> p j i"
@@ -133,10 +135,10 @@ def tile_fluxjointattention_pa_kernel(
             for qk in range(2):
                 nc.sync.dma_start(out=gain_all[:, 2 * s + qk, :], in_=gain_in[2 * s + qk].partition_broadcast(P))
 
-        def load_rope():
+        def load_rope(first, last):
             nc.sync.dma_start(
-                out=rope_sb[:].rearrange("p (k t) f -> p k (t f)", t=TILES),
-                in_=image_rotary_emb.rearrange("a b (k p t) j r c -> p (a b k) (t j r c)", p=P, t=TILES),
+                out=rope_sb[:].rearrange("p (k t) f -> p k (t f)", t=TILES)[:, first:last, :],
+                in_=image_rotary_emb.rearrange("a b (k p t) j r c -> p (a b k) (t j r c)", p=P, t=TILES)[:, first:last, :],
             )
 
         def load_vec_rows():
@@ -150,14 +152,15 @@ def tile_fluxjointattention_pa_kernel(
                 )
 
         load_x(0)
-        load_x(1)
-        load_x(2)
         load_scales(0)
         load_words(0, 0)
-        load_rope()
-        load_vec_rows()
         load_bias(0, 0, 1)
+        load_rope(0, 1)
         load_gains(0)
+        load_x(1)
+        load_x(2)
+        load_rope(1, BLOCKS)
+        load_vec_rows()
         load_words(0, 4)
         load_bias(0, 4, CHUNKS)
         load_scales(1)
@@ -179,7 +182,18 @@ def tile_fluxjointattention_pa_kernel(
 
         grouped_x = {}
 
+        def keep_clock_up(count):
+            idle_ps = turn.tile([P, BANK], F32, tag="turn")
+            for i in range(count):
+                nc.tensor.matmul(idle_ps[:], lhsT=idle_sb[:, 0:P], rhs=idle_sb[:], start=True, stop=True)
+
         def transpose_tile(blk, t):
+            turn_x(blk, t)
+            copy_x(blk, t, nc.scalar.copy)
+
+        turned_x = {}
+
+        def turn_x(blk, t):
             x_pairs = x_sb[:].bitcast(F32)
             if blk < BLOCKS - 1:
                 x_t = sums.tile([P, PASSES * 2, P], F32, tag="acc")
@@ -190,10 +204,13 @@ def tile_fluxjointattention_pa_kernel(
                     nc.tensor.transpose(
                         x_t[:, 2 * g + u, :], x_pairs[:, blk, t, 256 * g + u : 256 * (g + 1) : 2], ident[:]
                     )
-            if t == 0:
+            turned_x[(blk, t)] = x_t
+
+        def copy_x(blk, t, copy):
+            if blk not in grouped_x:
                 grouped = stage.tile([P, PASSES, TILES, P, 2], F32, align_bytes=64)
                 grouped_x[blk] = grouped
-            nc.scalar.copy(out=grouped_x[blk][:, :, t], in_=x_t[:].rearrange("p (g u) r -> p g r u", u=2))
+            copy(out=grouped_x[blk][:, :, t], in_=turned_x[(blk, t)][:].rearrange("p (g u) r -> p g r u", u=2))
 
         def quantise_block(blk):
             first = blk * TILES * P
@@ -240,11 +257,11 @@ def tile_fluxjointattention_pa_kernel(
         def pick_coefficients():
             first = COL_FIRST * TILES
             coef = rope_sb[:, first : first + COL_TILES, :].rearrange("p n (j c) -> p n j c", c=4)
-            nc.gpsimd.tensor_copy(
+            nc.scalar.copy(
                 out=picked[:, 0].rearrange("p n (j e) -> p n j e", e=2), in_=coef[:, :, :, 0:4:3]
             )
             for e in range(2):
-                nc.gpsimd.tensor_copy(
+                nc.scalar.copy(
                     out=picked[:, 1].rearrange("p n (j e) -> p n j e", e=2)[:, :, :, e], in_=coef[:, :, :, 2 - e]
                 )
 
@@ -448,7 +465,7 @@ def tile_fluxjointattention_pa_kernel(
             part = steps[n][1]
             st = live[n]
             products = colwork.tile([P, 2, BANK], F32, tag="products")
-            on_gpsimd = n % 4 == 1
+            on_gpsimd = n % 8 in (1, 3, 5)
             kinds = 1 if on_gpsimd else 2
             nc.vector.scalar_tensor_tensor(
                 out=products[:, 0:kinds, :],
@@ -519,7 +536,7 @@ def tile_fluxjointattention_pa_kernel(
         fillers = []
         for k in range(n_row):
             fillers += [k, n_row + k]
-        LEAD = 2
+        LEAD = 1
         SCALE_LAG = 3
         DRAIN = 2
         n_slots = len(col_steps) + LEAD + DRAIN
@@ -538,10 +555,7 @@ def tile_fluxjointattention_pa_kernel(
                 stage_of(n)
 
         extras = {
-            (0, 0): lambda: (pick_coefficients(), turn_vectors()),
-            (0, 1): lambda: (build_row_tables(0), stage_coefficients(0)),
-            (0, 2): lambda: turn_tables(),
-            (3, 1): lambda: scale_tables(1),
+            (2, 1): lambda: scale_tables(1),
             (3, 2): lambda: transpose_tile(3, 0),
             (4, 2): lambda: transpose_tile(3, 1),
             (5, 0): lambda: (quantise_block(3), build_row_tables(1)),
@@ -552,12 +566,33 @@ def tile_fluxjointattention_pa_kernel(
             if (k, place) in extras:
                 extras[(k, place)]()
 
-        for blk in range(BLOCKS - 1):
-            for t in range(TILES):
-                transpose_tile(blk, t)
-            quantise_block(blk)
+        keep_clock_up(8)
+        turn_x(0, 0)
+        copy_x(0, 0, nc.scalar.copy)
+        turn_x(0, 1)
+        copy_x(0, 1, nc.vector.tensor_copy)
+        quantise_block(0)
+        build_row_tables(0)
         project(fillers[0])
-        for k in range(n_slots):
+        turn_x(1, 0)
+        turn_x(1, 1)
+        stage_coefficients(0)
+        row_bias(fillers[0])
+        copy_x(1, 0, nc.vector.tensor_copy)
+        copy_x(1, 1, nc.vector.tensor_copy)
+        quantise_block(1)
+        row_products(fillers[0])
+        row_squares(0, fillers[0])
+        turn_x(2, 0)
+        turn_x(2, 1)
+        pick_coefficients()
+        copy_x(2, 0, nc.scalar.copy)
+        copy_x(2, 1, nc.vector.tensor_copy)
+        quantise_block(2)
+        project(fillers[1])
+        turn_vectors()
+        turn_tables()
+        for k in range(1, n_slots):
             do(project, col(k))
             do(row_bias, filler(k))
             extra(k, 0)

@@ -66,7 +66,7 @@ def tile_fluxjointattention_pa_kernel(
         tc.tile_pool(name="rowwork", bufs=4) as rowwork,
         tc.tile_pool(name="colwork", bufs=3) as colwork,
         tc.tile_pool(name="small", bufs=6) as small,
-        tc.tile_pool(name="result", bufs=4) as result,
+        tc.tile_pool(name="result", bufs=6) as result,
         tc.psum_pool(name="sums", bufs=4) as sums,
         tc.psum_pool(name="turn", bufs=3) as turn,
         tc.psum_pool(name="coefs", bufs=1) as coefs,
@@ -91,13 +91,17 @@ def tile_fluxjointattention_pa_kernel(
         ident_bf = keep.tile([P, P], BF16)
         eps = keep.tile([P, 1], F32)
         idle_sb = keep.tile([P, BANK], BF16)
+        HALF = N_OUT // 2
+        spread_rows = [keep.tile([P, HALF + 2 * DH], BF16, name="spread_rows_%d" % s) for s in range(2)]
 
-        nc.gpsimd.memset(idle_sb[:].bitcast(F32), 0.0)
+        nc.gpsimd.memset(spread_rows[0][:].bitcast(F32), 0.0)
+        nc.vector.memset(idle_sb[:].bitcast(I32), 0)
         nc.vector.memset(w_planes[0][:].rearrange("p g n -> p (g n)").bitcast(I32), 0)
         nc.vector.memset(eps[:], EPS)
         nc.vector.memset(vec_rows[:].bitcast(I32), 0)
-        nc.gpsimd.memset(w_planes[1][:].rearrange("p g n -> p (g n)").bitcast(F32), 0.0)
         make_identity(nc, ident[:])
+        nc.gpsimd.memset(spread_rows[1][:].bitcast(F32), 0.0)
+        nc.gpsimd.memset(w_planes[1][:].rearrange("p g n -> p (g n)").bitcast(F32), 0.0)
         nc.vector.tensor_copy(out=ident_bf[:], in_=ident[:])
         pairs_of = "p (j i) -> p j i"
         for i in range(2):
@@ -125,15 +129,13 @@ def tile_fluxjointattention_pa_kernel(
                 in_=words_in[s].bitcast(I32)[:, :, c * width : (c + 1) * width].rearrange("g p n -> p g n"),
             )
 
-        def load_bias(s, first, last):
-            nc.sync.dma_start(
-                out=bias_all[s][:, first * BANK : last * BANK],
-                in_=bias_in[s][first * BANK : last * BANK].partition_broadcast(P),
-            )
-
-        def load_gains(s):
+        def load_vectors(s):
+            nc.sync.dma_start(out=spread_rows[s][0:2, 0:HALF], in_=bias_in[s].rearrange("(r n) -> r n", r=2))
             for qk in range(2):
-                nc.sync.dma_start(out=gain_all[:, 2 * s + qk, :], in_=gain_in[2 * s + qk].partition_broadcast(P))
+                nc.sync.dma_start(
+                    out=spread_rows[s][0:1, HALF + qk * DH : HALF + (qk + 1) * DH],
+                    in_=gain_in[2 * s + qk].rearrange("(o n) -> o n", o=1),
+                )
 
         def load_rope(first, last):
             nc.sync.dma_start(
@@ -152,33 +154,23 @@ def tile_fluxjointattention_pa_kernel(
                 )
 
         load_x(0)
+        load_vectors(0)
         load_scales(0)
         load_words(0, 0)
-        load_bias(0, 0, 1)
         load_rope(0, 1)
-        load_gains(0)
         load_x(1)
         load_x(2)
         load_rope(1, BLOCKS)
         load_vec_rows()
         load_words(0, 4)
-        load_bias(0, 4, CHUNKS)
         load_scales(1)
         load_words(1, 0)
         load_words(0, 2)
-        load_bias(0, 1, 4)
-        load_words(1, 2)
+        load_vectors(1)
         load_words(0, 5)
         load_words(0, 1)
         load_x(3)
-        load_words(0, 3)
-        load_words(1, 1)
-        load_words(1, 3)
         load_words(1, 4)
-        load_words(1, 5)
-        load_bias(1, 4, CHUNKS)
-        load_gains(1)
-        load_bias(1, 0, 4)
 
         grouped_x = {}
 
@@ -220,6 +212,27 @@ def tile_fluxjointattention_pa_kernel(
                     scales=x_planes[:, g, first : first + TILES * P],
                     in_=grouped_x[blk][:, g].rearrange("p t r u -> p (t r u)").bitcast(BF16),
                 )
+
+        def spread(s, row, first, width, out_ps):
+            nc.tensor.matmul(
+                out_ps,
+                lhsT=ident_bf[:, row : row + 1].to_broadcast([P, P]),
+                rhs=spread_rows[s][:, first : first + width],
+                start=True,
+                stop=True,
+            )
+
+        def spread_bias(s, pair, copy):
+            both = turn.tile([P, 2 * BANK], BF16, tag="turn")
+            for j in range(2):
+                c = 2 * pair + j
+                spread(s, c // 3, (c % 3) * BANK, BANK, both[:, j * BANK : (j + 1) * BANK])
+            copy(out=bias_all[s][:, 2 * pair * BANK : 2 * (pair + 1) * BANK], in_=both[:])
+
+        def spread_gains(s, copy):
+            two = turn.tile([P, 2 * BANK], BF16, tag="turn")
+            spread(s, 0, HALF, 2 * DH, two[:, 0 : 2 * DH])
+            copy(out=gain_all[:, 2 * s : 2 * s + 2, :].rearrange("p g d -> p (g d)"), in_=two[:, 0 : 2 * DH])
 
         def build_row_tables(kb):
             blk = ROW_BLOCKS[kb]
@@ -555,10 +568,14 @@ def tile_fluxjointattention_pa_kernel(
                 stage_of(n)
 
         extras = {
+            (1, 2): lambda: (load_words(1, 2), load_words(0, 3)),
             (2, 1): lambda: scale_tables(1),
-            (3, 2): lambda: transpose_tile(3, 0),
-            (4, 2): lambda: transpose_tile(3, 1),
+            (2, 2): lambda: (spread_bias(1, 2, nc.scalar.copy), load_words(1, 5)),
+            (3, 2): lambda: (transpose_tile(3, 0), spread_gains(1, nc.scalar.copy)),
+            (4, 2): lambda: (transpose_tile(3, 1), load_words(1, 1)),
             (5, 0): lambda: (quantise_block(3), build_row_tables(1)),
+            (5, 2): lambda: spread_bias(1, 0, nc.scalar.copy),
+            (6, 2): lambda: (spread_bias(1, 1, nc.scalar.copy), load_words(1, 3)),
             (7, 1): lambda: stage_coefficients(1),
         }
 
@@ -572,6 +589,9 @@ def tile_fluxjointattention_pa_kernel(
         turn_x(0, 1)
         copy_x(0, 1, nc.vector.tensor_copy)
         quantise_block(0)
+        spread_gains(0, nc.scalar.copy)
+        spread_bias(0, 0, nc.scalar.copy)
+        spread_bias(0, 2, nc.scalar.copy)
         build_row_tables(0)
         project(fillers[0])
         turn_x(1, 0)
@@ -592,6 +612,7 @@ def tile_fluxjointattention_pa_kernel(
         project(fillers[1])
         turn_vectors()
         turn_tables()
+        spread_bias(0, 1, nc.scalar.copy)
         for k in range(1, n_slots):
             do(project, col(k))
             do(row_bias, filler(k))

@@ -95,9 +95,11 @@ def tile_fluxjointattention_pa_kernel(
         spread_rows = [keep.tile([P, HALF + 2 * DH], BF16, name="spread_rows_%d" % s) for s in range(2)]
 
         nc.gpsimd.memset(spread_rows[0][:].bitcast(F32), 0.0)
+        nc.vector.memset(eps[:], EPS)
         nc.vector.memset(idle_sb[:].bitcast(I32), 0)
         nc.vector.memset(w_planes[0][:].rearrange("p g n -> p (g n)").bitcast(I32), 0)
-        nc.vector.memset(eps[:], EPS)
+        first_act = keep.tile([P, 1], F32)
+        nc.scalar.activation(out=first_act[:], in_=eps[:], func=ACT.Abs_reciprocal_sqrt, bias=eps[:], scale=1.0)
         nc.vector.memset(vec_rows[:].bitcast(I32), 0)
         make_identity(nc, ident[:])
         nc.gpsimd.memset(spread_rows[1][:].bitcast(F32), 0.0)
@@ -583,7 +585,7 @@ def tile_fluxjointattention_pa_kernel(
             if (k, place) in extras:
                 extras[(k, place)]()
 
-        keep_clock_up(8)
+        keep_clock_up(4)
         turn_x(0, 0)
         copy_x(0, 0, nc.scalar.copy)
         turn_x(0, 1)

@@ -383,6 +383,7 @@ def tile_fluxjointattention_pa_kernel(
                 st["u"] = u
 
         sums_of = {}
+        inverted = set()
 
         def slot_sums(k, n):
             if k not in sums_of:
@@ -392,8 +393,9 @@ def tile_fluxjointattention_pa_kernel(
             return sums_of[k][0]
 
         def inverse_rms(k):
-            if k not in sums_of:
+            if k not in sums_of or k in inverted:
                 return
+            inverted.add(k)
             sum_sq, writers = sums_of[k]
             first = 0 if any(steps[n][0] == "col" for n in writers) else COL_TILES
             last = COL_TILES + TILES * GROUP if any(steps[n][0] == "row" for n in writers) else COL_TILES
@@ -480,7 +482,7 @@ def tile_fluxjointattention_pa_kernel(
             part = steps[n][1]
             st = live[n]
             products = colwork.tile([P, 2, BANK], F32, tag="products")
-            on_gpsimd = n % 8 in (1, 3, 5)
+            on_gpsimd = n % 2 == 1 and n < 29
             kinds = 1 if on_gpsimd else 2
             nc.vector.scalar_tensor_tensor(
                 out=products[:, 0:kinds, :],
@@ -496,14 +498,20 @@ def tile_fluxjointattention_pa_kernel(
 
         def col_turn_plain(n):
             st = live[n]
-            plain_ps = turn.tile([P, COL_TILES, DH], F32, tag="turn")
+            if n >= len(steps) - 2:
+                plain_ps = sums.tile([P, COL_TILES, DH], F32, tag="acc")
+            else:
+                plain_ps = turn.tile([P, COL_TILES, DH], F32, tag="turn")
             for k in range(COL_TILES):
                 nc.tensor.transpose(plain_ps[:, k, :], st["plain"][:, k * P : (k + 1) * P], ident[:])
             st["plain_ps"] = plain_ps
 
         def col_turn_products(n):
             st = live[n]
-            rotated_ps = turn.tile([P, COL_TILES, DH], F32, tag="turn")
+            if n >= len(steps) - 2:
+                rotated_ps = sums.tile([P, COL_TILES, DH], F32, tag="acc")
+            else:
+                rotated_ps = turn.tile([P, COL_TILES, DH], F32, tag="turn")
             for k in range(COL_TILES):
                 nc.tensor.matmul(
                     rotated_ps[:, k, :],
@@ -578,7 +586,7 @@ def tile_fluxjointattention_pa_kernel(
             (5, 0): lambda: (quantise_block(3), build_row_tables(1)),
             (5, 2): lambda: spread_bias(1, 0, nc.scalar.copy),
             (6, 2): lambda: (spread_bias(1, 1, nc.scalar.copy), load_words(1, 3)),
-            (7, 1): lambda: stage_coefficients(1),
+            (7, 3): lambda: stage_coefficients(1),
         }
 
         def extra(k, place):
@@ -625,7 +633,10 @@ def tile_fluxjointattention_pa_kernel(
             do(col_turn_products, col(k - 2))
             if col(k - 1) is not None:
                 col_squares(k, col(k - 1))
+                if col(k) is None:
+                    inverse_rms(k)
             do(col_products, col(k))
+            extra(k, 3)
             do(project, filler(k + 1))
             extra(k, 1)
             do(col_scale, col(k - 2))

import concourse.mybir as mybir
from concourse.masks import make_identity

F32 = mybir.dt.float32
BF16 = mybir.dt.bfloat16
I32 = mybir.dt.int32
U32 = mybir.dt.uint32
U8 = mybir.dt.uint8
FP8X4 = mybir.dt.float8_e4m3fn_x4
FP4X4 = mybir.dt.float4_e2m1fn_x4
ACT = mybir.ActivationFunctionType
ALU = mybir.AluOpType

P = 128
D_MODEL = 1024
K_PASS = 512
PASSES = D_MODEL // K_PASS
DH = 128
HEADS = 8
PAIRS = DH // 2
GROUP = 4
BANK = GROUP * DH
N_OUT = 3 * D_MODEL
CHUNKS = N_OUT // BANK
TILES = 2
BLOCKS = 4
ALL_TILES = BLOCKS * TILES
EPS = 1e-6
ROW_BLOCKS = (0, 3)
COL_FIRST = 1
COL_TILES = 2 * TILES
COL_TOKEN = COL_FIRST * TILES * P

FLOPS = 2 * BLOCKS * TILES * P * D_MODEL * N_OUT


def tile_fluxjointattention_pa_kernel(
    tc,
    hidden_states_a,
    hidden_states_b,
    image_rotary_emb,
    a_qkv_w_words,
    a_qkv_w_scales,
    a_qkv_b,
    b_qkv_w_words,
    b_qkv_w_scales,
    b_qkv_b,
    norm_q_a_w,
    norm_k_a_w,
    norm_q_b_w,
    norm_k_b_w,
    out_0,
    out_1,
    out_2,
):
    nc = tc.nc
    words_in = (b_qkv_w_words, a_qkv_w_words)
    scales_in = (b_qkv_w_scales, a_qkv_w_scales)
    bias_in = (b_qkv_b, a_qkv_b)
    gain_in = (norm_q_b_w, norm_k_b_w, norm_q_a_w, norm_k_a_w)
    outs = (out_0, out_1, out_2)

    with (
        tc.tile_pool(name="keep", bufs=1) as keep,
        tc.tile_pool(name="stage", bufs=3) as stage,
        tc.tile_pool(name="rowwork", bufs=4) as rowwork,
        tc.tile_pool(name="colwork", bufs=3) as colwork,
        tc.tile_pool(name="small", bufs=6) as small,
        tc.tile_pool(name="result", bufs=6) as result,
        tc.psum_pool(name="sums", bufs=4) as sums,
        tc.psum_pool(name="turn", bufs=3) as turn,
        tc.psum_pool(name="coefs", bufs=1) as coefs,
        tc.manual_schedule(),
    ):
        x_sb = keep.tile([P, BLOCKS, TILES, D_MODEL], BF16)
        x_codes = keep.tile([P, PASSES, ALL_TILES * P], U32, align_bytes=64)
        x_planes = keep.tile([P, PASSES, ALL_TILES * P], U8, align_bytes=64)
        w_words = keep.tile([P, 2, CHUNKS, PASSES, 2 * BANK], U8, align_bytes=64)
        w_planes = [keep.tile([P, PASSES, N_OUT], U8, align_bytes=64, name="w_planes_%d" % s) for s in range(2)]
        bias_all = [keep.tile([P, N_OUT], BF16, name="bias_all_%d" % s) for s in range(2)]
        gain_all = keep.tile([P, 4, DH], BF16)
        rope_sb = keep.tile([P, ALL_TILES, 4 * PAIRS], BF16)
        row_straight_tab = keep.tile([P, 2, 2, TILES, DH], F32)
        row_crossed_tab = keep.tile([P, 2, 2, TILES, 2, PAIRS], F32)
        vec_rows = keep.tile([P, P], BF16)
        vec_cols = keep.tile([P, 2 * HEADS + 2], F32)
        picked = keep.tile([P, 2, COL_TILES, DH], BF16)
        col_tab = keep.tile([P, 2, 2, COL_TILES * P], F32)
        ident = keep.tile([P, P], F32)
        swap = keep.tile([P, P], F32)
        ident_bf = keep.tile([P, P], BF16)
        eps = keep.tile([P, 1], F32)
        idle_sb = keep.tile([P, BANK], BF16)
        HALF = N_OUT // 2
        spread_rows = [keep.tile([P, HALF + 2 * DH], BF16, name="spread_rows_%d" % s) for s in range(2)]

        nc.gpsimd.memset(spread_rows[0][:].bitcast(F32), 0.0)
        nc.vector.memset(eps[:], EPS)
        nc.vector.memset(idle_sb[:].bitcast(I32), 0)
        nc.vector.memset(w_planes[0][:].rearrange("p g n -> p (g n)").bitcast(I32), 0)
        first_act = keep.tile([P, 1], F32)
        nc.scalar.activation(out=first_act[:], in_=eps[:], func=ACT.Abs_reciprocal_sqrt, bias=eps[:], scale=1.0)
        nc.vector.memset(vec_rows[:].bitcast(I32), 0)
        make_identity(nc, ident[:])
        nc.gpsimd.memset(spread_rows[1][:].bitcast(F32), 0.0)
        nc.gpsimd.memset(w_planes[1][:].rearrange("p g n -> p (g n)").bitcast(F32), 0.0)
        nc.vector.tensor_copy(out=ident_bf[:], in_=ident[:])
        pairs_of = "p (j i) -> p j i"
        for i in range(2):
            nc.vector.tensor_copy(
                out=swap[:].rearrange(pairs_of, i=2)[:, :, i], in_=ident[:].rearrange(pairs_of, i=2)[:, :, 1 - i]
            )

        def load_x(blk):
            if blk == 0:
                rows = hidden_states_b[0]
            else:
                rows = hidden_states_a[0, (blk - 1) * TILES * P : blk * TILES * P, :]
            nc.sync.dma_start(out=x_sb[:, blk], in_=rows.rearrange("(p t) k -> p t k", t=TILES))

        def load_scales(s):
            planes = w_planes[s][:].bitcast(I32)
            rows = scales_in[s].bitcast(I32)
            for r in range(4):
                nc.sync.dma_start(out=planes[r:P:32], in_=rows[:, r:16:4, :].rearrange("g q n -> q g n"))

        def load_words(s, c):
            width = 2 * BANK // 4
            nc.sync.dma_start(
                out=w_words[:, s, c].bitcast(I32),
                in_=words_in[s].bitcast(I32)[:, :, c * width : (c + 1) * width].rearrange("g p n -> p g n"),
            )

        def load_vectors(s):
            nc.sync.dma_start(out=spread_rows[s][0:2, 0:HALF], in_=bias_in[s].rearrange("(r n) -> r n", r=2))
            for qk in range(2):
                nc.sync.dma_start(
                    out=spread_rows[s][0:1, HALF + qk * DH : HALF + (qk + 1) * DH],
                    in_=gain_in[2 * s + qk].rearrange("(o n) -> o n", o=1),
                )

        def load_rope(first, last):
            nc.sync.dma_start(
                out=rope_sb[:].rearrange("p (k t) f -> p k (t f)", t=TILES)[:, first:last, :],
                in_=image_rotary_emb.rearrange("a b (k p t) j r c -> p (a b k) (t j r c)", p=P, t=TILES)[:, first:last, :],
            )

        def load_vec_rows():
            nc.sync.dma_start(
                out=vec_rows[0 : 2 * HEADS, :], in_=a_qkv_b[0 : 2 * HEADS * DH].rearrange("(h f) -> h f", f=DH)
            )
            for qk in range(2):
                nc.sync.dma_start(
                    out=vec_rows[2 * HEADS + qk : 2 * HEADS + qk + 1, :],
                    in_=gain_in[2 + qk].rearrange("(o n) -> o n", o=1),
                )

        load_x(0)
        load_vectors(0)
        load_scales(0)
        load_words(0, 0)
        load_rope(0, 1)
        load_x(1)
        load_x(2)
        load_rope(1, BLOCKS)
        load_vec_rows()
        load_words(0, 4)
        load_scales(1)
        load_words(1, 0)
        load_words(0, 2)
        load_vectors(1)
        load_words(0, 5)
        load_words(0, 1)
        load_x(3)
        load_words(1, 4)

        grouped_x = {}

        def keep_clock_up(count):
            idle_ps = turn.tile([P, BANK], F32, tag="turn")
            for i in range(count):
                nc.tensor.matmul(idle_ps[:], lhsT=idle_sb[:, 0:P], rhs=idle_sb[:], start=True, stop=True)

        def transpose_tile(blk, t):
            turn_x(blk, t)
            copy_x(blk, t, nc.scalar.copy)

        turned_x = {}

        def turn_x(blk, t):
            x_pairs = x_sb[:].bitcast(F32)
            if blk < BLOCKS - 1:
                x_t = sums.tile([P, PASSES * 2, P], F32, tag="acc")
            else:
                x_t = turn.tile([P, PASSES * 2, P], F32, tag="turn")
            for g in range(PASSES):
                for u in range(2):
                    nc.tensor.transpose(
                        x_t[:, 2 * g + u, :], x_pairs[:, blk, t, 256 * g + u : 256 * (g + 1) : 2], ident[:]
                    )
            turned_x[(blk, t)] = x_t

        def copy_x(blk, t, copy):
            if blk not in grouped_x:
                grouped = stage.tile([P, PASSES, TILES, P, 2], F32, align_bytes=64)
                grouped_x[blk] = grouped
            copy(out=grouped_x[blk][:, :, t], in_=turned_x[(blk, t)][:].rearrange("p (g u) r -> p g r u", u=2))

        def quantise_block(blk):
            first = blk * TILES * P
            for g in range(PASSES):
                nc.vector.quantize_mx(
                    out=x_codes[:, g, first : first + TILES * P].bitcast(FP8X4),
                    scales=x_planes[:, g, first : first + TILES * P],
                    in_=grouped_x[blk][:, g].rearrange("p t r u -> p (t r u)").bitcast(BF16),
                )

        def spread(s, row, first, width, out_ps):
            nc.tensor.matmul(
                out_ps,
                lhsT=ident_bf[:, row : row + 1].to_broadcast([P, P]),
                rhs=spread_rows[s][:, first : first + width],
                start=True,
                stop=True,
            )

        def spread_bias(s, pair, copy):
            both = turn.tile([P, 2 * BANK], BF16, tag="turn")
            for j in range(2):
                c = 2 * pair + j
                spread(s, c // 3, (c % 3) * BANK, BANK, both[:, j * BANK : (j + 1) * BANK])
            copy(out=bias_all[s][:, 2 * pair * BANK : 2 * (pair + 1) * BANK], in_=both[:])

        def spread_gains(s, copy):
            two = turn.tile([P, 2 * BANK], BF16, tag="turn")
            spread(s, 0, HALF, 2 * DH, two[:, 0 : 2 * DH])
            copy(out=gain_all[:, 2 * s : 2 * s + 2, :].rearrange("p g d -> p (g d)"), in_=two[:, 0 : 2 * DH])

        def build_row_tables(kb):
            blk = ROW_BLOCKS[kb]
            s = 0 if blk == 0 else 1
            coef = rope_sb[:, blk * TILES : (blk + 1) * TILES, :].rearrange("p n (j c) -> p n c j", c=4)
            for qk in range(2):
                gain = gain_all[:, 2 * s + qk, :].rearrange("p (j i) -> p i j", i=2)
                nc.vector.tensor_tensor(
                    out=row_straight_tab[:, kb, qk].rearrange("p n (i j) -> p n i j", i=2),
                    in0=coef[:, :, 0:4:3, :],
                    in1=gain.unsqueeze(1).to_broadcast([P, TILES, 2, PAIRS]),
                    op=ALU.mult,
                )
                for i in range(2):
                    nc.gpsimd.tensor_tensor(
                        out=row_crossed_tab[:, kb, qk, :, i, :],
                        in0=coef[:, :, 1 + i, :],
                        in1=gain[:, 1 - i, :].unsqueeze(1).to_broadcast([P, TILES, PAIRS]),
                        op=ALU.mult,
                    )

        coef_ps = {}

        def stage_coefficients(kb):
            coef = coefs.tile([P, 2, TILES, DH], F32)
            nc.tensor.matmul(
                coef[:].rearrange("p q t f -> p (q t f)"),
                lhsT=ident[:],
                rhs=row_straight_tab[:, kb].rearrange("p q t f -> p (q t f)"),
                start=True,
                stop=True,
            )
            coef_ps[kb] = coef

        def pick_coefficients():
            first = COL_FIRST * TILES
            coef = rope_sb[:, first : first + COL_TILES, :].rearrange("p n (j c) -> p n j c", c=4)
            nc.scalar.copy(
                out=picked[:, 0].rearrange("p n (j e) -> p n j e", e=2), in_=coef[:, :, :, 0:4:3]
            )
            for e in range(2):
                nc.scalar.copy(
                    out=picked[:, 1].rearrange("p n (j e) -> p n j e", e=2)[:, :, :, e], in_=coef[:, :, :, 2 - e]
                )

        def turn_vectors():
            col_ps = turn.tile([P, P], BF16, tag="turn")
            nc.tensor.transpose(col_ps[:], vec_rows[:], ident_bf[:])
            nc.scalar.copy(out=vec_cols[:], in_=col_ps[:, 0 : 2 * HEADS + 2])

        picked_ps = []

        def scale_tables(qk):
            nc.scalar.activation(
                out=col_tab[:, qk].rearrange("p k n -> p (k n)"),
                in_=picked_ps[0][:].rearrange("p k n -> p (k n)"),
                func=ACT.Copy,
                scale=vec_cols[:, 2 * HEADS + qk : 2 * HEADS + qk + 1],
            )

        def turn_tables():
            tab_ps = turn.tile([P, 2, COL_TILES * P], BF16, tag="turn")
            for k in range(2):
                for n in range(COL_TILES):
                    nc.tensor.transpose(tab_ps[:, k, n * P : (n + 1) * P], picked[:, k, n, :], ident_bf[:])
            picked_ps.append(tab_ps)
            scale_tables(0)

        row_steps = [("row", blk, part, m) for blk in ROW_BLOCKS for m in range(2) for part in range(2)]
        val_steps = [("row", blk, 2, m) for blk in range(BLOCKS) for m in range(2)]
        col_steps = [("col", part, GROUP * m + h) for m in range(2) for part in range(2) for h in range(GROUP)]
        steps = row_steps + val_steps + col_steps
        n_row, n_val = len(row_steps), len(val_steps)
        live = {}

        def project(n):
            st = live.setdefault(n, {})
            if steps[n][0] == "col":
                part, h = steps[n][1:]
                c = 2 * part + h // GROUP
                hl = h % GROUP
                acc = sums.tile([P, BANK], F32, tag="acc")
                for g in range(PASSES):
                    nc.tensor.matmul_mx(
                        out=acc[:],
                        lhsT=w_words[:, 1, c, g, hl * 2 * DH : (hl + 1) * 2 * DH].bitcast(FP4X4),
                        lhsT_scale=w_planes[1][:, g, c * BANK + hl * DH : c * BANK + (hl + 1) * DH],
                        rhs=x_codes[:, g, COL_TOKEN : COL_TOKEN + BANK].bitcast(FP8X4),
                        rhs_scale=x_planes[:, g, COL_TOKEN : COL_TOKEN + BANK],
                        start=(g == 0),
                        stop=(g == PASSES - 1),
                    )
                st["acc"] = acc
                return
            blk, part, m = steps[n][1:]
            s = 0 if blk == 0 else 1
            c = 2 * part + m
            for t in range(TILES):
                k = blk * TILES + t
                acc = sums.tile([P, BANK], F32, tag="acc")
                for g in range(PASSES):
                    nc.tensor.matmul_mx(
                        out=acc[:],
                        lhsT=x_codes[:, g, k * P : (k + 1) * P].bitcast(FP8X4),
                        lhsT_scale=x_planes[:, g, k * P : (k + 1) * P],
                        rhs=w_words[:, s, c, g, :].bitcast(FP4X4),
                        rhs_scale=w_planes[s][:, g, c * BANK : (c + 1) * BANK],
                        start=(g == 0),
                        stop=(g == PASSES - 1),
                    )
                st[("acc", t)] = acc

        def store_rows(n, out_sb):
            blk, part, m = steps[n][1:]
            rows = outs[part][0, m * GROUP : (m + 1) * GROUP, blk * TILES * P : (blk + 1) * TILES * P, :]
            nc.sync.dma_start(
                out=rows.rearrange("h (p t) d -> p h (t d)", t=TILES),
                in_=out_sb[:].rearrange("p h t d -> p h (t d)"),
            )

        def row_bias(n):
            blk, part, m = steps[n][1:]
            s = 0 if blk == 0 else 1
            c = 2 * part + m
            st = live[n]
            bias = bias_all[s][:, c * BANK : (c + 1) * BANK]
            if part == 2:
                out_sb = result.tile([P, GROUP, TILES, DH], F32, tag="out_sb")
                for t in range(TILES):
                    nc.vector.tensor_tensor(
                        out=out_sb[:, :, t, :],
                        in0=st[("acc", t)][:].rearrange("p (h d) -> p h d", h=GROUP),
                        in1=bias.rearrange("p (h d) -> p h d", h=GROUP),
                        op=ALU.add,
                    )
                store_rows(n, out_sb)
            else:
                u = rowwork.tile([P, TILES, GROUP, 2, PAIRS], F32)
                for t in range(TILES):
                    nc.vector.tensor_tensor(
                        out=u[:, t],
                        in0=st[("acc", t)][:].rearrange("p (h j i) -> p h i j", h=GROUP, i=2),
                        in1=bias.rearrange("p (h j i) -> p h i j", h=GROUP, i=2),
                        op=ALU.add,
                    )
                st["u"] = u

        sums_of = {}
        inverted = set()

        def slot_sums(k, n):
            if k not in sums_of:
                sum_sq = small.tile([P, COL_TILES + TILES * GROUP], F32, tag="sum_sq")
                sums_of[k] = (sum_sq, [])
            sums_of[k][1].append(n)
            return sums_of[k][0]

        def inverse_rms(k):
            if k not in sums_of or k in inverted:
                return
            inverted.add(k)
            sum_sq, writers = sums_of[k]
            first = 0 if any(steps[n][0] == "col" for n in writers) else COL_TILES
            last = COL_TILES + TILES * GROUP if any(steps[n][0] == "row" for n in writers) else COL_TILES
            inv_rms = small.tile([P, COL_TILES + TILES * GROUP], F32, tag="inv_rms")
            nc.scalar.activation(
                out=inv_rms[:, first:last],
                in_=sum_sq[:, first:last],
                func=ACT.Abs_reciprocal_sqrt,
                bias=eps[:],
                scale=1.0 / DH,
            )
            for n in writers:
                live[n]["inv_rms"] = inv_rms[:, 0:COL_TILES] if steps[n][0] == "col" else inv_rms[:, COL_TILES:]

        def row_squares(k, n):
            st = live[n]
            u = st["u"]
            squares = rowwork.tile([P, TILES, GROUP, DH], BF16)
            sum_sq = slot_sums(k, n)
            for t in range(TILES):
                for h in range(GROUP):
                    column = COL_TILES + t * GROUP + h
                    nc.scalar.activation(
                        out=squares[:, t, h, :],
                        in_=u[:, t, h].rearrange("p i j -> p (i j)"),
                        func=ACT.Square,
                        accum_out=sum_sq[:, column : column + 1],
                    )

        def row_products(n):
            blk, part, m = steps[n][1:]
            kb = ROW_BLOCKS.index(blk)
            st = live[n]
            u = st["u"]
            straight = rowwork.tile([P, TILES, GROUP, 2, PAIRS], F32)
            nc.vector.tensor_tensor(
                out=straight[:].rearrange("p t h i j -> p t h (i j)"),
                in0=u[:].rearrange("p t h i j -> p t h (i j)"),
                in1=coef_ps[kb][:, part].unsqueeze(2).to_broadcast([P, TILES, GROUP, DH]),
                op=ALU.mult,
            )
            crossed = rowwork.tile([P, TILES, GROUP, 2, PAIRS], F32)
            for i in range(2):
                nc.gpsimd.tensor_tensor(
                    out=crossed[:, :, :, i, :],
                    in0=u[:, :, :, 1 - i, :],
                    in1=row_crossed_tab[:, kb, part, :, i, :].unsqueeze(2).to_broadcast([P, TILES, GROUP, PAIRS]),
                    op=ALU.mult,
                )
            nc.gpsimd.tensor_tensor(
                out=straight[:].rearrange("p t h i j -> p (t h i j)"),
                in0=straight[:].rearrange("p t h i j -> p (t h i j)"),
                in1=crossed[:].rearrange("p t h i j -> p (t h i j)"),
                op=ALU.add,
            )
            st["rotated"] = straight

        def row_scale(n):
            st = live[n]
            rotated = st["rotated"]
            inv_rms = st["inv_rms"]
            out_sb = result.tile([P, GROUP, TILES, DH], F32, tag="out_sb")
            for t in range(TILES):
                for h in range(GROUP):
                    nc.scalar.activation(
                        out=out_sb[:, h, t, :].rearrange("p (j i) -> p j i", i=2),
                        in_=rotated[:, t, h].rearrange("p i j -> p j i"),
                        func=ACT.Copy,
                        scale=inv_rms[:, t * GROUP + h : t * GROUP + h + 1],
                    )
            store_rows(n, out_sb)

        def col_bias_of(n):
            part, h = steps[n][1:]
            return vec_cols[:, part * HEADS + h : part * HEADS + h + 1]

        def col_plain(n):
            st = live[n]
            plain = colwork.tile([P, BANK], F32)
            nc.scalar.activation(out=plain[:], in_=st["acc"][:], func=ACT.Identity, bias=col_bias_of(n), scale=1.0)
            st["plain"] = plain

        def col_products(n):
            part = steps[n][1]
            st = live[n]
            products = colwork.tile([P, 2, BANK], F32, tag="products")
            on_gpsimd = n % 2 == 1 and n < 29
            kinds = 1 if on_gpsimd else 2
            nc.vector.scalar_tensor_tensor(
                out=products[:, 0:kinds, :],
                in0=st["acc"][:].unsqueeze(1).to_broadcast([P, kinds, BANK]),
                scalar=col_bias_of(n),
                in1=col_tab[:, part, 0:kinds, :],
                op0=ALU.add,
                op1=ALU.mult,
            )
            if on_gpsimd:
                nc.gpsimd.tensor_tensor(out=products[:, 1, :], in0=st["plain"][:], in1=col_tab[:, part, 1, :], op=ALU.mult)
            st["products"] = products

        def col_turn_plain(n):
            st = live[n]
            if n >= len(steps) - 2:
                plain_ps = sums.tile([P, COL_TILES, DH], F32, tag="acc")
            else:
                plain_ps = turn.tile([P, COL_TILES, DH], F32, tag="turn")
            for k in range(COL_TILES):
                nc.tensor.transpose(plain_ps[:, k, :], st["plain"][:, k * P : (k + 1) * P], ident[:])
            st["plain_ps"] = plain_ps

        def col_turn_products(n):
            st = live[n]
            if n >= len(steps) - 2:
                rotated_ps = sums.tile([P, COL_TILES, DH], F32, tag="acc")
            else:
                rotated_ps = turn.tile([P, COL_TILES, DH], F32, tag="turn")
            for k in range(COL_TILES):
                nc.tensor.matmul(
                    rotated_ps[:, k, :],
                    lhsT=st["products"][:, 0, k * P : (k + 1) * P],
                    rhs=ident[:],
                    is_transpose=True,
                    start=True,
                    stop=False,
                )
                nc.tensor.matmul(
                    rotated_ps[:, k, :],
                    lhsT=st["products"][:, 1, k * P : (k + 1) * P],
                    rhs=swap[:],
                    is_transpose=True,
                    start=False,
                    stop=True,
                )
            st["rotated_ps"] = rotated_ps

        def col_squares(slot, n):
            st = live[n]
            squares = colwork.tile([P, COL_TILES, DH], BF16, tag="col_squares")
            sum_sq = slot_sums(slot, n)
            for k in range(COL_TILES):
                nc.scalar.activation(
                    out=squares[:, k, :], in_=st["plain_ps"][:, k, :], func=ACT.Square, accum_out=sum_sq[:, k : k + 1]
                )

        def col_scale(n):
            part, h = steps[n][1:]
            st = live[n]
            out_sb = result.tile([P, COL_TILES, DH], F32, tag="col_out")
            nc.vector.tensor_tensor(
                out=out_sb[:],
                in0=st["rotated_ps"][:],
                in1=st["inv_rms"].unsqueeze(2).to_broadcast([P, COL_TILES, DH]),
                op=ALU.mult,
            )
            rows = outs[part][0, h, COL_TOKEN : COL_TOKEN + COL_TILES * P, :]
            nc.sync.dma_start(
                out=rows.rearrange("(b p t) d -> p b (t d)", p=P, t=TILES),
                in_=out_sb[:].rearrange("p (b t) d -> p b (t d)", t=TILES),
            )

        fillers = []
        for k in range(n_row):
            fillers += [k, n_row + k]
        LEAD = 1
        SCALE_LAG = 3
        DRAIN = 2
        n_slots = len(col_steps) + LEAD + DRAIN

        def filler(k):
            return fillers[k] if 0 <= k < len(fillers) else None

        def col(k):
            return n_row + n_val + k - LEAD if 0 <= k - LEAD < len(col_steps) else None

        def is_row(n):
            return n is not None and n < n_row

        def do(stage_of, n):
            if n is not None:
                stage_of(n)

        extras = {
            (1, 2): lambda: (load_words(1, 2), load_words(0, 3)),
            (2, 1): lambda: scale_tables(1),
            (2, 2): lambda: (spread_bias(1, 2, nc.scalar.copy), load_words(1, 5)),
            (3, 2): lambda: (transpose_tile(3, 0), spread_gains(1, nc.scalar.copy)),
            (4, 2): lambda: (transpose_tile(3, 1), load_words(1, 1)),
            (5, 0): lambda: (quantise_block(3), build_row_tables(1)),
            (5, 2): lambda: spread_bias(1, 0, nc.scalar.copy),
            (6, 2): lambda: (spread_bias(1, 1, nc.scalar.copy), load_words(1, 3)),
            (7, 3): lambda: stage_coefficients(1),
        }

        def extra(k, place):
            if (k, place) in extras:
                extras[(k, place)]()

        keep_clock_up(4)
        turn_x(0, 0)
        copy_x(0, 0, nc.scalar.copy)
        turn_x(0, 1)
        copy_x(0, 1, nc.vector.tensor_copy)
        quantise_block(0)
        spread_gains(0, nc.scalar.copy)
        spread_bias(0, 0, nc.scalar.copy)
        spread_bias(0, 2, nc.scalar.copy)
        build_row_tables(0)
        project(fillers[0])
        turn_x(1, 0)
        turn_x(1, 1)
        stage_coefficients(0)
        row_bias(fillers[0])
        copy_x(1, 0, nc.vector.tensor_copy)
        copy_x(1, 1, nc.vector.tensor_copy)
        quantise_block(1)
        row_products(fillers[0])
        row_squares(0, fillers[0])
        turn_x(2, 0)
        turn_x(2, 1)
        pick_coefficients()
        copy_x(2, 0, nc.scalar.copy)
        copy_x(2, 1, nc.vector.tensor_copy)
        quantise_block(2)
        project(fillers[1])
        turn_vectors()
        turn_tables()
        spread_bias(0, 1, nc.scalar.copy)
        for k in range(1, n_slots):
            do(project, col(k))
            do(row_bias, filler(k))
            extra(k, 0)
            do(col_turn_plain, col(k - 1))
            do(col_plain, col(k))
            inverse_rms(k - 1)
            do(col_turn_products, col(k - 2))
            if col(k - 1) is not None:
                col_squares(k, col(k - 1))
                if col(k) is None:
                    inverse_rms(k)
            do(col_products, col(k))
            extra(k, 3)
            do(project, filler(k + 1))
            extra(k, 1)
            do(col_scale, col(k - 2))
            if is_row(filler(k)):
                row_products(filler(k))
                row_squares(k, filler(k))
            if is_row(filler(k - SCALE_LAG)):
                row_scale(filler(k - SCALE_LAG))
            extra(k, 2)
